import numpy as np
import ml_dtypes


def mxq(x, axis, fmt="e4m3"):
    dtype, down = {"e4m3": (ml_dtypes.float8_e4m3fn, 7), "e5m2": (ml_dtypes.float8_e5m2, 14)}[fmt]
    v = np.moveaxis(np.asarray(x, np.float32).astype(ml_dtypes.bfloat16).astype(np.float64), axis, -1)
    blocks = v.reshape(v.shape[:-1] + (-1, 32))
    amax = np.abs(blocks).max(-1, keepdims=True)
    byte = np.maximum(np.where(amax > 0, np.frexp(amax)[1] - 1 + 127, 0) - down, 1)
    scale = np.exp2(byte - 127.0)
    codes = (blocks / scale).astype(np.float32).astype(dtype).astype(np.float64)
    return np.moveaxis((codes * scale).reshape(v.shape), -1, axis)


WIDE = False


def mx_kscale(k):
    if not WIDE:
        return np.ones(k)
    levels = np.array([18, -18])
    if k % 512:
        return np.exp2(np.random.permutation(np.resize(levels, k // 32))).repeat(32)
    a = np.empty((k // 512, 16))
    for p in range(k // 512):
        a[p, :8] = np.random.permutation(np.resize(levels, 8))
        for g in range(8):
            far = levels[np.abs(levels - a[p, g]) >= 10]
            a[p, g + 8] = far[np.random.randint(len(far))]
    return np.exp2(a.ravel()).repeat(32)


BF16 = ml_dtypes.bfloat16


def bf(x):
    return np.asarray(x, np.float32).astype(BF16)


def f64(x):
    return np.asarray(x).astype(np.float64)


B, L, E, H, HD, F, G = 4, 128, 1024, 8, 128, 2048, 2048
EPS = 1e-6
T, J = B * L, H * HD


def rope_diag():
    pair = np.arange(HD) // 2
    theta = 10000.0 ** (-2.0 * pair / HD)
    return np.cos(np.arange(L)[:, None] * theta[None, :])


def setup_inputs():
    s = mx_kscale(T)
    uq = mx_kscale(J).reshape(1, H, 1, HD)
    uk = mx_kscale(J).reshape(1, H, 1, HD)
    x0 = bf(np.random.standard_normal((B, L, E)))
    g = bf(1.0 + 0.1 * np.random.standard_normal(E))
    wq0 = bf(np.random.standard_normal((E, J)) / np.sqrt(E))
    wk0 = bf(np.random.standard_normal((E, J)) / np.sqrt(E))
    st = s.reshape(B, 1, L, 1)
    g0 = 2.0 * np.random.standard_normal((B, H, L, HD)) * np.exp2(np.random.randint(-6, 1, (B, 1, L, 1)))
    g1 = 2.0 * np.random.standard_normal((B, H, L, HD)) * np.exp2(np.random.randint(-6, 1, (B, 1, L, 1)))
    xf = f64(x0)
    rstd = 1.0 / np.sqrt(np.mean(xf * xf, axis=-1) + EPS)
    return {"x": bf(xf * s.reshape(B, L, 1)),
            "g": g,
            "wq": bf(f64(wq0) / uq.reshape(1, J)),
            "wk": bf(f64(wk0) / uk.reshape(1, J)),
            "rstd": np.asarray(rstd, np.float32),
            "grad_0": bf(g0 / st * uq),
            "grad_1": bf(g1 / st * uk)}


def reference(x, g, wq, wk, rstd, grad_0, grad_1):
    c = rope_diag()
    xf = f64(x).reshape(T, E)
    gf = f64(g)
    r = f64(rstd).reshape(T, 1)
    dq = (f64(grad_0) * c).transpose(0, 2, 1, 3).reshape(T, J)
    dk = (f64(grad_1) * c).transpose(0, 2, 1, 3).reshape(T, J)
    dz = np.concatenate([dq, dk], axis=1)
    w = np.concatenate([f64(wq), f64(wk)], axis=1)
    dh = mxq(dz, 1, "e5m2") @ mxq(w, 1, "e4m3").T
    h = xf * r * gf
    dw = mxq(h, 0, "e4m3").T @ mxq(dz, 0, "e5m2")
    a = gf * dh
    dx = r * a - xf * r ** 3 * np.mean(xf * a, axis=1, keepdims=True)
    return dx.reshape(B, L, E), dw[:, :J], dw[:, J:]

@@ -1,0 +1,302 @@
+import math
+from contextlib import ExitStack
+
+import concourse.mybir as mybir
+from concourse.masks import make_identity
+
+F32 = mybir.dt.float32
+BF16 = mybir.dt.bfloat16
+I32 = mybir.dt.int32
+U32 = mybir.dt.uint32
+U8 = mybir.dt.uint8
+E4M3 = mybir.dt.float8_e4m3fn_x4
+E5M2 = mybir.dt.float8_e5m2_x4
+ALU = mybir.AluOpType
+ACT = mybir.ActivationFunctionType
+
+P = 128
+B, L, E, HEADS, HD = 4, 128, 1024, 8, 128
+T = B * L
+J = HEADS * HD
+SLOTS = 4
+UNIT = 512
+HALF = 512
+UNITS = 2 * J // UNIT
+FLOPS = 2 * 2 * T * E * 2 * J
+
+ORDER = """
+rope0 rg03 rg13
+rope1 rg12 rg02 dk2 dk3
+qz0 rg11 rg00
+qz1 tz01 rg01 tw101 cz01
+norm0 tz00 cw101 tw001 cz00
+qt0 tw000 cw001 tz11 cw000
+rope2 tw200 cz11 cw200
+rope3 tz10 rg10 cz10
+qh0 tw100 tw201 cw100 tz21 cw201
+norm1 tw301 cz21
+qz2 tw210 cw301 tw110 cw210
+qh1 tz30 cw110 tw300 cz30
+qw20 tz20 cw300 dw10 cz20
+qw10 dw20 cd10 dw00 cd20
+qt1 tz31 cd00 tw310 cz31v
+qz3 dw04 cw310 dw14 cd04
+qw00 tw311 cd14 dw11 cw311
+qw30 cd11 tw111 tw211 cw111
+qt2 dw21 cw211 dw05 cd21
+qt3 tw010 cd05v dw15 cw010v dh10
+qw11 tw011 cd15 cw011
+qw31
+gain10 dw01 dh00
+qw21 cd01 dw30 cd30
+qw01 dw02 dw16 cd02v cd16 dh11
+gain00 dw34 dw35 cd34
+gain11 dw31 cd35 dh20
+dot1 cd31 dw24 cd24 dw06 dh01
+gain20 dw17 cd06
+out1 cd17 dw36 dw07 cd36 cd07 dh31
+gain01 dw25
+dot0 dw37 cd25 dw12 cd37 cd12 dh21
+gain31 dw32 cd32
+out0 dw26 cd26 dw33 cd33 dh30
+gain21
+dot2 dw13 dw22 cd13
+gain30 dw03 cd22
+out2 dw23 cd03 cd23 dw27 cd27
+dot3
+out3
+"""
+
+
+def tile_llamaselfattentionblock_pa_v_kernel(tc, x, g, wq, wk, rstd, grad_0, grad_1, out_0, out_1, out_2):
+    nc = tc.nc
+    grads = (grad_0, grad_1)
+    weights = (wq, wk)
+    weight_grads = (out_1, out_2)
+    x_rows = x.flatten_outer_dims().rearrange("(p j) e -> p j e", j=SLOTS)
+    out_rows = out_0.flatten_outer_dims().rearrange("(p j) (h e) -> p j h e", j=SLOTS, h=2)
+
+    with ExitStack() as ctx:
+        keep = ctx.enter_context(tc.tile_pool(name="keep", bufs=1))
+        reused = ctx.enter_context(tc.tile_pool(name="reused", bufs=2))
+        psum = ctx.enter_context(tc.psum_pool(name="psum", bufs=1))
+
+        def kept(name, shape, dtype):
+            return keep.tile(shape, dtype, name=name, align_bytes=64)
+
+        def codes(name):
+            return kept(name + "_codes", [P, 512], U32), kept(name + "_scales", [P, 512], U8)
+
+        grad_sb = [reused.tile([P, HEADS, SLOTS, HD], BF16, name="grad%d" % a, tag="early_late", bufs=2, align_bytes=64) for a in range(2)]
+        pairs = [reused.tile([P, 2, 2, HALF], F32, name="pair%d" % i, tag="early_late", bufs=2, align_bytes=64) for i in range(2)]
+        scaled = [pairs[j // 2][:, j % 2] for j in range(SLOTS)]
+        rstd_sb = kept("rstd_sb", [P, SLOTS], F32)
+        gain_row = kept("gain_row", [P, E], BF16)
+        ones = kept("ones", [P, P], BF16)
+        identity = kept("identity", [P, P], F32)
+        x_sb = kept("x_sb", [P, 2, SLOTS, HALF], BF16)
+        rg = kept("rg", [P, 2, SLOTS, HALF], F32)
+        w_sb = [[kept("w%d%d" % (a, h), [P, 4, J], BF16) for h in range(2)] for a in range(2)]
+        h_tok = [kept("h_tok%d" % h, [P, HALF, SLOTS], BF16) for h in range(2)]
+        dz_tok = [kept("dz_tok%d" % u, [P, UNIT, SLOTS], BF16) for u in range(UNITS)]
+        dz_feat = [kept("dz_feat%d" % u, [P, SLOTS, P, 4], BF16) for u in range(UNITS)]
+        w_feat = [[kept("w_feat%d%d" % (u, h), [P, HALF, 4], BF16) for h in range(2)] for u in range(UNITS)]
+        h_q = [codes("h_q%d" % h) for h in range(2)]
+        dz_tok_q = [codes("dz_tok_q%d" % u) for u in range(UNITS)]
+        dz_feat_q = [codes("dz_feat_q%d" % u) for u in range(UNITS)]
+        w_q = [[codes("w_q%d%d" % (u, h)) for h in range(2)] for u in range(UNITS)]
+        neg_r2 = kept("neg_r2", [P, SLOTS], F32)
+        coef = [kept("coef%d" % j, [P, 1], F32) for j in range(SLOTS)]
+
+        ctx.enter_context(tc.manual_schedule())
+
+        def load_grad(a, b, n0, n1, queue):
+            queue.dma_start(out=grad_sb[a][32 * b : 32 * b + 32, n0:n1].rearrange("q n j d -> q n (j d)"),
+                            in_=grads[a][b, n0:n1].rearrange("n (q j) d -> q n (j d)", j=SLOTS))
+
+        def load_x(h):
+            nc.sync.dma_start(out=x_sb[:, h], in_=x_rows[:, :, h * HALF : (h + 1) * HALF])
+
+        def load_w(a, h):
+            nc.sync.dma_start(out=w_sb[a][h][:], in_=weights[a][h * HALF : (h + 1) * HALF, :].rearrange("(q i) f -> q i f", i=4))
+
+        tokens = kept("tokens", [P, SLOTS], I32)
+        nc.gpsimd.iota(tokens[:], pattern=[[1, SLOTS]], base=0, channel_multiplier=SLOTS)
+        make_identity(nc, identity[:])
+        nc.vector.memset(gain_row[:], 0.0)
+        nc.vector.memset(ones[:], 1.0)
+        nc.sync.dma_start(out=rstd_sb[:], in_=rstd.rearrange("b (q j) -> (b q) j", j=SLOTS))
+        load_grad(0, 0, 0, 4, nc.sync)
+        load_grad(0, 2, 0, 4, nc.scalar)
+        load_grad(0, 1, 0, 4, nc.sync)
+        nc.scalar.dma_start(out=gain_row[0:1, :], in_=g.rearrange("(o e) -> o e", o=1))
+        load_grad(0, 3, 0, 4, nc.scalar)
+        load_grad(0, 2, 4, 8, nc.scalar)
+        load_grad(0, 3, 4, 8, nc.scalar)
+        load_grad(0, 0, 4, 8, nc.sync)
+        load_grad(0, 1, 4, 8, nc.sync)
+        load_w(0, 0)
+        load_x(0)
+        load_w(1, 0)
+        load_grad(1, 0, 0, HEADS, nc.sync)
+        load_grad(1, 1, 0, HEADS, nc.sync)
+        load_w(1, 1)
+        load_w(0, 1)
+        load_x(1)
+
+        positions = kept("positions", [P, SLOTS], I32)
+        theta_hi = kept("theta_hi", [P, 8], F32)
+        theta_lo = kept("theta_lo", [P, 8], F32)
+        theta = kept("theta", [P, 8, 8], F32)
+        turn_unit = kept("turn_unit", [P, SLOTS], F32)
+        turns = kept("turns", [P, SLOTS, HD // 2], F32)
+        whole = kept("whole", [P, SLOTS, HD // 2], I32)
+        fraction = kept("fraction", [P, SLOTS, HD // 2], F32)
+        cosines = kept("cosines", [P, SLOTS, HD], F32)
+        nc.vector.memset(theta_hi[:], 1.0)
+        nc.vector.memset(theta_lo[:], 1.0)
+        for s in (1, 2, 4):
+            nc.vector.tensor_single_scalar(theta_hi[:, s : 2 * s], theta_hi[:, 0:s], 10000.0 ** (-s / 8.0), ALU.mult)
+            nc.vector.tensor_single_scalar(theta_lo[:, s : 2 * s], theta_lo[:, 0:s], 10000.0 ** (-s / 64.0), ALU.mult)
+        nc.vector.tensor_single_scalar(positions[:], tokens[:], L - 1, ALU.bitwise_and)
+        nc.vector.tensor_tensor(theta[:], theta_hi[:].unsqueeze(2).to_broadcast([P, 8, 8]),
+                                theta_lo[:].unsqueeze(1).to_broadcast([P, 8, 8]), ALU.mult)
+        nc.vector.tensor_single_scalar(turn_unit[:], positions[:], 0.5 / math.pi, ALU.mult)
+        nc.vector.tensor_tensor(turns[:], theta[:].rearrange("p a b -> p (a b)").unsqueeze(1).to_broadcast([P, SLOTS, HD // 2]),
+                                turn_unit[:].unsqueeze(2).to_broadcast([P, SLOTS, HD // 2]), ALU.mult)
+        nc.vector.tensor_single_scalar(whole[:], turns[:], 0.25, ALU.add)
+        nc.vector.scalar_tensor_tensor(fraction[:].rearrange("p j i -> p (j i)"), turns[:].rearrange("p j i -> p (j i)"), 0.25,
+                                       whole[:].rearrange("p j i -> p (j i)"), ALU.add, ALU.subtract)
+        nc.scalar.activation(out=cosines[:].rearrange("p j (i s) -> p (j i) s", s=2),
+                             in_=fraction[:].rearrange("p j i -> p (j i)").unsqueeze(2).to_broadcast([P, SLOTS * HD // 2, 2]),
+                             func=ACT.Sin, scale=2.0 * math.pi)
+        nc.vector.scalar_tensor_tensor(neg_r2[:], rstd_sb[:], -1.0 / E, rstd_sb[:], ALU.mult, ALU.mult)
+
+        gain = psum.tile([P, E], BF16, name="gain", tag="dh", bufs=2)
+        for h in range(2):
+            cols = slice(h * HALF, (h + 1) * HALF)
+            nc.tensor.matmul(gain[:, cols], lhsT=ones[:], rhs=gain_row[:, cols], start=True, stop=True)
+
+        banks = {}
+
+        def dk(b):
+            load_grad(1, b, 0, HEADS, nc.scalar)
+
+        def rg_step(h, j):
+            nc.scalar.activation(out=rg[:, h, j], in_=gain[:, h * HALF : (h + 1) * HALF], func=ACT.Copy, scale=rstd_sb[:, j : j + 1])
+
+        def rope(u):
+            for n in range(4):
+                nc.vector.tensor_tensor(
+                    out=dz_tok[u][:, n * HD : (n + 1) * HD, :].rearrange("p (c i) j -> p c j i", i=4),
+                    in0=grad_sb[u // 2][:, 4 * (u % 2) + n].rearrange("p j (c i) -> p c j i", i=4),
+                    in1=cosines[:].rearrange("p j (c i) -> p c j i", i=4),
+                    op=ALU.mult)
+
+        def norm(h):
+            for c in range(2):
+                cols = slice(c * HALF // 2, (c + 1) * HALF // 2)
+                nc.vector.tensor_tensor(
+                    out=h_tok[h][:, cols, :].rearrange("p (c i) j -> p c j i", i=4),
+                    in0=x_sb[:, h, :, cols].rearrange("p j (c i) -> p c j i", i=4),
+                    in1=rg[:, h, :, cols].rearrange("p j (c i) -> p c j i", i=4),
+                    op=ALU.mult)
+
+        def quantize(pair, dtype, values):
+            nc.vector.quantize_mx(out=pair[0][:].bitcast(dtype), scales=pair[1][:], in_=values)
+
+        def qz(u):
+            quantize(dz_tok_q[u], E5M2, dz_tok[u][:].rearrange("p c j -> p (c j)"))
+
+        def qh(h):
+            quantize(h_q[h], E4M3, h_tok[h][:].rearrange("p c j -> p (c j)"))
+
+        def qt(u):
+            quantize(dz_feat_q[u], E5M2, dz_feat[u][:].rearrange("p j q t -> p (j q t)"))
+
+        def qw(u, h):
+            quantize(w_q[u][h], E4M3, w_feat[u][h][:].rearrange("p c t -> p (c t)"))
+
+        def tz(u, jp):
+            bank = psum.tile([P, 4, P], F32, name="tr", tag="tr", bufs=3)
+            words = dz_tok[u][:].rearrange("p c j -> p (c j)").bitcast(F32)
+            for t in range(4):
+                nc.tensor.transpose(bank[:, t, :], words[:, 2 * t + jp : 2 * UNIT : 8], identity[:])
+            banks["z", u, jp] = bank
+
+        def tw(u, h, ip):
+            bank = psum.tile([P, 4, P], F32, name="tr", tag="tr", bufs=3)
+            words = w_sb[u // 2][h][:].rearrange("p i f -> p (i f)").bitcast(F32)
+            for i in range(2):
+                first = (2 * ip + i) * (J // 2) + (u % 2) * (UNIT // 2)
+                for s in range(2):
+                    nc.tensor.transpose(bank[:, 2 * i + s, :], words[:, first + s : first + UNIT // 2 : 2], identity[:])
+            banks["w", u, h, ip] = bank
+
+        def dw(u, e):
+            bank = psum.tile([P, UNIT], F32, name="dw", tag="dw", bufs=3)
+            lhs, lhs_scale = h_q[e // 4]
+            rhs, rhs_scale = dz_tok_q[u]
+            cols = slice((e % 4) * P, (e % 4 + 1) * P)
+            nc.tensor.matmul_mx(out=bank[:], lhsT=lhs[:, cols].bitcast(E4M3), lhsT_scale=lhs_scale[:, cols],
+                                rhs=rhs[:].bitcast(E5M2), rhs_scale=rhs_scale[:], start=True, stop=True)
+            banks["d", u, e] = bank
+
+        def copy(on_vector, out, in_):
+            if on_vector:
+                nc.vector.tensor_copy(out=out, in_=in_)
+            else:
+                nc.scalar.copy(out=out, in_=in_)
+
+        def cz(on_vector, u, jp):
+            bank = banks["z", u, jp]
+            copy(on_vector, dz_feat[u][:, 2 * jp : 2 * jp + 2],
+                 bank[:].rearrange("p t q -> p (t q)").bitcast(BF16).rearrange("p (t q s) -> p s q t", t=4, s=2))
+
+        def cw(on_vector, u, h, ip):
+            bank = banks["w", u, h, ip]
+            rows = w_feat[u][h][:].rearrange("p c t -> p (c t)").bitcast(F32).rearrange("p (q w) -> p q w", w=8)
+            copy(on_vector, rows[:, :, 4 * ip : 4 * ip + 4], bank[:].rearrange("p w q -> p q w"))
+
+        def cd(on_vector, u, e):
+            tile = reused.tile([P, UNIT], F32, name="store", tag="store", bufs=8)
+            copy(on_vector, tile[:], banks["d", u, e][:])
+            nc.sync.dma_start(out=weight_grads[u // 2][e * P : (e + 1) * P, (u % 2) * UNIT : (u % 2 + 1) * UNIT], in_=tile[:])
+
+        def dh(j, h):
+            bank = psum.tile([P, HALF], F32, name="dh", tag="dh", bufs=2)
+            cols = slice(j * P, (j + 1) * P)
+            for u in range(UNITS):
+                lhs, lhs_scale = dz_feat_q[u]
+                rhs, rhs_scale = w_q[u][h]
+                nc.tensor.matmul_mx(out=bank[:], lhsT=lhs[:, cols].bitcast(E5M2), lhsT_scale=lhs_scale[:, cols],
+                                    rhs=rhs[:].bitcast(E4M3), rhs_scale=rhs_scale[:], start=(u == 0), stop=(u == UNITS - 1))
+            banks["h", j, h] = bank
+
+        def scale(j, h):
+            nc.vector.tensor_tensor(out=scaled[j][:, h], in0=banks["h", j, h][:], in1=rg[:, h, j], op=ALU.mult)
+
+        def dot(j):
+            product = reused.tile([P, 2, HALF], F32, name="product", tag="product", bufs=2)
+            nc.vector.scalar_tensor_tensor(product[:], x_sb[:, :, j], neg_r2[:, j : j + 1], scaled[j], ALU.mult, ALU.mult,
+                                           accum_out=coef[j][:])
+
+        def out(j, pieces):
+            result = reused.tile([P, 2, HALF], F32, name="result", tag="result", bufs=2)
+            for piece in pieces:
+                nc.vector.scalar_tensor_tensor(result[:, piece], x_sb[:, piece, j], coef[j][:], scaled[j][:, piece], ALU.mult, ALU.add)
+                nc.sync.dma_start(out=out_rows[:, j, piece], in_=result[:, piece])
+
+        steps = {"dk": dk, "rope": rope, "norm": norm, "qz": qz, "qh": qh, "qt": qt, "qw": qw, "tz": tz, "tw": tw, "dw": dw,
+                 "dh": dh, "rg": rg_step, "gain": scale, "dot": dot}
+        copies = {"cz": cz, "cw": cw, "cd": cd}
+        order = ORDER.split()
+        for step in order:
+            digits = [int(c) for c in step if c in "0123456789"]
+            kind = [k for k in list(steps) + list(copies) + ["out"] if step.startswith(k)][0]
+            if kind in copies:
+                copies[kind](step[-1] == "v", *digits)
+            elif kind == "out":
+                out(digits[0], [slice(0, 1), slice(1, 2)] if step == order[-1] else [slice(0, 2)])
+            else:
+                steps[kind](*digits)

@@ -24,49 +24,6 @@ HALF = 512
 UNITS = 2 * J // UNIT
 FLOPS = 2 * 2 * T * E * 2 * J
 
-ORDER = """
-rope0 rg03 rg13
-rope1 rg12 rg02 dk2 dk3
-qz0 rg11 rg00
-qz1 tz01 rg01 tw101 cz01
-norm0 tz00 cw101 tw001 cz00
-qt0 tw000 cw001 tz11 cw000
-rope2 tw200 cz11 cw200
-rope3 tz10 rg10 cz10
-qh0 tw100 tw201 cw100 tz21 cw201
-norm1 tw301 cz21
-qz2 tw210 cw301 tw110 cw210
-qh1 tz30 cw110 tw300 cz30
-qw20 tz20 cw300 dw10 cz20
-qw10 dw20 cd10 dw00 cd20
-qt1 tz31 cd00 tw310 cz31v
-qz3 dw04 cw310 dw14 cd04
-qw00 tw311 cd14 dw11 cw311
-qw30 cd11 tw111 tw211 cw111
-qt2 dw21 cw211 dw05 cd21
-qt3 tw010 cd05v dw15 cw010v dh10
-qw11 tw011 cd15 cw011
-qw31
-gain10 dw01 dh00
-qw21 cd01 dw30 cd30
-qw01 dw02 dw16 cd02v cd16 dh11
-gain00 dw34 dw35 cd34
-gain11 dw31 cd35 dh20
-dot1 cd31 dw24 cd24 dw06 dh01
-gain20 dw17 cd06
-out1 cd17 dw36 dw07 cd36 cd07 dh31
-gain01 dw25
-dot0 dw37 cd25 dw12 cd37 cd12 dh21
-gain31 dw32 cd32
-out0 dw26 cd26 dw33 cd33 dh30
-gain21
-dot2 dw13 dw22 cd13
-gain30 dw03 cd22
-out2 dw23 cd03 cd23 dw27 cd27
-dot3
-out3
-"""
-
 
 def tile_llamaselfattentionblock_pa_v_kernel(tc, x, g, wq, wk, rstd, grad_0, grad_1, out_0, out_1, out_2):
     nc = tc.nc
@@ -74,7 +31,7 @@ def tile_llamaselfattentionblock_pa_v_kernel(tc, x, g, wq, wk, rstd, grad_0, gra
     weights = (wq, wk)
     weight_grads = (out_1, out_2)
     x_rows = x.flatten_outer_dims().rearrange("(p j) e -> p j e", j=SLOTS)
-    out_rows = out_0.flatten_outer_dims().rearrange("(p j) (h e) -> p j h e", j=SLOTS, h=2)
+    out_rows = out_0.flatten_outer_dims().rearrange("(p j) e -> p j e", j=SLOTS)
 
     with ExitStack() as ctx:
         keep = ctx.enter_context(tc.tile_pool(name="keep", bufs=1))
@@ -84,38 +41,37 @@ def tile_llamaselfattentionblock_pa_v_kernel(tc, x, g, wq, wk, rstd, grad_0, gra
         def kept(name, shape, dtype):
             return keep.tile(shape, dtype, name=name, align_bytes=64)
 
+        def rotating(tag, shape, dtype, bufs):
+            return reused.tile(shape, dtype, name=tag, tag=tag, bufs=bufs, align_bytes=64)
+
         def codes(name):
             return kept(name + "_codes", [P, 512], U32), kept(name + "_scales", [P, 512], U8)
 
-        grad_sb = [reused.tile([P, HEADS, SLOTS, HD], BF16, name="grad%d" % a, tag="early_late", bufs=2, align_bytes=64) for a in range(2)]
-        pairs = [reused.tile([P, 2, 2, HALF], F32, name="pair%d" % i, tag="early_late", bufs=2, align_bytes=64) for i in range(2)]
-        scaled = [pairs[j // 2][:, j % 2] for j in range(SLOTS)]
+        dq_sb = [kept("dq%d" % u, [P, 4, SLOTS, HD], BF16) for u in range(2)]
+        dk_sb = kept("dk", [P, HEADS, SLOTS, HD], BF16)
+        grad_sb = [dq_sb[0][:], dq_sb[1][:], dk_sb[:, 0:4], dk_sb[:, 4:8]]
+        scaled = [kept("scaled%d" % j, [P, E], F32) for j in range(SLOTS)]
         rstd_sb = kept("rstd_sb", [P, SLOTS], F32)
         gain_row = kept("gain_row", [P, E], BF16)
         ones = kept("ones", [P, P], BF16)
         identity = kept("identity", [P, P], F32)
-        x_sb = kept("x_sb", [P, 2, SLOTS, HALF], BF16)
+        x_sb = kept("x_sb", [P, SLOTS, E], BF16)
         rg = kept("rg", [P, 2, SLOTS, HALF], F32)
         w_sb = [[kept("w%d%d" % (a, h), [P, 4, J], BF16) for h in range(2)] for a in range(2)]
         h_tok = [kept("h_tok%d" % h, [P, HALF, SLOTS], BF16) for h in range(2)]
-        dz_tok = [kept("dz_tok%d" % u, [P, UNIT, SLOTS], BF16) for u in range(UNITS)]
-        dz_feat = [kept("dz_feat%d" % u, [P, SLOTS, P, 4], BF16) for u in range(UNITS)]
-        w_feat = [[kept("w_feat%d%d" % (u, h), [P, HALF, 4], BF16) for h in range(2)] for u in range(UNITS)]
         h_q = [codes("h_q%d" % h) for h in range(2)]
         dz_tok_q = [codes("dz_tok_q%d" % u) for u in range(UNITS)]
         dz_feat_q = [codes("dz_feat_q%d" % u) for u in range(UNITS)]
         w_q = [[codes("w_q%d%d" % (u, h)) for h in range(2)] for u in range(UNITS)]
         neg_r2 = kept("neg_r2", [P, SLOTS], F32)
         coef = [kept("coef%d" % j, [P, 1], F32) for j in range(SLOTS)]
+        dz, dz_tok, dz_feat, w_feat, dh_bank, dw_rows = {}, {}, {}, {}, {}, {}
 
         ctx.enter_context(tc.manual_schedule())
 
-        def load_grad(a, b, n0, n1, queue):
-            queue.dma_start(out=grad_sb[a][32 * b : 32 * b + 32, n0:n1].rearrange("q n j d -> q n (j d)"),
+        def load_grad(dst, a, b, n0, n1, queue):
+            queue.dma_start(out=dst[32 * b : 32 * b + 32].rearrange("q n j d -> q n (j d)"),
                             in_=grads[a][b, n0:n1].rearrange("n (q j) d -> q n (j d)", j=SLOTS))
-
-        def load_x(h):
-            nc.sync.dma_start(out=x_sb[:, h], in_=x_rows[:, :, h * HALF : (h + 1) * HALF])
 
         def load_w(a, h):
             nc.sync.dma_start(out=w_sb[a][h][:], in_=weights[a][h * HALF : (h + 1) * HALF, :].rearrange("(q i) f -> q i f", i=4))
@@ -125,24 +81,20 @@ def tile_llamaselfattentionblock_pa_v_kernel(tc, x, g, wq, wk, rstd, grad_0, gra
         make_identity(nc, identity[:])
         nc.vector.memset(gain_row[:], 0.0)
         nc.vector.memset(ones[:], 1.0)
+        for b in range(2):
+            load_grad(dq_sb[0], 0, b, 0, 4, nc.sync)
+            load_grad(dq_sb[0], 0, b + 2, 0, 4, nc.scalar)
         nc.sync.dma_start(out=rstd_sb[:], in_=rstd.rearrange("b (q j) -> (b q) j", j=SLOTS))
-        load_grad(0, 0, 0, 4, nc.sync)
-        load_grad(0, 2, 0, 4, nc.scalar)
-        load_grad(0, 1, 0, 4, nc.sync)
-        nc.scalar.dma_start(out=gain_row[0:1, :], in_=g.rearrange("(o e) -> o e", o=1))
-        load_grad(0, 3, 0, 4, nc.scalar)
-        load_grad(0, 2, 4, 8, nc.scalar)
-        load_grad(0, 3, 4, 8, nc.scalar)
-        load_grad(0, 0, 4, 8, nc.sync)
-        load_grad(0, 1, 4, 8, nc.sync)
+        nc.sync.dma_start(out=gain_row[0:1, :], in_=g.rearrange("(o e) -> o e", o=1))
+        nc.sync.dma_start(out=x_sb[:], in_=x_rows)
         load_w(0, 0)
-        load_x(0)
+        for b in range(2):
+            load_grad(dq_sb[1], 0, b, 4, 8, nc.sync)
         load_w(1, 0)
-        load_grad(1, 0, 0, HEADS, nc.sync)
-        load_grad(1, 1, 0, HEADS, nc.sync)
-        load_w(1, 1)
+        for b in range(2):
+            load_grad(dk_sb, 1, b, 0, HEADS, nc.sync)
         load_w(0, 1)
-        load_x(1)
+        load_w(1, 1)
 
         positions = kept("positions", [P, SLOTS], I32)
         theta_hi = kept("theta_hi", [P, 8], F32)
@@ -152,7 +104,7 @@ def tile_llamaselfattentionblock_pa_v_kernel(tc, x, g, wq, wk, rstd, grad_0, gra
         turns = kept("turns", [P, SLOTS, HD // 2], F32)
         whole = kept("whole", [P, SLOTS, HD // 2], I32)
         fraction = kept("fraction", [P, SLOTS, HD // 2], F32)
-        cosines = kept("cosines", [P, SLOTS, HD], F32)
+        cosines = kept("cosines", [P, 2, SLOTS * HD // 2], F32)
         nc.vector.memset(theta_hi[:], 1.0)
         nc.vector.memset(theta_lo[:], 1.0)
         for s in (1, 2, 4):
@@ -167,40 +119,46 @@ def tile_llamaselfattentionblock_pa_v_kernel(tc, x, g, wq, wk, rstd, grad_0, gra
         nc.vector.tensor_single_scalar(whole[:], turns[:], 0.25, ALU.add)
         nc.vector.scalar_tensor_tensor(fraction[:].rearrange("p j i -> p (j i)"), turns[:].rearrange("p j i -> p (j i)"), 0.25,
                                        whole[:].rearrange("p j i -> p (j i)"), ALU.add, ALU.subtract)
-        nc.scalar.activation(out=cosines[:].rearrange("p j (i s) -> p (j i) s", s=2),
-                             in_=fraction[:].rearrange("p j i -> p (j i)").unsqueeze(2).to_broadcast([P, SLOTS * HD // 2, 2]),
+
+        nc.scalar.activation(out=cosines[:].rearrange("p v (k s) -> p v k s", s=2),
+                             in_=fraction[:].rearrange("p j (w v) -> p v (j w)", v=2).unsqueeze(3).to_broadcast([P, 2, P, 2]),
                              func=ACT.Sin, scale=2.0 * math.pi)
         nc.vector.scalar_tensor_tensor(neg_r2[:], rstd_sb[:], -1.0 / E, rstd_sb[:], ALU.mult, ALU.mult)
 
-        gain = psum.tile([P, E], BF16, name="gain", tag="dh", bufs=2)
+        gain = psum.tile([P, E], BF16, name="gain", tag="dh", bufs=4)
         for h in range(2):
             cols = slice(h * HALF, (h + 1) * HALF)
             nc.tensor.matmul(gain[:, cols], lhsT=ones[:], rhs=gain_row[:, cols], start=True, stop=True)
-
-        banks = {}
-
-        def dk(b):
-            load_grad(1, b, 0, HEADS, nc.scalar)
 
         def rg_step(h, j):
             nc.scalar.activation(out=rg[:, h, j], in_=gain[:, h * HALF : (h + 1) * HALF], func=ACT.Copy, scale=rstd_sb[:, j : j + 1])
 
         def rope(u):
-            for n in range(4):
-                nc.vector.tensor_tensor(
-                    out=dz_tok[u][:, n * HD : (n + 1) * HD, :].rearrange("p (c i) j -> p c j i", i=4),
-                    in0=grad_sb[u // 2][:, 4 * (u % 2) + n].rearrange("p j (c i) -> p c j i", i=4),
-                    in1=cosines[:].rearrange("p j (c i) -> p c j i", i=4),
-                    op=ALU.mult)
+            dz[u] = rotating("dz", [P, SLOTS, 2, UNIT // 2], BF16, 2)
+            pairs = grad_sb[u].rearrange("p n j (w v s) -> p (n j w) v s", v=2, s=2)
+            for v in range(2):
+                nc.vector.tensor_tensor(out=dz[u][:, :, v, :].rearrange("p j (n c) -> p n j c", n=4), in0=pairs[:, :, v, :],
+                                        in1=cosines[:, v, :].unsqueeze(1).to_broadcast([P, 4, SLOTS * HD // 2]), op=ALU.mult)
 
-        def norm(h):
-            for c in range(2):
-                cols = slice(c * HALF // 2, (c + 1) * HALF // 2)
-                nc.vector.tensor_tensor(
-                    out=h_tok[h][:, cols, :].rearrange("p (c i) j -> p c j i", i=4),
-                    in0=x_sb[:, h, :, cols].rearrange("p j (c i) -> p c j i", i=4),
-                    in1=rg[:, h, :, cols].rearrange("p j (c i) -> p c j i", i=4),
-                    op=ALU.mult)
+        def copy(engine, out, in_):
+            if engine == "V":
+                nc.vector.tensor_copy(out=out, in_=in_)
+            else:
+                nc.scalar.copy(out=out, in_=in_)
+
+        def interleave(u, engine="V"):
+            dz_tok[u] = rotating("dz_tok", [P, UNIT, SLOTS], BF16, 2)
+            copy(engine, dz_tok[u][:].rearrange("p (c i) j -> p c j i", i=4),
+                 dz[u][:].rearrange("p j v c -> p j (v c)").rearrange("p j (c i) -> p c j i", i=4))
+
+        def norm(h, c):
+            cols = slice(c * HALF // 2, (c + 1) * HALF // 2)
+            x_cols = slice(h * HALF + cols.start, h * HALF + cols.stop)
+            nc.vector.tensor_tensor(
+                out=h_tok[h][:, cols, :].rearrange("p (c i) j -> p c j i", i=4),
+                in0=x_sb[:, :, x_cols].rearrange("p j (c i) -> p c j i", i=4),
+                in1=rg[:, h, :, cols].rearrange("p j (c i) -> p c j i", i=4),
+                op=ALU.mult)
 
         def quantize(pair, dtype, values):
             nc.vector.quantize_mx(out=pair[0][:].bitcast(dtype), scales=pair[1][:], in_=values)
@@ -212,91 +170,121 @@ def tile_llamaselfattentionblock_pa_v_kernel(tc, x, g, wq, wk, rstd, grad_0, gra
             quantize(h_q[h], E4M3, h_tok[h][:].rearrange("p c j -> p (c j)"))
 
         def qt(u):
-            quantize(dz_feat_q[u], E5M2, dz_feat[u][:].rearrange("p j q t -> p (j q t)"))
+            quantize(dz_feat_q[u], E5M2, dz_feat[u][:])
 
         def qw(u, h):
-            quantize(w_q[u][h], E4M3, w_feat[u][h][:].rearrange("p c t -> p (c t)"))
+            quantize(w_q[u][h], E4M3, w_feat[u, h][:])
 
-        def tz(u, jp):
-            bank = psum.tile([P, 4, P], F32, name="tr", tag="tr", bufs=3)
-            words = dz_tok[u][:].rearrange("p c j -> p (c j)").bitcast(F32)
-            for t in range(4):
-                nc.tensor.transpose(bank[:, t, :], words[:, 2 * t + jp : 2 * UNIT : 8], identity[:])
-            banks["z", u, jp] = bank
+        def stream_bank(shape):
+            return psum.tile(shape, F32, name="stream", tag="stream", bufs=4)
 
-        def tw(u, h, ip):
-            bank = psum.tile([P, 4, P], F32, name="tr", tag="tr", bufs=3)
+        def turn_dz(u, jp, engine="S"):
+            if jp == 0:
+                dz_feat[u] = rotating("dz_feat", [P, 4 * T], BF16, 2)
+            bank = stream_bank([P, 4, P])
+            words = dz[u][:].rearrange("p j v c -> p (j v c)").bitcast(F32)
+            for k in range(4):
+                first = (4 * jp + k) * P
+                nc.tensor.transpose(bank[:, k, :], words[:, first : first + P], identity[:])
+            rows = dz_feat[u][:].bitcast(F32)[:, jp * 4 * P : (jp + 1) * 4 * P]
+            copy(engine, rows.rearrange("p (j q v) -> p j q v", j=2, v=2), bank[:].rearrange("p (j v) q -> p j q v", v=2))
+
+        def turn_w(u, h, ip, engine="S"):
+            if ip == 0:
+                w_feat[u, h] = rotating("w_feat", [P, 4 * HALF], BF16, 4)
+            bank = stream_bank([P, 4, P])
             words = w_sb[u // 2][h][:].rearrange("p i f -> p (i f)").bitcast(F32)
             for i in range(2):
                 first = (2 * ip + i) * (J // 2) + (u % 2) * (UNIT // 2)
                 for s in range(2):
                     nc.tensor.transpose(bank[:, 2 * i + s, :], words[:, first + s : first + UNIT // 2 : 2], identity[:])
-            banks["w", u, h, ip] = bank
+            rows = w_feat[u, h][:].bitcast(F32).rearrange("p (q w) -> p q w", w=8)
+            copy(engine, rows[:, :, 4 * ip : 4 * ip + 4], bank[:].rearrange("p w q -> p q w"))
 
-        def dw(u, e):
-            bank = psum.tile([P, UNIT], F32, name="dw", tag="dw", bufs=3)
+        def dw(u, e, engine="S"):
+            bank = stream_bank([P, UNIT])
             lhs, lhs_scale = h_q[e // 4]
             rhs, rhs_scale = dz_tok_q[u]
             cols = slice((e % 4) * P, (e % 4 + 1) * P)
             nc.tensor.matmul_mx(out=bank[:], lhsT=lhs[:, cols].bitcast(E4M3), lhsT_scale=lhs_scale[:, cols],
                                 rhs=rhs[:].bitcast(E5M2), rhs_scale=rhs_scale[:], start=True, stop=True)
-            banks["d", u, e] = bank
+            if u % 2 == 0:
+                dw_rows[u // 2, e] = rotating("dw_rows", [P, J], F32, 6)
+            rows = dw_rows[u // 2, e]
+            copy(engine, rows[:, (u % 2) * UNIT : (u % 2 + 1) * UNIT].rearrange("p (m v s) -> p m v s", v=2, s=2),
+                 bank[:].rearrange("p (v m s) -> p m v s", v=2, s=2))
+            if u % 2 == 1:
+                nc.sync.dma_start(out=weight_grads[u // 2][e * P : (e + 1) * P, :], in_=rows[:])
 
-        def copy(on_vector, out, in_):
-            if on_vector:
-                nc.vector.tensor_copy(out=out, in_=in_)
-            else:
-                nc.scalar.copy(out=out, in_=in_)
-
-        def cz(on_vector, u, jp):
-            bank = banks["z", u, jp]
-            copy(on_vector, dz_feat[u][:, 2 * jp : 2 * jp + 2],
-                 bank[:].rearrange("p t q -> p (t q)").bitcast(BF16).rearrange("p (t q s) -> p s q t", t=4, s=2))
-
-        def cw(on_vector, u, h, ip):
-            bank = banks["w", u, h, ip]
-            rows = w_feat[u][h][:].rearrange("p c t -> p (c t)").bitcast(F32).rearrange("p (q w) -> p q w", w=8)
-            copy(on_vector, rows[:, :, 4 * ip : 4 * ip + 4], bank[:].rearrange("p w q -> p q w"))
-
-        def cd(on_vector, u, e):
-            tile = reused.tile([P, UNIT], F32, name="store", tag="store", bufs=8)
-            copy(on_vector, tile[:], banks["d", u, e][:])
-            nc.sync.dma_start(out=weight_grads[u // 2][e * P : (e + 1) * P, (u % 2) * UNIT : (u % 2 + 1) * UNIT], in_=tile[:])
-
-        def dh(j, h):
-            bank = psum.tile([P, HALF], F32, name="dh", tag="dh", bufs=2)
+        def dh(j, h, u):
+            if u == 0:
+                dh_bank[j, h] = psum.tile([P, HALF], F32, name="dh", tag="dh", bufs=4)
             cols = slice(j * P, (j + 1) * P)
-            for u in range(UNITS):
-                lhs, lhs_scale = dz_feat_q[u]
-                rhs, rhs_scale = w_q[u][h]
-                nc.tensor.matmul_mx(out=bank[:], lhsT=lhs[:, cols].bitcast(E5M2), lhsT_scale=lhs_scale[:, cols],
-                                    rhs=rhs[:].bitcast(E4M3), rhs_scale=rhs_scale[:], start=(u == 0), stop=(u == UNITS - 1))
-            banks["h", j, h] = bank
+            lhs, lhs_scale = dz_feat_q[u]
+            rhs, rhs_scale = w_q[u][h]
+            nc.tensor.matmul_mx(out=dh_bank[j, h][:], lhsT=lhs[:, cols].bitcast(E5M2), lhsT_scale=lhs_scale[:, cols],
+                                rhs=rhs[:].bitcast(E4M3), rhs_scale=rhs_scale[:], start=(u == 0), stop=(u == UNITS - 1))
 
         def scale(j, h):
-            nc.vector.tensor_tensor(out=scaled[j][:, h], in0=banks["h", j, h][:], in1=rg[:, h, j], op=ALU.mult)
+            nc.vector.tensor_tensor(out=scaled[j][:, h * HALF : (h + 1) * HALF], in0=dh_bank[j, h][:], in1=rg[:, h, j], op=ALU.mult)
 
         def dot(j):
-            product = reused.tile([P, 2, HALF], F32, name="product", tag="product", bufs=2)
-            nc.vector.scalar_tensor_tensor(product[:], x_sb[:, :, j], neg_r2[:, j : j + 1], scaled[j], ALU.mult, ALU.mult,
+            product = rotating("product", [P, E], F32, 2)
+            nc.vector.scalar_tensor_tensor(product[:], x_sb[:, j], neg_r2[:, j : j + 1], scaled[j][:], ALU.mult, ALU.mult,
                                            accum_out=coef[j][:])
 
-        def out(j, pieces):
-            result = reused.tile([P, 2, HALF], F32, name="result", tag="result", bufs=2)
-            for piece in pieces:
-                nc.vector.scalar_tensor_tensor(result[:, piece], x_sb[:, piece, j], coef[j][:], scaled[j][:, piece], ALU.mult, ALU.add)
-                nc.sync.dma_start(out=out_rows[:, j, piece], in_=result[:, piece])
+        def out(j, pieces=1):
+            result = rotating("result", [P, E], F32, 2)
+            for k in range(pieces):
+                cols = slice(k * E // pieces, (k + 1) * E // pieces)
+                nc.vector.scalar_tensor_tensor(result[:, cols], x_sb[:, j, cols], coef[j][:], scaled[j][:, cols], ALU.mult, ALU.add)
+                nc.sync.dma_start(out=out_rows[:, j, cols], in_=result[:, cols])
 
-        steps = {"dk": dk, "rope": rope, "norm": norm, "qz": qz, "qh": qh, "qt": qt, "qw": qw, "tz": tz, "tw": tw, "dw": dw,
-                 "dh": dh, "rg": rg_step, "gain": scale, "dot": dot}
-        copies = {"cz": cz, "cw": cw, "cd": cd}
-        order = ORDER.split()
-        for step in order:
-            digits = [int(c) for c in step if c in "0123456789"]
-            kind = [k for k in list(steps) + list(copies) + ["out"] if step.startswith(k)][0]
-            if kind in copies:
-                copies[kind](step[-1] == "v", *digits)
-            elif kind == "out":
-                out(digits[0], [slice(0, 1), slice(1, 2)] if step == order[-1] else [slice(0, 2)])
-            else:
-                steps[kind](*digits)
+        for h in range(2):
+            for j in range(4): rg_step(h,j)
+        for b in range(2, 4): load_grad(dq_sb[1], 0, b, 4, 8, nc.scalar)
+        rope(0)
+        for jp in range(2): turn_dz(0,jp)
+        norm(0,0); interleave(0); norm(0,1); qz(0); qh(0)
+        for u in range(2):
+            for ip in range(2): turn_w(u,0,ip)
+        for b in range(2, 4): load_grad(dk_sb, 1, b, 0, HEADS, nc.scalar)
+        rope(1)
+        for e in range(4): dw(0,e)
+        for jp in range(2): turn_dz(1,jp)
+        qt(0); interleave(1); qw(0,0); qz(1)
+        for ip in range(2): turn_w(2,0,ip)
+        for j in range(4): dh(j,0,0)
+        for ip in range(2): turn_w(3,0,ip)
+        norm(1,0); norm(1,1); qt(1); qh(1); qw(1,0)
+        for e in range(4): dw(1,e)
+        for ip in range(2): turn_w(0,1,ip)
+        rope(2)
+        dw(0,4); dw(1,4)
+        for j in range(4): dh(j,0,1)
+        for jp in range(2): turn_dz(2,jp)
+        rope(3)
+        dw(0,5); dw(1,5)
+        for ip in range(2): turn_w(1,1,ip)
+        dw(0,6); dw(1,6)
+        for jp in range(2): turn_dz(3,jp)
+        interleave(2); qt(2); qw(2,0); interleave(3); qz(2); qt(3); qz(3); qw(3,0)
+        dw(0,7); dw(1,7)
+        for j in range(4): dh(j,0,2)
+        for ip in range(2): turn_w(2,1,ip)
+        dw(2,0); dw(3,0)
+        for j in range(4): dh(j,0,3)
+        for ip in range(2): turn_w(3,1,ip)
+        qw(0,1); qw(1,1)
+        for j in range(4): scale(j,0)
+        qw(2,1); qw(3,1)
+        dw(2,1); dw(3,1)
+        dw(2,2); dw(3,2)
+        for j in range(4):
+            for u in range(4): dh(j,1,u)
+            dw(2,3+j); dw(3,3+j)
+            scale(j,1)
+            if j>0: out(j-1)
+            dot(j)
+        dw(2,7); dw(3,7)
+        out(3,2)

@@ -44,25 +44,24 @@ def tile_llamaselfattentionblock_pa_v_kernel(tc, x, g, wq, wk, rstd, grad_0, gra
         def rotating(tag, shape, dtype, bufs):
             return reused.tile(shape, dtype, name=tag, tag=tag, bufs=bufs, align_bytes=64)
 
-        def codes(name):
-            return kept(name + "_codes", [P, 512], U32), kept(name + "_scales", [P, 512], U8)
+        def codes(name, width=512):
+            return kept(name + "_codes", [P, width], U32), kept(name + "_scales", [P, width], U8)
 
         dq_sb = [kept("dq%d" % u, [P, 4, SLOTS, HD], BF16) for u in range(2)]
         dk_sb = kept("dk", [P, HEADS, SLOTS, HD], BF16)
         grad_sb = [dq_sb[0][:], dq_sb[1][:], dk_sb[:, 0:4], dk_sb[:, 4:8]]
         scaled = [kept("scaled%d" % j, [P, E], F32) for j in range(SLOTS)]
         rstd_sb = kept("rstd_sb", [P, SLOTS], F32)
-        gain_row = kept("gain_row", [P, E], BF16)
-        ones = kept("ones", [P, P], BF16)
+        g_sb = kept("g_sb", [P, E // P], BF16)
         identity = kept("identity", [P, P], F32)
         x_sb = kept("x_sb", [P, SLOTS, E], BF16)
-        rg = kept("rg", [P, 2, SLOTS, HALF], F32)
+        rg = kept("rg", [P, 2, HALF // 4, SLOTS, 4], F32)
         w_sb = [[kept("w%d%d" % (a, h), [P, 4, J], BF16) for h in range(2)] for a in range(2)]
         h_tok = [kept("h_tok%d" % h, [P, HALF, SLOTS], BF16) for h in range(2)]
         h_q = [codes("h_q%d" % h) for h in range(2)]
         dz_tok_q = [codes("dz_tok_q%d" % u) for u in range(UNITS)]
         dz_feat_q = [codes("dz_feat_q%d" % u) for u in range(UNITS)]
-        w_q = [[codes("w_q%d%d" % (u, h)) for h in range(2)] for u in range(UNITS)]
+        w_q = [[codes("w_q%d%d" % (a, h), 2 * HALF) for h in range(2)] for a in range(2)]
         neg_r2 = kept("neg_r2", [P, SLOTS], F32)
         coef = [kept("coef%d" % j, [P, 1], F32) for j in range(SLOTS)]
         dz, dz_tok, dz_feat, w_feat, dh_bank, dw_rows = {}, {}, {}, {}, {}, {}
@@ -79,66 +78,67 @@ def tile_llamaselfattentionblock_pa_v_kernel(tc, x, g, wq, wk, rstd, grad_0, gra
         tokens = kept("tokens", [P, SLOTS], I32)
         nc.gpsimd.iota(tokens[:], pattern=[[1, SLOTS]], base=0, channel_multiplier=SLOTS)
         make_identity(nc, identity[:])
-        nc.vector.memset(gain_row[:], 0.0)
-        nc.vector.memset(ones[:], 1.0)
+        nc.sync.dma_start(out=g_sb[:], in_=g.rearrange("(p c) -> p c", p=P))
+        nc.scalar.dma_start(out=rstd_sb[:], in_=rstd.rearrange("b (q j) -> (b q) j", j=SLOTS))
         for b in range(2):
             load_grad(dq_sb[0], 0, b, 0, 4, nc.sync)
             load_grad(dq_sb[0], 0, b + 2, 0, 4, nc.scalar)
-        nc.sync.dma_start(out=rstd_sb[:], in_=rstd.rearrange("b (q j) -> (b q) j", j=SLOTS))
-        nc.sync.dma_start(out=gain_row[0:1, :], in_=g.rearrange("(o e) -> o e", o=1))
         nc.sync.dma_start(out=x_sb[:], in_=x_rows)
         load_w(0, 0)
-        for b in range(2):
-            load_grad(dq_sb[1], 0, b, 4, 8, nc.sync)
-        load_w(1, 0)
-        for b in range(2):
-            load_grad(dk_sb, 1, b, 0, HEADS, nc.sync)
-        load_w(0, 1)
-        load_w(1, 1)
 
         positions = kept("positions", [P, SLOTS], I32)
-        theta_hi = kept("theta_hi", [P, 8], F32)
-        theta_lo = kept("theta_lo", [P, 8], F32)
-        theta = kept("theta", [P, 8, 8], F32)
-        turn_unit = kept("turn_unit", [P, SLOTS], F32)
+        coarse = kept("coarse", [P, SLOTS, 4], F32)
+        fine = kept("fine", [P, 16], F32)
         turns = kept("turns", [P, SLOTS, HD // 2], F32)
         whole = kept("whole", [P, SLOTS, HD // 2], I32)
         fraction = kept("fraction", [P, SLOTS, HD // 2], F32)
-        cosines = kept("cosines", [P, 2, SLOTS * HD // 2], F32)
-        nc.vector.memset(theta_hi[:], 1.0)
-        nc.vector.memset(theta_lo[:], 1.0)
-        for s in (1, 2, 4):
-            nc.vector.tensor_single_scalar(theta_hi[:, s : 2 * s], theta_hi[:, 0:s], 10000.0 ** (-s / 8.0), ALU.mult)
-            nc.vector.tensor_single_scalar(theta_lo[:, s : 2 * s], theta_lo[:, 0:s], 10000.0 ** (-s / 64.0), ALU.mult)
+        cos_b = kept("cos_b", [P, 2, P], F32)
+        nc.vector.memset(fine[:, 0:1], 1.0)
         nc.vector.tensor_single_scalar(positions[:], tokens[:], L - 1, ALU.bitwise_and)
-        nc.vector.tensor_tensor(theta[:], theta_hi[:].unsqueeze(2).to_broadcast([P, 8, 8]),
-                                theta_lo[:].unsqueeze(1).to_broadcast([P, 8, 8]), ALU.mult)
-        nc.vector.tensor_single_scalar(turn_unit[:], positions[:], 0.5 / math.pi, ALU.mult)
-        nc.vector.tensor_tensor(turns[:], theta[:].rearrange("p a b -> p (a b)").unsqueeze(1).to_broadcast([P, SLOTS, HD // 2]),
-                                turn_unit[:].unsqueeze(2).to_broadcast([P, SLOTS, HD // 2]), ALU.mult)
-        nc.vector.tensor_single_scalar(whole[:], turns[:], 0.25, ALU.add)
-        nc.vector.scalar_tensor_tensor(fraction[:].rearrange("p j i -> p (j i)"), turns[:].rearrange("p j i -> p (j i)"), 0.25,
-                                       whole[:].rearrange("p j i -> p (j i)"), ALU.add, ALU.subtract)
+        for k in range(1, 4):
+            nc.vector.tensor_single_scalar(fine[:, k : k + 1], fine[:, 0:1], 10000.0 ** (-k / 64.0), ALU.mult)
+        for k in range(4):
+            nc.vector.tensor_single_scalar(coarse[:, :, k], positions[:], 10000.0 ** (-k / 4.0) * 0.5 / math.pi, ALU.mult)
+        for k in range(1, 4):
+            nc.vector.tensor_single_scalar(fine[:, 4 * k : 4 * k + 4], fine[:, 0:4], 10000.0 ** (-k / 16.0), ALU.mult)
+        halves = [slice(0, 2), slice(2, 4)]
+        for js in halves:
+            nc.vector.tensor_tensor(turns[:, js].rearrange("p j (a b) -> p (j a) b", b=16),
+                                    coarse[:, js].rearrange("p j a -> p (j a)").unsqueeze(2).to_broadcast([P, 8, 16]),
+                                    fine[:].unsqueeze(1).to_broadcast([P, 8, 16]), ALU.mult)
+        for js in halves:
+            nc.vector.tensor_single_scalar(whole[:, js], turns[:, js], 0.25, ALU.add)
+        for js in halves:
+            nc.vector.scalar_tensor_tensor(fraction[:, js].rearrange("p j i -> p (j i)"), turns[:, js].rearrange("p j i -> p (j i)"), 0.25,
+                                           whole[:, js].rearrange("p j i -> p (j i)"), ALU.add, ALU.subtract)
 
-        nc.scalar.activation(out=cosines[:].rearrange("p v (k s) -> p v k s", s=2),
-                             in_=fraction[:].rearrange("p j (w v) -> p v (j w)", v=2).unsqueeze(3).to_broadcast([P, 2, P, 2]),
-                             func=ACT.Sin, scale=2.0 * math.pi)
-        nc.vector.scalar_tensor_tensor(neg_r2[:], rstd_sb[:], -1.0 / E, rstd_sb[:], ALU.mult, ALU.mult)
+        def table_b():
+            nc.scalar.activation(out=cos_b[:], in_=fraction[:].rearrange("p j (w v) -> p v (j w)", v=2), func=ACT.Sin, scale=2.0 * math.pi)
 
-        gain = psum.tile([P, E], BF16, name="gain", tag="dh", bufs=4)
-        for h in range(2):
-            cols = slice(h * HALF, (h + 1) * HALF)
-            nc.tensor.matmul(gain[:, cols], lhsT=ones[:], rhs=gain_row[:, cols], start=True, stop=True)
+        def row_factor():
+            nc.vector.scalar_tensor_tensor(neg_r2[:], rstd_sb[:], -1.0 / E, rstd_sb[:], ALU.mult, ALU.mult)
+
+        def load_pair(dst, a, n0, n1):
+            for b in range(2):
+                load_grad(dst, a, b, n0, n1, nc.sync)
+                load_grad(dst, a, b + 2, n0, n1, nc.scalar)
+
+        gain_words = psum.tile([P, P, 4], F32, name="gain", tag="dh", bufs=4)
+        for k in range(4):
+            nc.tensor.transpose(gain_words[:, :, k], g_sb[:].bitcast(F32)[:, k : k + 1].to_broadcast([P, P]), identity[:])
+        gain = gain_words[:].rearrange("p q k -> p (q k)").bitcast(BF16)
 
         def rg_step(h, j):
-            nc.scalar.activation(out=rg[:, h, j], in_=gain[:, h * HALF : (h + 1) * HALF], func=ACT.Copy, scale=rstd_sb[:, j : j + 1])
+            nc.scalar.activation(out=rg[:, h, :, j, :], in_=gain[:, h * HALF : (h + 1) * HALF].rearrange("p (c i) -> p c i", i=4), func=ACT.Copy, scale=rstd_sb[:, j : j + 1])
 
         def rope(u):
             dz[u] = rotating("dz", [P, SLOTS, 2, UNIT // 2], BF16, 2)
             pairs = grad_sb[u].rearrange("p n j (w v s) -> p (n j w) v s", v=2, s=2)
             for v in range(2):
                 nc.vector.tensor_tensor(out=dz[u][:, :, v, :].rearrange("p j (n c) -> p n j c", n=4), in0=pairs[:, :, v, :],
-                                        in1=cosines[:, v, :].unsqueeze(1).to_broadcast([P, 4, SLOTS * HD // 2]), op=ALU.mult)
+                                        in1=cos_b[:, v, :].unsqueeze(1).unsqueeze(3).to_broadcast([P, 4, P, 2]), op=ALU.mult)
+
+        fused = set()
 
         def copy(engine, out, in_):
             if engine == "V":
@@ -151,14 +151,11 @@ def tile_llamaselfattentionblock_pa_v_kernel(tc, x, g, wq, wk, rstd, grad_0, gra
             copy(engine, dz_tok[u][:].rearrange("p (c i) j -> p c j i", i=4),
                  dz[u][:].rearrange("p j v c -> p j (v c)").rearrange("p j (c i) -> p c j i", i=4))
 
-        def norm(h, c):
-            cols = slice(c * HALF // 2, (c + 1) * HALF // 2)
-            x_cols = slice(h * HALF + cols.start, h * HALF + cols.stop)
+        def norm(h):
             nc.vector.tensor_tensor(
-                out=h_tok[h][:, cols, :].rearrange("p (c i) j -> p c j i", i=4),
-                in0=x_sb[:, :, x_cols].rearrange("p j (c i) -> p c j i", i=4),
-                in1=rg[:, h, :, cols].rearrange("p j (c i) -> p c j i", i=4),
-                op=ALU.mult)
+                out=h_tok[h][:].rearrange("p (c i) j -> p c j i", i=4),
+                in0=x_sb[:, :, h * HALF : (h + 1) * HALF].rearrange("p j (c i) -> p c j i", i=4),
+                in1=rg[:, h], op=ALU.mult)
 
         def quantize(pair, dtype, values):
             nc.vector.quantize_mx(out=pair[0][:].bitcast(dtype), scales=pair[1][:], in_=values)
@@ -172,8 +169,8 @@ def tile_llamaselfattentionblock_pa_v_kernel(tc, x, g, wq, wk, rstd, grad_0, gra
         def qt(u):
             quantize(dz_feat_q[u], E5M2, dz_feat[u][:])
 
-        def qw(u, h):
-            quantize(w_q[u][h], E4M3, w_feat[u, h][:])
+        def qw(a, h):
+            quantize(w_q[a][h], E4M3, w_feat[a, h][:].rearrange("p u c -> p (u c)"))
 
         def stream_bank(shape):
             return psum.tile(shape, F32, name="stream", tag="stream", bufs=4)
@@ -190,18 +187,18 @@ def tile_llamaselfattentionblock_pa_v_kernel(tc, x, g, wq, wk, rstd, grad_0, gra
             copy(engine, rows.rearrange("p (j q v) -> p j q v", j=2, v=2), bank[:].rearrange("p (j v) q -> p j q v", v=2))
 
         def turn_w(u, h, ip, engine="S"):
-            if ip == 0:
-                w_feat[u, h] = rotating("w_feat", [P, 4 * HALF], BF16, 4)
+            if ip == 0 and u % 2 == 0:
+                w_feat[u // 2, h] = rotating("w_feat", [P, 2, 4 * HALF], BF16, 2)
             bank = stream_bank([P, 4, P])
             words = w_sb[u // 2][h][:].rearrange("p i f -> p (i f)").bitcast(F32)
             for i in range(2):
                 first = (2 * ip + i) * (J // 2) + (u % 2) * (UNIT // 2)
                 for s in range(2):
                     nc.tensor.transpose(bank[:, 2 * i + s, :], words[:, first + s : first + UNIT // 2 : 2], identity[:])
-            rows = w_feat[u, h][:].bitcast(F32).rearrange("p (q w) -> p q w", w=8)
+            rows = w_feat[u // 2, h][:, u % 2].bitcast(F32).rearrange("p (q w) -> p q w", w=8)
             copy(engine, rows[:, :, 4 * ip : 4 * ip + 4], bank[:].rearrange("p w q -> p q w"))
 
-        def dw(u, e, engine="S"):
+        def dw(u, e, engine="S", alone=False):
             bank = stream_bank([P, UNIT])
             lhs, lhs_scale = h_q[e // 4]
             rhs, rhs_scale = dz_tok_q[u]
@@ -209,11 +206,17 @@ def tile_llamaselfattentionblock_pa_v_kernel(tc, x, g, wq, wk, rstd, grad_0, gra
             nc.tensor.matmul_mx(out=bank[:], lhsT=lhs[:, cols].bitcast(E4M3), lhsT_scale=lhs_scale[:, cols],
                                 rhs=rhs[:].bitcast(E5M2), rhs_scale=rhs_scale[:], start=True, stop=True)
             if u % 2 == 0:
-                dw_rows[u // 2, e] = rotating("dw_rows", [P, J], F32, 6)
+                dw_rows[u // 2, e] = rotating("dw_rows", [P, J], F32, 8)
             rows = dw_rows[u // 2, e]
-            copy(engine, rows[:, (u % 2) * UNIT : (u % 2 + 1) * UNIT].rearrange("p (m v s) -> p m v s", v=2, s=2),
-                 bank[:].rearrange("p (v m s) -> p m v s", v=2, s=2))
-            if u % 2 == 1:
+            if u in fused:
+                copy(engine, rows[:, (u % 2) * UNIT : (u % 2 + 1) * UNIT], bank[:])
+            else:
+                copy(engine, rows[:, (u % 2) * UNIT : (u % 2 + 1) * UNIT].rearrange("p (m v s) -> p m v s", v=2, s=2),
+                     bank[:].rearrange("p (v m s) -> p m v s", v=2, s=2))
+            if alone:
+                part = slice((u % 2) * UNIT, (u % 2 + 1) * UNIT)
+                nc.sync.dma_start(out=weight_grads[u // 2][e * P : (e + 1) * P, part], in_=rows[:, part])
+            elif u % 2 == 1:
                 nc.sync.dma_start(out=weight_grads[u // 2][e * P : (e + 1) * P, :], in_=rows[:])
 
         def dh(j, h, u):
@@ -221,70 +224,78 @@ def tile_llamaselfattentionblock_pa_v_kernel(tc, x, g, wq, wk, rstd, grad_0, gra
                 dh_bank[j, h] = psum.tile([P, HALF], F32, name="dh", tag="dh", bufs=4)
             cols = slice(j * P, (j + 1) * P)
             lhs, lhs_scale = dz_feat_q[u]
-            rhs, rhs_scale = w_q[u][h]
+            rhs, rhs_scale = w_q[u // 2][h]
+            e_cols = slice((u % 2) * HALF, (u % 2 + 1) * HALF)
             nc.tensor.matmul_mx(out=dh_bank[j, h][:], lhsT=lhs[:, cols].bitcast(E5M2), lhsT_scale=lhs_scale[:, cols],
-                                rhs=rhs[:].bitcast(E4M3), rhs_scale=rhs_scale[:], start=(u == 0), stop=(u == UNITS - 1))
+                                rhs=rhs[:, e_cols].bitcast(E4M3), rhs_scale=rhs_scale[:, e_cols], start=(u == 0), stop=(u == UNITS - 1))
 
         def scale(j, h):
-            nc.vector.tensor_tensor(out=scaled[j][:, h * HALF : (h + 1) * HALF], in0=dh_bank[j, h][:], in1=rg[:, h, j], op=ALU.mult)
+            nc.vector.tensor_tensor(out=scaled[j][:, h * HALF : (h + 1) * HALF].rearrange("p (c i) -> p c i", i=4),
+                                    in0=dh_bank[j, h][:].rearrange("p (c i) -> p c i", i=4), in1=rg[:, h, :, j, :], op=ALU.mult)
 
         def dot(j):
             product = rotating("product", [P, E], F32, 2)
             nc.vector.scalar_tensor_tensor(product[:], x_sb[:, j], neg_r2[:, j : j + 1], scaled[j][:], ALU.mult, ALU.mult,
                                            accum_out=coef[j][:])
 
-        def out(j, pieces=1):
-            result = rotating("result", [P, E], F32, 2)
-            for k in range(pieces):
-                cols = slice(k * E // pieces, (k + 1) * E // pieces)
-                nc.vector.scalar_tensor_tensor(result[:, cols], x_sb[:, j, cols], coef[j][:], scaled[j][:, cols], ALU.mult, ALU.add)
-                nc.sync.dma_start(out=out_rows[:, j, cols], in_=result[:, cols])
+        def out(j, cols=slice(0, E)):
+            nc.vector.scalar_tensor_tensor(scaled[j][:, cols], x_sb[:, j, cols], coef[j][:], scaled[j][:, cols], ALU.mult, ALU.add)
+            nc.sync.dma_start(out=out_rows[:, j, cols], in_=scaled[j][:, cols])
 
-        for h in range(2):
-            for j in range(4): rg_step(h,j)
-        for b in range(2, 4): load_grad(dq_sb[1], 0, b, 4, 8, nc.scalar)
+        table_b()
+        for j in range(4): rg_step(0,j)
+        load_pair(dq_sb[1], 0, 4, 8)
+        load_w(1, 0)
+        for j in range(4): rg_step(1,j)
         rope(0)
         for jp in range(2): turn_dz(0,jp)
-        norm(0,0); interleave(0); norm(0,1); qz(0); qh(0)
+        norm(0); interleave(0); qh(0); qz(0)
         for u in range(2):
             for ip in range(2): turn_w(u,0,ip)
-        for b in range(2, 4): load_grad(dk_sb, 1, b, 0, HEADS, nc.scalar)
+        load_pair(dk_sb, 1, 0, HEADS)
+        load_w(0, 1)
+        load_w(1, 1)
         rope(1)
-        for e in range(4): dw(0,e)
+        for e in range(4): dw(0,e,alone=True)
         for jp in range(2): turn_dz(1,jp)
         qt(0); interleave(1); qw(0,0); qz(1)
         for ip in range(2): turn_w(2,0,ip)
-        for j in range(4): dh(j,0,0)
         for ip in range(2): turn_w(3,0,ip)
-        norm(1,0); norm(1,1); qt(1); qh(1); qw(1,0)
-        for e in range(4): dw(1,e)
+        norm(1); qt(1); qh(1)
+        for e in range(4): dw(1,e,alone=True); dh(e,0,0)
         for ip in range(2): turn_w(0,1,ip)
         rope(2)
-        dw(0,4); dw(1,4)
-        for j in range(4): dh(j,0,1)
+        dw(0,4); dh(0,0,1); dw(1,4); dh(1,0,1)
+        dw(0,5); dh(2,0,1); dw(1,5); dh(3,0,1)
         for jp in range(2): turn_dz(2,jp)
         rope(3)
-        dw(0,5); dw(1,5)
         for ip in range(2): turn_w(1,1,ip)
         dw(0,6); dw(1,6)
+        interleave(2); qw(1,0); qt(2); interleave(3); qz(2)
         for jp in range(2): turn_dz(3,jp)
-        interleave(2); qt(2); qw(2,0); interleave(3); qz(2); qt(3); qz(3); qw(3,0)
-        dw(0,7); dw(1,7)
-        for j in range(4): dh(j,0,2)
+        dw(0,7); dh(0,0,2); dw(1,7); dh(1,0,2)
         for ip in range(2): turn_w(2,1,ip)
-        dw(2,0); dw(3,0)
-        for j in range(4): dh(j,0,3)
+        dh(2,0,2); dh(3,0,2)
+        qt(3); qz(3)
         for ip in range(2): turn_w(3,1,ip)
-        qw(0,1); qw(1,1)
-        for j in range(4): scale(j,0)
-        qw(2,1); qw(3,1)
+        dw(2,0); dh(0,0,3); dh(1,0,3); dw(3,0); dh(2,0,3); dh(3,0,3)
+        qw(0,1); row_factor()
+        for j in range(2): scale(j,0)
+        qw(1,1)
+        for j in range(2,4): scale(j,0)
         dw(2,1); dw(3,1)
-        dw(2,2); dw(3,2)
-        for j in range(4):
-            for u in range(4): dh(j,1,u)
-            dw(2,3+j); dw(3,3+j)
-            scale(j,1)
-            if j>0: out(j-1)
-            dot(j)
+        for u in range(2):
+            for j in range(2): dh(j,1,u)
+        dw(2,2)
+        for j in range(2):
+            for u in range(2,4): dh(j,1,u)
+        dw(3,2)
+        scale(0,1); scale(1,1); dot(0); dot(1)
+        for e in range(3,7):
+            dw(2,e); dh((e+1)//2,1,2*((e+1)%2)); dw(3,e); dh((e+1)//2,1,2*((e+1)%2)+1)
+            if e == 5: out(0)
+        scale(2,1)
         dw(2,7); dw(3,7)
-        out(3,2)
+        out(1); dot(2); scale(3,1)
+        first, second = slice(0, HALF), slice(HALF, E)
+        out(2, first); dot(3); out(2, second); out(3, first); out(3, second)

@@ -55,7 +55,7 @@ def tile_llamaselfattentionblock_pa_v_kernel(tc, x, g, wq, wk, rstd, grad_0, gra
         g_sb = kept("g_sb", [P, E // P], BF16)
         identity = kept("identity", [P, P], F32)
         x_sb = kept("x_sb", [P, SLOTS, E], BF16)
-        rg = kept("rg", [P, 2, HALF // 4, SLOTS, 4], F32)
+        rg = kept("rg", [P, 2, SLOTS, HALF], F32)
         w_sb = [[kept("w%d%d" % (a, h), [P, 4, J], BF16) for h in range(2)] for a in range(2)]
         h_tok = [kept("h_tok%d" % h, [P, HALF, SLOTS], BF16) for h in range(2)]
         h_q = [codes("h_q%d" % h) for h in range(2)]
@@ -79,10 +79,10 @@ def tile_llamaselfattentionblock_pa_v_kernel(tc, x, g, wq, wk, rstd, grad_0, gra
         nc.gpsimd.iota(tokens[:], pattern=[[1, SLOTS]], base=0, channel_multiplier=SLOTS)
         make_identity(nc, identity[:])
         nc.sync.dma_start(out=g_sb[:], in_=g.rearrange("(p c) -> p c", p=P))
-        nc.scalar.dma_start(out=rstd_sb[:], in_=rstd.rearrange("b (q j) -> (b q) j", j=SLOTS))
         for b in range(2):
             load_grad(dq_sb[0], 0, b, 0, 4, nc.sync)
             load_grad(dq_sb[0], 0, b + 2, 0, 4, nc.scalar)
+        nc.sync.dma_start(out=rstd_sb[:], in_=rstd.rearrange("b (q j) -> (b q) j", j=SLOTS))
         nc.sync.dma_start(out=x_sb[:], in_=x_rows)
         load_w(0, 0)
 
@@ -92,7 +92,7 @@ def tile_llamaselfattentionblock_pa_v_kernel(tc, x, g, wq, wk, rstd, grad_0, gra
         turns = kept("turns", [P, SLOTS, HD // 2], F32)
         whole = kept("whole", [P, SLOTS, HD // 2], I32)
         fraction = kept("fraction", [P, SLOTS, HD // 2], F32)
-        cos_b = kept("cos_b", [P, 2, P], F32)
+        cos_b = kept("cos_b", [P, 2, 2 * P], F32)
         nc.vector.memset(fine[:, 0:1], 1.0)
         nc.vector.tensor_single_scalar(positions[:], tokens[:], L - 1, ALU.bitwise_and)
         for k in range(1, 4):
@@ -113,7 +113,10 @@ def tile_llamaselfattentionblock_pa_v_kernel(tc, x, g, wq, wk, rstd, grad_0, gra
                                            whole[:, js].rearrange("p j i -> p (j i)"), ALU.add, ALU.subtract)
 
         def table_b():
-            nc.scalar.activation(out=cos_b[:], in_=fraction[:].rearrange("p j (w v) -> p v (j w)", v=2), func=ACT.Sin, scale=2.0 * math.pi)
+            angles = fraction[:].rearrange("p j (w v) -> p v (j w)", v=2)
+            for v in range(2):
+                nc.scalar.activation(out=cos_b[:, v].rearrange("p (k s) -> p k s", s=2), in_=angles[:, v].unsqueeze(2).to_broadcast([P, P, 2]),
+                                     func=ACT.Sin, scale=2.0 * math.pi)
 
         def row_factor():
             nc.vector.scalar_tensor_tensor(neg_r2[:], rstd_sb[:], -1.0 / E, rstd_sb[:], ALU.mult, ALU.mult)
@@ -129,14 +132,14 @@ def tile_llamaselfattentionblock_pa_v_kernel(tc, x, g, wq, wk, rstd, grad_0, gra
         gain = gain_words[:].rearrange("p q k -> p (q k)").bitcast(BF16)
 
         def rg_step(h, j):
-            nc.scalar.activation(out=rg[:, h, :, j, :], in_=gain[:, h * HALF : (h + 1) * HALF].rearrange("p (c i) -> p c i", i=4), func=ACT.Copy, scale=rstd_sb[:, j : j + 1])
+            nc.scalar.activation(out=rg[:, h, j], in_=gain[:, h * HALF : (h + 1) * HALF], func=ACT.Copy, scale=rstd_sb[:, j : j + 1])
 
         def rope(u):
             dz[u] = rotating("dz", [P, SLOTS, 2, UNIT // 2], BF16, 2)
             pairs = grad_sb[u].rearrange("p n j (w v s) -> p (n j w) v s", v=2, s=2)
             for v in range(2):
                 nc.vector.tensor_tensor(out=dz[u][:, :, v, :].rearrange("p j (n c) -> p n j c", n=4), in0=pairs[:, :, v, :],
-                                        in1=cos_b[:, v, :].unsqueeze(1).unsqueeze(3).to_broadcast([P, 4, P, 2]), op=ALU.mult)
+                                        in1=cos_b[:, v, :].unsqueeze(1).to_broadcast([P, 4, 2 * P]), op=ALU.mult)
 
         fused = set()
 
@@ -148,14 +151,14 @@ def tile_llamaselfattentionblock_pa_v_kernel(tc, x, g, wq, wk, rstd, grad_0, gra
 
         def interleave(u, engine="V"):
             dz_tok[u] = rotating("dz_tok", [P, UNIT, SLOTS], BF16, 2)
-            copy(engine, dz_tok[u][:].rearrange("p (c i) j -> p c j i", i=4),
-                 dz[u][:].rearrange("p j v c -> p j (v c)").rearrange("p j (c i) -> p c j i", i=4))
+            copy(engine, dz_tok[u][:].rearrange("p (c i) j -> p c j i", i=2),
+                 dz[u][:].rearrange("p j v c -> p j (v c)").rearrange("p j (c i) -> p c j i", i=2))
 
         def norm(h):
             nc.vector.tensor_tensor(
-                out=h_tok[h][:].rearrange("p (c i) j -> p c j i", i=4),
-                in0=x_sb[:, :, h * HALF : (h + 1) * HALF].rearrange("p j (c i) -> p c j i", i=4),
-                in1=rg[:, h], op=ALU.mult)
+                out=h_tok[h][:].rearrange("p (c i) j -> p c j i", i=2),
+                in0=x_sb[:, :, h * HALF : (h + 1) * HALF].rearrange("p j (c i) -> p c j i", i=2),
+                in1=rg[:, h].rearrange("p j (c i) -> p c j i", i=2), op=ALU.mult)
 
         def quantize(pair, dtype, values):
             nc.vector.quantize_mx(out=pair[0][:].bitcast(dtype), scales=pair[1][:], in_=values)
@@ -230,8 +233,7 @@ def tile_llamaselfattentionblock_pa_v_kernel(tc, x, g, wq, wk, rstd, grad_0, gra
                                 rhs=rhs[:, e_cols].bitcast(E4M3), rhs_scale=rhs_scale[:, e_cols], start=(u == 0), stop=(u == UNITS - 1))
 
         def scale(j, h):
-            nc.vector.tensor_tensor(out=scaled[j][:, h * HALF : (h + 1) * HALF].rearrange("p (c i) -> p c i", i=4),
-                                    in0=dh_bank[j, h][:].rearrange("p (c i) -> p c i", i=4), in1=rg[:, h, :, j, :], op=ALU.mult)
+            nc.vector.tensor_tensor(out=scaled[j][:, h * HALF : (h + 1) * HALF], in0=dh_bank[j, h][:], in1=rg[:, h, j], op=ALU.mult)
 
         def dot(j):
             product = rotating("product", [P, E], F32, 2)

@@ -79,9 +79,10 @@ def tile_llamaselfattentionblock_pa_v_kernel(tc, x, g, wq, wk, rstd, grad_0, gra
         nc.gpsimd.iota(tokens[:], pattern=[[1, SLOTS]], base=0, channel_multiplier=SLOTS)
         make_identity(nc, identity[:])
         nc.sync.dma_start(out=g_sb[:], in_=g.rearrange("(p c) -> p c", p=P))
-        for b in range(2):
-            load_grad(dq_sb[0], 0, b, 0, 4, nc.sync)
-            load_grad(dq_sb[0], 0, b + 2, 0, 4, nc.scalar)
+        for u in range(2):
+            for b in range(2):
+                load_grad(dq_sb[u], 0, b, 4 * u, 4 * u + 4, nc.sync)
+                load_grad(dq_sb[u], 0, b + 2, 4 * u, 4 * u + 4, nc.scalar)
         nc.sync.dma_start(out=rstd_sb[:], in_=rstd.rearrange("b (q j) -> (b q) j", j=SLOTS))
         nc.sync.dma_start(out=x_sb[:], in_=x_rows)
         load_w(0, 0)
@@ -134,10 +135,11 @@ def tile_llamaselfattentionblock_pa_v_kernel(tc, x, g, wq, wk, rstd, grad_0, gra
         def rg_step(h, j):
             nc.scalar.activation(out=rg[:, h, j], in_=gain[:, h * HALF : (h + 1) * HALF], func=ACT.Copy, scale=rstd_sb[:, j : j + 1])
 
-        def rope(u):
-            dz[u] = rotating("dz", [P, SLOTS, 2, UNIT // 2], BF16, 2)
+        def rope(u, halves=(0, 1)):
+            if 0 in halves:
+                dz[u] = rotating("dz", [P, SLOTS, 2, UNIT // 2], BF16, 2)
             pairs = grad_sb[u].rearrange("p n j (w v s) -> p (n j w) v s", v=2, s=2)
-            for v in range(2):
+            for v in halves:
                 nc.vector.tensor_tensor(out=dz[u][:, :, v, :].rearrange("p j (n c) -> p n j c", n=4), in0=pairs[:, :, v, :],
                                         in1=cos_b[:, v, :].unsqueeze(1).to_broadcast([P, 4, 2 * P]), op=ALU.mult)
 
@@ -245,26 +247,24 @@ def tile_llamaselfattentionblock_pa_v_kernel(tc, x, g, wq, wk, rstd, grad_0, gra
             nc.sync.dma_start(out=out_rows[:, j, cols], in_=scaled[j][:, cols])
 
         table_b()
-        for j in range(4): rg_step(0,j)
-        load_pair(dq_sb[1], 0, 4, 8)
-        load_w(1, 0)
-        for j in range(4): rg_step(1,j)
-        rope(0)
+        for h in range(2):
+            for j in range(4): rg_step(h,j)
+        rope(0); rope(1,(0,)); interleave(0); rope(1,(1,))
         for jp in range(2): turn_dz(0,jp)
-        norm(0); interleave(0); qh(0); qz(0)
-        for u in range(2):
-            for ip in range(2): turn_w(u,0,ip)
         load_pair(dk_sb, 1, 0, HEADS)
+        load_w(1, 0)
         load_w(0, 1)
         load_w(1, 1)
-        rope(1)
-        for e in range(4): dw(0,e,alone=True)
         for jp in range(2): turn_dz(1,jp)
-        qt(0); interleave(1); qw(0,0); qz(1)
-        for ip in range(2): turn_w(2,0,ip)
-        for ip in range(2): turn_w(3,0,ip)
+        norm(0); qt(0); qh(0); qz(0)
+        for u in range(2):
+            for ip in range(2): turn_w(u,0,ip)
+        for e in range(4): dw(0,e)
+        interleave(1); qw(0,0); qz(1)
+        for u in range(2,4):
+            for ip in range(2): turn_w(u,0,ip)
         norm(1); qt(1); qh(1)
-        for e in range(4): dw(1,e,alone=True); dh(e,0,0)
+        for e in range(4): dh(e,0,0); dw(1,e)
         for ip in range(2): turn_w(0,1,ip)
         rope(2)
         dw(0,4); dh(0,0,1); dw(1,4); dh(1,0,1)
@@ -299,5 +299,4 @@ def tile_llamaselfattentionblock_pa_v_kernel(tc, x, g, wq, wk, rstd, grad_0, gra
         scale(2,1)
         dw(2,7); dw(3,7)
         out(1); dot(2); scale(3,1)
-        first, second = slice(0, HALF), slice(HALF, E)
-        out(2, first); dot(3); out(2, second); out(3, first); out(3, second)
+        out(2); dot(3); out(3, slice(0, HALF)); out(3, slice(HALF, E))

@@ -47,16 +47,16 @@ def tile_llamaselfattentionblock_pa_v_kernel(tc, x, g, wq, wk, rstd, grad_0, gra
         def codes(name, width=512):
             return kept(name + "_codes", [P, width], U32), kept(name + "_scales", [P, width], U8)
 
-        dq_sb = [kept("dq%d" % u, [P, 4, SLOTS, HD], BF16) for u in range(2)]
-        dk_sb = kept("dk", [P, HEADS, SLOTS, HD], BF16)
+        dq_sb = [rotating("dq%d" % u, [P, 4, SLOTS, HD], BF16, 1) for u in range(2)]
+        dk_sb = rotating("dk", [P, HEADS, SLOTS, HD], BF16, 1)
         grad_sb = [dq_sb[0][:], dq_sb[1][:], dk_sb[:, 0:4], dk_sb[:, 4:8]]
-        scaled = [kept("scaled%d" % j, [P, E], F32) for j in range(SLOTS)]
+        scaled = {}
         rstd_sb = kept("rstd_sb", [P, SLOTS], F32)
         g_sb = kept("g_sb", [P, E // P], BF16)
         identity = kept("identity", [P, P], F32)
         x_sb = kept("x_sb", [P, SLOTS, E], BF16)
         rg = kept("rg", [P, 2, SLOTS, HALF], F32)
-        w_sb = [[kept("w%d%d" % (a, h), [P, 4, J], BF16) for h in range(2)] for a in range(2)]
+        w_sb = [[rotating("w%d%d" % (a, h), [P, 4, J], BF16, 1) for h in range(2)] for a in range(2)]
         h_tok = [kept("h_tok%d" % h, [P, HALF, SLOTS], BF16) for h in range(2)]
         h_q = [codes("h_q%d" % h) for h in range(2)]
         dz_tok_q = [codes("dz_tok_q%d" % u) for u in range(UNITS)]
@@ -73,19 +73,20 @@ def tile_llamaselfattentionblock_pa_v_kernel(tc, x, g, wq, wk, rstd, grad_0, gra
                             in_=grads[a][b, n0:n1].rearrange("n (q j) d -> q n (j d)", j=SLOTS))
 
         def load_w(a, h):
-            nc.sync.dma_start(out=w_sb[a][h][:], in_=weights[a][h * HALF : (h + 1) * HALF, :].rearrange("(q i) f -> q i f", i=4))
+            nc.sync.dma_start(out=w_sb[a][h][:], in_=weights[a][h * HALF : (h + 1) * HALF, :].rearrange("(i q) f -> q i f", i=4))
 
         tokens = kept("tokens", [P, SLOTS], I32)
         nc.gpsimd.iota(tokens[:], pattern=[[1, SLOTS]], base=0, channel_multiplier=SLOTS)
+        nc.gpsimd.dma_start(out=rstd_sb[:], in_=rstd.rearrange("b (q j) -> (b q) j", j=SLOTS))
         make_identity(nc, identity[:])
         nc.sync.dma_start(out=g_sb[:], in_=g.rearrange("(p c) -> p c", p=P))
         for u in range(2):
             for b in range(2):
                 load_grad(dq_sb[u], 0, b, 4 * u, 4 * u + 4, nc.sync)
                 load_grad(dq_sb[u], 0, b + 2, 4 * u, 4 * u + 4, nc.scalar)
-        nc.sync.dma_start(out=rstd_sb[:], in_=rstd.rearrange("b (q j) -> (b q) j", j=SLOTS))
-        nc.sync.dma_start(out=x_sb[:], in_=x_rows)
         load_w(0, 0)
+        nc.sync.dma_start(out=x_sb[:], in_=x_rows)
+        load_w(1, 0)
 
         positions = kept("positions", [P, SLOTS], I32)
         coarse = kept("coarse", [P, SLOTS, 4], F32)
@@ -132,8 +133,8 @@ def tile_llamaselfattentionblock_pa_v_kernel(tc, x, g, wq, wk, rstd, grad_0, gra
             nc.tensor.transpose(gain_words[:, :, k], g_sb[:].bitcast(F32)[:, k : k + 1].to_broadcast([P, P]), identity[:])
         gain = gain_words[:].rearrange("p q k -> p (q k)").bitcast(BF16)
 
-        def rg_step(h, j):
-            nc.scalar.activation(out=rg[:, h, j], in_=gain[:, h * HALF : (h + 1) * HALF], func=ACT.Copy, scale=rstd_sb[:, j : j + 1])
+        def rg2(j):
+            nc.scalar.activation(out=rg[:, :, j], in_=gain.rearrange("p (h c) -> p h c", h=2), func=ACT.Copy, scale=rstd_sb[:, j : j + 1])
 
         def rope(u, halves=(0, 1)):
             if 0 in halves:
@@ -143,8 +144,6 @@ def tile_llamaselfattentionblock_pa_v_kernel(tc, x, g, wq, wk, rstd, grad_0, gra
                 nc.vector.tensor_tensor(out=dz[u][:, :, v, :].rearrange("p j (n c) -> p n j c", n=4), in0=pairs[:, :, v, :],
                                         in1=cos_b[:, v, :].unsqueeze(1).to_broadcast([P, 4, 2 * P]), op=ALU.mult)
 
-        fused = set()
-
         def copy(engine, out, in_):
             if engine == "V":
                 nc.vector.tensor_copy(out=out, in_=in_)
@@ -153,8 +152,7 @@ def tile_llamaselfattentionblock_pa_v_kernel(tc, x, g, wq, wk, rstd, grad_0, gra
 
         def interleave(u, engine="V"):
             dz_tok[u] = rotating("dz_tok", [P, UNIT, SLOTS], BF16, 2)
-            copy(engine, dz_tok[u][:].rearrange("p (c i) j -> p c j i", i=2),
-                 dz[u][:].rearrange("p j v c -> p j (v c)").rearrange("p j (c i) -> p c j i", i=2))
+            copy(engine, dz_tok[u][:].rearrange("p (m v s) j -> p v m j s", v=2, s=2), dz[u][:].rearrange("p j v (m s) -> p v m j s", s=2))
 
         def norm(h):
             nc.vector.tensor_tensor(
@@ -182,7 +180,7 @@ def tile_llamaselfattentionblock_pa_v_kernel(tc, x, g, wq, wk, rstd, grad_0, gra
 
         def turn_dz(u, jp, engine="S"):
             if jp == 0:
-                dz_feat[u] = rotating("dz_feat", [P, 4 * T], BF16, 2)
+                dz_feat[u] = rotating("dz_feat", [P, 4 * T], BF16, 4)
             bank = stream_bank([P, 4, P])
             words = dz[u][:].rearrange("p j v c -> p (j v c)").bitcast(F32)
             for k in range(4):
@@ -193,15 +191,15 @@ def tile_llamaselfattentionblock_pa_v_kernel(tc, x, g, wq, wk, rstd, grad_0, gra
 
         def turn_w(u, h, ip, engine="S"):
             if ip == 0 and u % 2 == 0:
-                w_feat[u // 2, h] = rotating("w_feat", [P, 2, 4 * HALF], BF16, 2)
+                w_feat[u // 2, h] = rotating("w_feat", [P, 2, 4 * HALF], BF16, 4)
             bank = stream_bank([P, 4, P])
             words = w_sb[u // 2][h][:].rearrange("p i f -> p (i f)").bitcast(F32)
             for i in range(2):
                 first = (2 * ip + i) * (J // 2) + (u % 2) * (UNIT // 2)
                 for s in range(2):
                     nc.tensor.transpose(bank[:, 2 * i + s, :], words[:, first + s : first + UNIT // 2 : 2], identity[:])
-            rows = w_feat[u // 2, h][:, u % 2].bitcast(F32).rearrange("p (q w) -> p q w", w=8)
-            copy(engine, rows[:, :, 4 * ip : 4 * ip + 4], bank[:].rearrange("p w q -> p q w"))
+            rows = w_feat[u // 2, h][:, u % 2].bitcast(F32)[:, ip * 4 * P : (ip + 1) * 4 * P]
+            copy(engine, rows.rearrange("p (i q s) -> p i q s", i=2, s=2), bank[:].rearrange("p (i s) q -> p i q s", s=2))
 
         def dw(u, e, engine="S", alone=False):
             bank = stream_bank([P, UNIT])
@@ -210,19 +208,18 @@ def tile_llamaselfattentionblock_pa_v_kernel(tc, x, g, wq, wk, rstd, grad_0, gra
             cols = slice((e % 4) * P, (e % 4 + 1) * P)
             nc.tensor.matmul_mx(out=bank[:], lhsT=lhs[:, cols].bitcast(E4M3), lhsT_scale=lhs_scale[:, cols],
                                 rhs=rhs[:].bitcast(E5M2), rhs_scale=rhs_scale[:], start=True, stop=True)
-            if u % 2 == 0:
-                dw_rows[u // 2, e] = rotating("dw_rows", [P, J], F32, 8)
+            if u == 0:
+                dw_rows[0, e] = rotating("dw_rows", [P, J], F32, 8)[:]
+            if u == 2 and e % 2 == 0:
+                two = rotating("w%d%d" % (e // 2 % 2, e // 4), [P, 2, J], F32, 1)
+                dw_rows[1, e], dw_rows[1, e + 1] = two[:, 0], two[:, 1]
             rows = dw_rows[u // 2, e]
-            if u in fused:
-                copy(engine, rows[:, (u % 2) * UNIT : (u % 2 + 1) * UNIT], bank[:])
-            else:
-                copy(engine, rows[:, (u % 2) * UNIT : (u % 2 + 1) * UNIT].rearrange("p (m v s) -> p m v s", v=2, s=2),
-                     bank[:].rearrange("p (v m s) -> p m v s", v=2, s=2))
+            copy(engine, rows[:, (u % 2) * UNIT : (u % 2 + 1) * UNIT], bank[:])
             if alone:
                 part = slice((u % 2) * UNIT, (u % 2 + 1) * UNIT)
                 nc.sync.dma_start(out=weight_grads[u // 2][e * P : (e + 1) * P, part], in_=rows[:, part])
             elif u % 2 == 1:
-                nc.sync.dma_start(out=weight_grads[u // 2][e * P : (e + 1) * P, :], in_=rows[:])
+                nc.sync.dma_start(out=weight_grads[u // 2][e * P : (e + 1) * P, :], in_=rows)
 
         def dh(j, h, u):
             if u == 0:
@@ -235,39 +232,46 @@ def tile_llamaselfattentionblock_pa_v_kernel(tc, x, g, wq, wk, rstd, grad_0, gra
                                 rhs=rhs[:, e_cols].bitcast(E4M3), rhs_scale=rhs_scale[:, e_cols], start=(u == 0), stop=(u == UNITS - 1))
 
         def scale(j, h):
+            if h == 0 and j < 2:
+                scaled[j] = rotating("dq%d" % j, [P, E], F32, 1)[:]
+            if h == 0 and j == 2:
+                two = rotating("dk", [P, 2, E], F32, 1)
+                scaled[2], scaled[3] = two[:, 0], two[:, 1]
             nc.vector.tensor_tensor(out=scaled[j][:, h * HALF : (h + 1) * HALF], in0=dh_bank[j, h][:], in1=rg[:, h, j], op=ALU.mult)
 
         def dot(j):
-            product = rotating("product", [P, E], F32, 2)
-            nc.vector.scalar_tensor_tensor(product[:], x_sb[:, j], neg_r2[:, j : j + 1], scaled[j][:], ALU.mult, ALU.mult,
+            product = rotating("dz", [P, E], F32, 2)
+            nc.vector.scalar_tensor_tensor(product[:], x_sb[:, j], neg_r2[:, j : j + 1], scaled[j], ALU.mult, ALU.mult,
                                            accum_out=coef[j][:])
 
-        def out(j, cols=slice(0, E)):
+        def out(j, cols=slice(0, E), later=False):
             nc.vector.scalar_tensor_tensor(scaled[j][:, cols], x_sb[:, j, cols], coef[j][:], scaled[j][:, cols], ALU.mult, ALU.add)
+            if not later:
+                store_dx(j, cols)
+
+        def store_dx(j, cols=slice(0, E)):
             nc.sync.dma_start(out=out_rows[:, j, cols], in_=scaled[j][:, cols])
 
         table_b()
-        for h in range(2):
-            for j in range(4): rg_step(h,j)
+        for j in range(4): rg2(j)
         rope(0); rope(1,(0,)); interleave(0); rope(1,(1,))
         for jp in range(2): turn_dz(0,jp)
+        for u in range(2):
+            for ip in range(2): turn_w(u,0,ip)
         load_pair(dk_sb, 1, 0, HEADS)
-        load_w(1, 0)
         load_w(0, 1)
         load_w(1, 1)
         for jp in range(2): turn_dz(1,jp)
         norm(0); qt(0); qh(0); qz(0)
-        for u in range(2):
-            for ip in range(2): turn_w(u,0,ip)
+        for ip in range(2): turn_w(2,0,ip)
         for e in range(4): dw(0,e)
         interleave(1); qw(0,0); qz(1)
-        for u in range(2,4):
-            for ip in range(2): turn_w(u,0,ip)
+        for ip in range(2): turn_w(3,0,ip)
         norm(1); qt(1); qh(1)
         for e in range(4): dh(e,0,0); dw(1,e)
-        for ip in range(2): turn_w(0,1,ip)
         rope(2)
-        dw(0,4); dh(0,0,1); dw(1,4); dh(1,0,1)
+        dw(0,4,"V"); dh(0,0,1); dw(1,4,"V"); dh(1,0,1)
+        for ip in range(2): turn_w(0,1,ip)
         dw(0,5); dh(2,0,1); dw(1,5); dh(3,0,1)
         for jp in range(2): turn_dz(2,jp)
         rope(3)
@@ -295,8 +299,8 @@ def tile_llamaselfattentionblock_pa_v_kernel(tc, x, g, wq, wk, rstd, grad_0, gra
         scale(0,1); scale(1,1); dot(0); dot(1)
         for e in range(3,7):
             dw(2,e); dh((e+1)//2,1,2*((e+1)%2)); dw(3,e); dh((e+1)//2,1,2*((e+1)%2)+1)
-            if e == 5: out(0)
-        scale(2,1)
+            if e == 4: out(0)
+        scale(2,1); out(1)
         dw(2,7); dw(3,7)
-        out(1); dot(2); scale(3,1)
+        dot(2); scale(3,1)
         out(2); dot(3); out(3, slice(0, HALF)); out(3, slice(HALF, E))

@@ -22,6 +22,10 @@ SLOTS = 4
 UNIT = 512
 HALF = 512
 UNITS = 2 * J // UNIT
+UNIT_HEADS = UNIT // HD
+ROW_TILES = E // P
+DH_BANKS = 4
+STREAM_BANKS = 4
 FLOPS = 2 * 2 * T * E * 2 * J
 
 
@@ -44,13 +48,12 @@ def tile_llamaselfattentionblock_pa_v_kernel(tc, x, g, wq, wk, rstd, grad_0, gra
         def rotating(tag, shape, dtype, bufs):
             return reused.tile(shape, dtype, name=tag, tag=tag, bufs=bufs, align_bytes=64)
 
-        def codes(name, width=512):
+        def codes(name, width):
             return kept(name + "_codes", [P, width], U32), kept(name + "_scales", [P, width], U8)
 
-        dq_sb = [rotating("dq%d" % u, [P, 4, SLOTS, HD], BF16, 1) for u in range(2)]
+        dq_sb = [rotating("dq%d" % u, [P, UNIT_HEADS, SLOTS, HD], BF16, 1) for u in range(2)]
         dk_sb = rotating("dk", [P, HEADS, SLOTS, HD], BF16, 1)
-        grad_sb = [dq_sb[0][:], dq_sb[1][:], dk_sb[:, 0:4], dk_sb[:, 4:8]]
-        scaled = {}
+        grad_sb = [dq_sb[0][:], dq_sb[1][:], dk_sb[:, 0:UNIT_HEADS], dk_sb[:, UNIT_HEADS:HEADS]]
         rstd_sb = kept("rstd_sb", [P, SLOTS], F32)
         g_sb = kept("g_sb", [P, E // P], BF16)
         identity = kept("identity", [P, P], F32)
@@ -58,19 +61,21 @@ def tile_llamaselfattentionblock_pa_v_kernel(tc, x, g, wq, wk, rstd, grad_0, gra
         rg = kept("rg", [P, 2, SLOTS, HALF], F32)
         w_sb = [[rotating("w%d%d" % (a, h), [P, 4, J], BF16, 1) for h in range(2)] for a in range(2)]
         h_tok = [kept("h_tok%d" % h, [P, HALF, SLOTS], BF16) for h in range(2)]
-        h_q = [codes("h_q%d" % h) for h in range(2)]
-        dz_tok_q = [codes("dz_tok_q%d" % u) for u in range(UNITS)]
-        dz_feat_q = [codes("dz_feat_q%d" % u) for u in range(UNITS)]
+        h_q = [codes("h_q%d" % h, HALF) for h in range(2)]
+        dz_tok_q = [codes("dz_tok_q%d" % u, UNIT) for u in range(UNITS)]
+        dz_feat_q = [codes("dz_feat_q%d" % u, T) for u in range(UNITS)]
         w_q = [[codes("w_q%d%d" % (a, h), 2 * HALF) for h in range(2)] for a in range(2)]
         neg_r2 = kept("neg_r2", [P, SLOTS], F32)
         coef = [kept("coef%d" % j, [P, 1], F32) for j in range(SLOTS)]
-        dz, dz_tok, dz_feat, w_feat, dh_bank, dw_rows = {}, {}, {}, {}, {}, {}
+        dz, dz_tok, dz_feat, w_feat, dh_bank, dw_rows, scaled = {}, {}, {}, {}, {}, {}, {}
 
         ctx.enter_context(tc.manual_schedule())
 
-        def load_grad(dst, a, b, n0, n1, queue):
-            queue.dma_start(out=dst[32 * b : 32 * b + 32].rearrange("q n j d -> q n (j d)"),
-                            in_=grads[a][b, n0:n1].rearrange("n (q j) d -> q n (j d)", j=SLOTS))
+        def load_grad(dst, a, first_head, heads):
+            for b in range(2):
+                for batch, queue in ((b, nc.sync), (b + 2, nc.scalar)):
+                    queue.dma_start(out=dst[32 * batch : 32 * batch + 32].rearrange("q n j d -> q n (j d)"),
+                                    in_=grads[a][batch, first_head : first_head + heads].rearrange("n (q j) d -> q n (j d)", j=SLOTS))
 
         def load_w(a, h):
             nc.sync.dma_start(out=w_sb[a][h][:], in_=weights[a][h * HALF : (h + 1) * HALF, :].rearrange("(i q) f -> q i f", i=4))
@@ -81,9 +86,7 @@ def tile_llamaselfattentionblock_pa_v_kernel(tc, x, g, wq, wk, rstd, grad_0, gra
         make_identity(nc, identity[:])
         nc.sync.dma_start(out=g_sb[:], in_=g.rearrange("(p c) -> p c", p=P))
         for u in range(2):
-            for b in range(2):
-                load_grad(dq_sb[u], 0, b, 4 * u, 4 * u + 4, nc.sync)
-                load_grad(dq_sb[u], 0, b + 2, 4 * u, 4 * u + 4, nc.scalar)
+            load_grad(dq_sb[u], 0, u * UNIT_HEADS, UNIT_HEADS)
         load_w(0, 0)
         nc.sync.dma_start(out=x_sb[:], in_=x_rows)
         load_w(1, 0)
@@ -94,7 +97,7 @@ def tile_llamaselfattentionblock_pa_v_kernel(tc, x, g, wq, wk, rstd, grad_0, gra
         turns = kept("turns", [P, SLOTS, HD // 2], F32)
         whole = kept("whole", [P, SLOTS, HD // 2], I32)
         fraction = kept("fraction", [P, SLOTS, HD // 2], F32)
-        cos_b = kept("cos_b", [P, 2, 2 * P], F32)
+        cosines = kept("cosines", [P, 2, SLOTS * HD // 2], F32)
         nc.vector.memset(fine[:, 0:1], 1.0)
         nc.vector.tensor_single_scalar(positions[:], tokens[:], L - 1, ALU.bitwise_and)
         for k in range(1, 4):
@@ -103,140 +106,67 @@ def tile_llamaselfattentionblock_pa_v_kernel(tc, x, g, wq, wk, rstd, grad_0, gra
             nc.vector.tensor_single_scalar(coarse[:, :, k], positions[:], 10000.0 ** (-k / 4.0) * 0.5 / math.pi, ALU.mult)
         for k in range(1, 4):
             nc.vector.tensor_single_scalar(fine[:, 4 * k : 4 * k + 4], fine[:, 0:4], 10000.0 ** (-k / 16.0), ALU.mult)
-        halves = [slice(0, 2), slice(2, 4)]
-        for js in halves:
+        slot_pairs = [slice(0, 2), slice(2, 4)]
+        for js in slot_pairs:
             nc.vector.tensor_tensor(turns[:, js].rearrange("p j (a b) -> p (j a) b", b=16),
                                     coarse[:, js].rearrange("p j a -> p (j a)").unsqueeze(2).to_broadcast([P, 8, 16]),
                                     fine[:].unsqueeze(1).to_broadcast([P, 8, 16]), ALU.mult)
-        for js in halves:
+        for js in slot_pairs:
             nc.vector.tensor_single_scalar(whole[:, js], turns[:, js], 0.25, ALU.add)
-        for js in halves:
+        for js in slot_pairs:
             nc.vector.scalar_tensor_tensor(fraction[:, js].rearrange("p j i -> p (j i)"), turns[:, js].rearrange("p j i -> p (j i)"), 0.25,
                                            whole[:, js].rearrange("p j i -> p (j i)"), ALU.add, ALU.subtract)
 
-        def table_b():
-            angles = fraction[:].rearrange("p j (w v) -> p v (j w)", v=2)
-            for v in range(2):
-                nc.scalar.activation(out=cos_b[:, v].rearrange("p (k s) -> p k s", s=2), in_=angles[:, v].unsqueeze(2).to_broadcast([P, P, 2]),
-                                     func=ACT.Sin, scale=2.0 * math.pi)
-
-        def row_factor():
-            nc.vector.scalar_tensor_tensor(neg_r2[:], rstd_sb[:], -1.0 / E, rstd_sb[:], ALU.mult, ALU.mult)
-
-        def load_pair(dst, a, n0, n1):
-            for b in range(2):
-                load_grad(dst, a, b, n0, n1, nc.sync)
-                load_grad(dst, a, b + 2, n0, n1, nc.scalar)
-
-        gain_words = psum.tile([P, P, 4], F32, name="gain", tag="dh", bufs=4)
+        gain_words = psum.tile([P, P, 4], F32, name="gain", tag="dh", bufs=DH_BANKS)
         for k in range(4):
             nc.tensor.transpose(gain_words[:, :, k], g_sb[:].bitcast(F32)[:, k : k + 1].to_broadcast([P, P]), identity[:])
         gain = gain_words[:].rearrange("p q k -> p (q k)").bitcast(BF16)
 
-        def rg2(j):
+        angles = fraction[:].rearrange("p j (w v) -> p v (j w)", v=2)
+        for v in range(2):
+            nc.scalar.activation(out=cosines[:, v].rearrange("p (k s) -> p k s", s=2), in_=angles[:, v].unsqueeze(2).to_broadcast([P, P, 2]),
+                                 func=ACT.Sin, scale=2.0 * math.pi)
+        for j in range(SLOTS):
             nc.scalar.activation(out=rg[:, :, j], in_=gain.rearrange("p (h c) -> p h c", h=2), func=ACT.Copy, scale=rstd_sb[:, j : j + 1])
 
-        def rope(u, halves=(0, 1)):
-            if 0 in halves:
+        def rope(u, v):
+            if v == 0:
                 dz[u] = rotating("dz", [P, SLOTS, 2, UNIT // 2], BF16, 2)
             pairs = grad_sb[u].rearrange("p n j (w v s) -> p (n j w) v s", v=2, s=2)
-            for v in halves:
-                nc.vector.tensor_tensor(out=dz[u][:, :, v, :].rearrange("p j (n c) -> p n j c", n=4), in0=pairs[:, :, v, :],
-                                        in1=cos_b[:, v, :].unsqueeze(1).to_broadcast([P, 4, 2 * P]), op=ALU.mult)
+            nc.vector.tensor_tensor(out=dz[u][:, :, v, :].rearrange("p j (n c) -> p n j c", n=UNIT_HEADS), in0=pairs[:, :, v, :],
+                                    in1=cosines[:, v, :].unsqueeze(1).to_broadcast([P, UNIT_HEADS, 2 * P]), op=ALU.mult)
 
-        def copy(engine, out, in_):
-            if engine == "V":
-                nc.vector.tensor_copy(out=out, in_=in_)
-            else:
-                nc.scalar.copy(out=out, in_=in_)
-
-        def interleave(u, engine="V"):
+        def interleave(u):
             dz_tok[u] = rotating("dz_tok", [P, UNIT, SLOTS], BF16, 2)
-            copy(engine, dz_tok[u][:].rearrange("p (m v s) j -> p v m j s", v=2, s=2), dz[u][:].rearrange("p j v (m s) -> p v m j s", s=2))
+            nc.vector.tensor_copy(out=dz_tok[u][:].rearrange("p (m v s) j -> p v m j s", v=2, s=2),
+                                  in_=dz[u][:].rearrange("p j v (m s) -> p v m j s", s=2))
 
         def norm(h):
-            nc.vector.tensor_tensor(
-                out=h_tok[h][:].rearrange("p (c i) j -> p c j i", i=2),
-                in0=x_sb[:, :, h * HALF : (h + 1) * HALF].rearrange("p j (c i) -> p c j i", i=2),
-                in1=rg[:, h].rearrange("p j (c i) -> p c j i", i=2), op=ALU.mult)
+            nc.vector.tensor_tensor(out=h_tok[h][:].rearrange("p (c i) j -> p c j i", i=2),
+                                    in0=x_sb[:, :, h * HALF : (h + 1) * HALF].rearrange("p j (c i) -> p c j i", i=2),
+                                    in1=rg[:, h].rearrange("p j (c i) -> p c j i", i=2), op=ALU.mult)
 
         def quantize(pair, dtype, values):
             nc.vector.quantize_mx(out=pair[0][:].bitcast(dtype), scales=pair[1][:], in_=values)
 
-        def qz(u):
+        def quantize_dz_tok(u):
             quantize(dz_tok_q[u], E5M2, dz_tok[u][:].rearrange("p c j -> p (c j)"))
 
-        def qh(h):
+        def quantize_h(h):
             quantize(h_q[h], E4M3, h_tok[h][:].rearrange("p c j -> p (c j)"))
 
-        def qt(u):
+        def quantize_dz_feat(u):
             quantize(dz_feat_q[u], E5M2, dz_feat[u][:])
 
-        def qw(a, h):
+        def quantize_w(a, h):
             quantize(w_q[a][h], E4M3, w_feat[a, h][:].rearrange("p u c -> p (u c)"))
-
-        def stream_bank(shape):
-            return psum.tile(shape, F32, name="stream", tag="stream", bufs=4)
-
-        def turn_dz(u, jp, engine="S"):
-            if jp == 0:
-                dz_feat[u] = rotating("dz_feat", [P, 4 * T], BF16, 4)
-            bank = stream_bank([P, 4, P])
-            words = dz[u][:].rearrange("p j v c -> p (j v c)").bitcast(F32)
-            for k in range(4):
-                first = (4 * jp + k) * P
-                nc.tensor.transpose(bank[:, k, :], words[:, first : first + P], identity[:])
-            rows = dz_feat[u][:].bitcast(F32)[:, jp * 4 * P : (jp + 1) * 4 * P]
-            copy(engine, rows.rearrange("p (j q v) -> p j q v", j=2, v=2), bank[:].rearrange("p (j v) q -> p j q v", v=2))
-
-        def turn_w(u, h, ip, engine="S"):
-            if ip == 0 and u % 2 == 0:
-                w_feat[u // 2, h] = rotating("w_feat", [P, 2, 4 * HALF], BF16, 4)
-            bank = stream_bank([P, 4, P])
-            words = w_sb[u // 2][h][:].rearrange("p i f -> p (i f)").bitcast(F32)
-            for i in range(2):
-                first = (2 * ip + i) * (J // 2) + (u % 2) * (UNIT // 2)
-                for s in range(2):
-                    nc.tensor.transpose(bank[:, 2 * i + s, :], words[:, first + s : first + UNIT // 2 : 2], identity[:])
-            rows = w_feat[u // 2, h][:, u % 2].bitcast(F32)[:, ip * 4 * P : (ip + 1) * 4 * P]
-            copy(engine, rows.rearrange("p (i q s) -> p i q s", i=2, s=2), bank[:].rearrange("p (i s) q -> p i q s", s=2))
-
-        def dw(u, e, engine="S", alone=False):
-            bank = stream_bank([P, UNIT])
-            lhs, lhs_scale = h_q[e // 4]
-            rhs, rhs_scale = dz_tok_q[u]
-            cols = slice((e % 4) * P, (e % 4 + 1) * P)
-            nc.tensor.matmul_mx(out=bank[:], lhsT=lhs[:, cols].bitcast(E4M3), lhsT_scale=lhs_scale[:, cols],
-                                rhs=rhs[:].bitcast(E5M2), rhs_scale=rhs_scale[:], start=True, stop=True)
-            if u == 0:
-                dw_rows[0, e] = rotating("dw_rows", [P, J], F32, 8)[:]
-            if u == 2 and e % 2 == 0:
-                two = rotating("w%d%d" % (e // 2 % 2, e // 4), [P, 2, J], F32, 1)
-                dw_rows[1, e], dw_rows[1, e + 1] = two[:, 0], two[:, 1]
-            rows = dw_rows[u // 2, e]
-            copy(engine, rows[:, (u % 2) * UNIT : (u % 2 + 1) * UNIT], bank[:])
-            if alone:
-                part = slice((u % 2) * UNIT, (u % 2 + 1) * UNIT)
-                nc.sync.dma_start(out=weight_grads[u // 2][e * P : (e + 1) * P, part], in_=rows[:, part])
-            elif u % 2 == 1:
-                nc.sync.dma_start(out=weight_grads[u // 2][e * P : (e + 1) * P, :], in_=rows)
-
-        def dh(j, h, u):
-            if u == 0:
-                dh_bank[j, h] = psum.tile([P, HALF], F32, name="dh", tag="dh", bufs=4)
-            cols = slice(j * P, (j + 1) * P)
-            lhs, lhs_scale = dz_feat_q[u]
-            rhs, rhs_scale = w_q[u // 2][h]
-            e_cols = slice((u % 2) * HALF, (u % 2 + 1) * HALF)
-            nc.tensor.matmul_mx(out=dh_bank[j, h][:], lhsT=lhs[:, cols].bitcast(E5M2), lhsT_scale=lhs_scale[:, cols],
-                                rhs=rhs[:, e_cols].bitcast(E4M3), rhs_scale=rhs_scale[:, e_cols], start=(u == 0), stop=(u == UNITS - 1))
 
         def scale(j, h):
             if h == 0 and j < 2:
                 scaled[j] = rotating("dq%d" % j, [P, E], F32, 1)[:]
             if h == 0 and j == 2:
-                two = rotating("dk", [P, 2, E], F32, 1)
-                scaled[2], scaled[3] = two[:, 0], two[:, 1]
+                both = rotating("dk", [P, 2, E], F32, 1)
+                scaled[2], scaled[3] = both[:, 0], both[:, 1]
             nc.vector.tensor_tensor(out=scaled[j][:, h * HALF : (h + 1) * HALF], in0=dh_bank[j, h][:], in1=rg[:, h, j], op=ALU.mult)
 
         def dot(j):
@@ -244,63 +174,158 @@ def tile_llamaselfattentionblock_pa_v_kernel(tc, x, g, wq, wk, rstd, grad_0, gra
             nc.vector.scalar_tensor_tensor(product[:], x_sb[:, j], neg_r2[:, j : j + 1], scaled[j], ALU.mult, ALU.mult,
                                            accum_out=coef[j][:])
 
-        def out(j, cols=slice(0, E), later=False):
+        def finish(j, cols):
             nc.vector.scalar_tensor_tensor(scaled[j][:, cols], x_sb[:, j, cols], coef[j][:], scaled[j][:, cols], ALU.mult, ALU.add)
-            if not later:
-                store_dx(j, cols)
 
-        def store_dx(j, cols=slice(0, E)):
+        def store_dx(j, cols):
             nc.sync.dma_start(out=out_rows[:, j, cols], in_=scaled[j][:, cols])
 
-        table_b()
-        for j in range(4): rg2(j)
-        rope(0); rope(1,(0,)); interleave(0); rope(1,(1,))
-        for jp in range(2): turn_dz(0,jp)
+        def stream_bank(shape):
+            return psum.tile(shape, F32, name="stream", tag="stream", bufs=STREAM_BANKS)
+
+        def turn_dz(u):
+            dz_feat[u] = rotating("dz_feat", [P, 4 * T], BF16, UNITS)
+            words = dz[u][:].rearrange("p j v c -> p (j v c)").bitcast(F32)
+            for jp in range(2):
+                bank = stream_bank([P, 4, P])
+                for k in range(4):
+                    first = (4 * jp + k) * P
+                    nc.tensor.transpose(bank[:, k, :], words[:, first : first + P], identity[:])
+                rows = dz_feat[u][:].bitcast(F32)[:, jp * 4 * P : (jp + 1) * 4 * P]
+                nc.scalar.copy(out=rows.rearrange("p (j q v) -> p j q v", j=2, v=2), in_=bank[:].rearrange("p (j v) q -> p j q v", v=2))
+
+        def turn_w(u, h):
+            if u % 2 == 0:
+                w_feat[u // 2, h] = rotating("w_feat", [P, 2, 4 * HALF], BF16, 4)
+            words = w_sb[u // 2][h][:].rearrange("p i f -> p (i f)").bitcast(F32)
+            for ip in range(2):
+                bank = stream_bank([P, 4, P])
+                for i in range(2):
+                    first = (2 * ip + i) * (J // 2) + (u % 2) * (UNIT // 2)
+                    for v in range(2):
+                        nc.tensor.transpose(bank[:, 2 * i + v, :], words[:, first + v : first + UNIT // 2 : 2], identity[:])
+                rows = w_feat[u // 2, h][:, u % 2].bitcast(F32)[:, ip * 4 * P : (ip + 1) * 4 * P]
+                nc.scalar.copy(out=rows.rearrange("p (i q v) -> p i q v", i=2, v=2), in_=bank[:].rearrange("p (i v) q -> p i q v", v=2))
+
+        def dw(u, r):
+            bank = stream_bank([P, UNIT])
+            lhs, lhs_scale = h_q[r // 4]
+            rhs, rhs_scale = dz_tok_q[u]
+            cols = slice((r % 4) * P, (r % 4 + 1) * P)
+            nc.tensor.matmul_mx(out=bank[:], lhsT=lhs[:, cols].bitcast(E4M3), lhsT_scale=lhs_scale[:, cols],
+                                rhs=rhs[:].bitcast(E5M2), rhs_scale=rhs_scale[:], start=True, stop=True)
+            if u == 0:
+                dw_rows[0, r] = rotating("dw_rows", [P, J], F32, ROW_TILES)[:]
+            if u == 2 and r % 2 == 0:
+                both = rotating("w%d%d" % (r // 2 % 2, r // 4), [P, 2, J], F32, 1)
+                dw_rows[1, r], dw_rows[1, r + 1] = both[:, 0], both[:, 1]
+            rows = dw_rows[u // 2, r]
+            nc.scalar.copy(out=rows[:, (u % 2) * UNIT : (u % 2 + 1) * UNIT], in_=bank[:])
+            if u % 2 == 1:
+                nc.sync.dma_start(out=weight_grads[u // 2][r * P : (r + 1) * P, :], in_=rows)
+
+        def dh(j, h, u):
+            if u == 0:
+                dh_bank[j, h] = psum.tile([P, HALF], F32, name="dh", tag="dh", bufs=DH_BANKS)
+            cols = slice(j * P, (j + 1) * P)
+            lhs, lhs_scale = dz_feat_q[u]
+            rhs, rhs_scale = w_q[u // 2][h]
+            e_cols = slice((u % 2) * HALF, (u % 2 + 1) * HALF)
+            nc.tensor.matmul_mx(out=dh_bank[j, h][:], lhsT=lhs[:, cols].bitcast(E5M2), lhsT_scale=lhs_scale[:, cols],
+                                rhs=rhs[:, e_cols].bitcast(E4M3), rhs_scale=rhs_scale[:, e_cols], start=(u == 0), stop=(u == UNITS - 1))
+
+        whole_row, first_half, second_half = slice(0, E), slice(0, HALF), slice(HALF, E)
+
+        rope(0, 0)
+        rope(0, 1)
+        rope(1, 0)
+        interleave(0)
+        rope(1, 1)
+        turn_dz(0)
         for u in range(2):
-            for ip in range(2): turn_w(u,0,ip)
-        load_pair(dk_sb, 1, 0, HEADS)
+            turn_w(u, 0)
+        load_grad(dk_sb, 1, 0, HEADS)
         load_w(0, 1)
         load_w(1, 1)
-        for jp in range(2): turn_dz(1,jp)
-        norm(0); qt(0); qh(0); qz(0)
-        for ip in range(2): turn_w(2,0,ip)
-        for e in range(4): dw(0,e)
-        interleave(1); qw(0,0); qz(1)
-        for ip in range(2): turn_w(3,0,ip)
-        norm(1); qt(1); qh(1)
-        for e in range(4): dh(e,0,0); dw(1,e)
-        rope(2)
-        dw(0,4,"V"); dh(0,0,1); dw(1,4,"V"); dh(1,0,1)
-        for ip in range(2): turn_w(0,1,ip)
-        dw(0,5); dh(2,0,1); dw(1,5); dh(3,0,1)
-        for jp in range(2): turn_dz(2,jp)
-        rope(3)
-        for ip in range(2): turn_w(1,1,ip)
-        dw(0,6); dw(1,6)
-        interleave(2); qw(1,0); qt(2); interleave(3); qz(2)
-        for jp in range(2): turn_dz(3,jp)
-        dw(0,7); dh(0,0,2); dw(1,7); dh(1,0,2)
-        for ip in range(2): turn_w(2,1,ip)
-        dh(2,0,2); dh(3,0,2)
-        qt(3); qz(3)
-        for ip in range(2): turn_w(3,1,ip)
-        dw(2,0); dh(0,0,3); dh(1,0,3); dw(3,0); dh(2,0,3); dh(3,0,3)
-        qw(0,1); row_factor()
-        for j in range(2): scale(j,0)
-        qw(1,1)
-        for j in range(2,4): scale(j,0)
-        dw(2,1); dw(3,1)
-        for u in range(2):
-            for j in range(2): dh(j,1,u)
-        dw(2,2)
+        turn_dz(1)
+        for u in range(2, 4):
+            turn_w(u, 0)
+        norm(0)
+        quantize_dz_tok(0)
+        interleave(1)
+        quantize_h(0)
+        quantize_dz_tok(1)
+        for r in range(4):
+            dw(0, r)
+            dw(1, r)
+
+        def out_1_rows(r):
+            for k in range(2):
+                dw(k, r)
+                dh(2 * (r % 2) + k, 0, (r - 4) // 2)
+
+        norm(1)
+        quantize_dz_feat(0)
+        quantize_h(1)
+        quantize_w(0, 0)
+        quantize_dz_feat(1)
+        rope(2, 0)
+        rope(2, 1)
+        turn_w(0, 1)
+        out_1_rows(4)
+        turn_w(1, 1)
+        out_1_rows(5)
+        turn_dz(2)
+        rope(3, 0)
+        interleave(2)
+        rope(3, 1)
+        quantize_dz_tok(2)
+        interleave(3)
+        quantize_w(1, 0)
+        quantize_dz_tok(3)
+        out_1_rows(6)
+        turn_dz(3)
+        out_1_rows(7)
+        turn_w(2, 1)
+        quantize_dz_feat(2)
+        quantize_dz_feat(3)
+        quantize_w(0, 1)
+        dw(2, 0)
+        dw(3, 0)
+        turn_w(3, 1)
+
+        for j in range(SLOTS):
+            dh(j, 0, 2)
+            dh(j, 0, 3)
+            dw(2 + j % 2, 1 + j // 2)
+        nc.vector.scalar_tensor_tensor(neg_r2[:], rstd_sb[:], -1.0 / E, rstd_sb[:], ALU.mult, ALU.mult)
         for j in range(2):
-            for u in range(2,4): dh(j,1,u)
-        dw(3,2)
-        scale(0,1); scale(1,1); dot(0); dot(1)
-        for e in range(3,7):
-            dw(2,e); dh((e+1)//2,1,2*((e+1)%2)); dw(3,e); dh((e+1)//2,1,2*((e+1)%2)+1)
-            if e == 4: out(0)
-        scale(2,1); out(1)
-        dw(2,7); dw(3,7)
-        dot(2); scale(3,1)
-        out(2); dot(3); out(3, slice(0, HALF)); out(3, slice(HALF, E))
+            scale(j, 0)
+        quantize_w(1, 1)
+        for j in range(2, 4):
+            scale(j, 0)
+
+        def norm_backward(j):
+            scale(j, 1)
+            if j > 0:
+                finish(j - 1, whole_row)
+            dot(j)
+
+        for j in range(2):
+            for k in range(2):
+                dh(j, 1, 2 * k)
+                dh(j, 1, 2 * k + 1)
+                dw(2 + k, 3 + j)
+            norm_backward(j)
+        for r in range(5, ROW_TILES):
+            dw(2, r)
+            dw(3, r)
+        for j in range(2, 4):
+            for u in range(UNITS):
+                dh(j, 1, u)
+            norm_backward(j)
+        for j in range(3):
+            store_dx(j, whole_row)
+        for cols in (first_half, second_half):
+            finish(3, cols)
+            store_dx(3, cols)

@@ -34,8 +34,8 @@ def tile_llamaselfattentionblock_pa_v_kernel(tc, x, g, wq, wk, rstd, grad_0, gra
     grads = (grad_0, grad_1)
     weights = (wq, wk)
     weight_grads = (out_1, out_2)
-    x_rows = x.flatten_outer_dims().rearrange("(p j) e -> p j e", j=SLOTS)
-    out_rows = out_0.flatten_outer_dims().rearrange("(p j) e -> p j e", j=SLOTS)
+    x_rows = x.flatten_outer_dims().rearrange("(p j) (h c) -> p h j c", j=SLOTS, h=2)
+    out_rows = out_0.flatten_outer_dims().rearrange("(p j) (h c) -> p j h c", j=SLOTS, h=2)
 
     with ExitStack() as ctx:
         keep = ctx.enter_context(tc.tile_pool(name="keep", bufs=1))
@@ -57,7 +57,7 @@ def tile_llamaselfattentionblock_pa_v_kernel(tc, x, g, wq, wk, rstd, grad_0, gra
         rstd_sb = kept("rstd_sb", [P, SLOTS], F32)
         g_sb = kept("g_sb", [P, E // P], BF16)
         identity = kept("identity", [P, P], F32)
-        x_sb = kept("x_sb", [P, SLOTS, E], BF16)
+        x_sb = kept("x_sb", [P, 2, SLOTS, HALF], BF16)
         rg = kept("rg", [P, 2, SLOTS, HALF], F32)
         w_sb = [[rotating("w%d%d" % (a, h), [P, 4, J], BF16, 1) for h in range(2)] for a in range(2)]
         h_tok = [kept("h_tok%d" % h, [P, HALF, SLOTS], BF16) for h in range(2)]
@@ -77,8 +77,8 @@ def tile_llamaselfattentionblock_pa_v_kernel(tc, x, g, wq, wk, rstd, grad_0, gra
                     queue.dma_start(out=dst[32 * batch : 32 * batch + 32].rearrange("q n j d -> q n (j d)"),
                                     in_=grads[a][batch, first_head : first_head + heads].rearrange("n (q j) d -> q n (j d)", j=SLOTS))
 
-        def load_w(a, h):
-            nc.sync.dma_start(out=w_sb[a][h][:], in_=weights[a][h * HALF : (h + 1) * HALF, :].rearrange("(i q) f -> q i f", i=4))
+        def load_w(a, h, queue):
+            queue.dma_start(out=w_sb[a][h][:], in_=weights[a][h * HALF : (h + 1) * HALF, :].rearrange("(i q) f -> q i f", i=4))
 
         tokens = kept("tokens", [P, SLOTS], I32)
         nc.gpsimd.iota(tokens[:], pattern=[[1, SLOTS]], base=0, channel_multiplier=SLOTS)
@@ -87,9 +87,10 @@ def tile_llamaselfattentionblock_pa_v_kernel(tc, x, g, wq, wk, rstd, grad_0, gra
         nc.sync.dma_start(out=g_sb[:], in_=g.rearrange("(p c) -> p c", p=P))
         for u in range(2):
             load_grad(dq_sb[u], 0, u * UNIT_HEADS, UNIT_HEADS)
-        load_w(0, 0)
-        nc.sync.dma_start(out=x_sb[:], in_=x_rows)
-        load_w(1, 0)
+        nc.sync.dma_start(out=x_sb[:, 0], in_=x_rows[:, 0])
+        load_w(0, 0, nc.sync)
+        load_w(1, 0, nc.sync)
+        nc.sync.dma_start(out=x_sb[:, 1], in_=x_rows[:, 1])
 
         positions = kept("positions", [P, SLOTS], I32)
         coarse = kept("coarse", [P, SLOTS, 4], F32)
@@ -143,7 +144,7 @@ def tile_llamaselfattentionblock_pa_v_kernel(tc, x, g, wq, wk, rstd, grad_0, gra
 
         def norm(h):
             nc.vector.tensor_tensor(out=h_tok[h][:].rearrange("p (c i) j -> p c j i", i=2),
-                                    in0=x_sb[:, :, h * HALF : (h + 1) * HALF].rearrange("p j (c i) -> p c j i", i=2),
+                                    in0=x_sb[:, h].rearrange("p j (c i) -> p c j i", i=2),
                                     in1=rg[:, h].rearrange("p j (c i) -> p c j i", i=2), op=ALU.mult)
 
         def quantize(pair, dtype, values):
@@ -163,22 +164,22 @@ def tile_llamaselfattentionblock_pa_v_kernel(tc, x, g, wq, wk, rstd, grad_0, gra
 
         def scale(j, h):
             if h == 0 and j < 2:
-                scaled[j] = rotating("dq%d" % j, [P, E], F32, 1)[:]
+                scaled[j] = rotating("dq%d" % j, [P, 2, HALF], F32, 1)[:]
             if h == 0 and j == 2:
-                both = rotating("dk", [P, 2, E], F32, 1)
+                both = rotating("dk", [P, 2, 2, HALF], F32, 1)
                 scaled[2], scaled[3] = both[:, 0], both[:, 1]
-            nc.vector.tensor_tensor(out=scaled[j][:, h * HALF : (h + 1) * HALF], in0=dh_bank[j, h][:], in1=rg[:, h, j], op=ALU.mult)
+            nc.vector.tensor_tensor(out=scaled[j][:, h], in0=dh_bank[j, h][:], in1=rg[:, h, j], op=ALU.mult)
 
         def dot(j):
-            product = rotating("dz", [P, E], F32, 2)
-            nc.vector.scalar_tensor_tensor(product[:], x_sb[:, j], neg_r2[:, j : j + 1], scaled[j], ALU.mult, ALU.mult,
+            product = rotating("dz", [P, 2, HALF], F32, 2)
+            nc.vector.scalar_tensor_tensor(product[:], x_sb[:, :, j], neg_r2[:, j : j + 1], scaled[j], ALU.mult, ALU.mult,
                                            accum_out=coef[j][:])
 
-        def finish(j, cols):
-            nc.vector.scalar_tensor_tensor(scaled[j][:, cols], x_sb[:, j, cols], coef[j][:], scaled[j][:, cols], ALU.mult, ALU.add)
+        def finish(j, halves):
+            nc.vector.scalar_tensor_tensor(scaled[j][:, halves], x_sb[:, halves, j], coef[j][:], scaled[j][:, halves], ALU.mult, ALU.add)
 
-        def store_dx(j, cols):
-            nc.sync.dma_start(out=out_rows[:, j, cols], in_=scaled[j][:, cols])
+        def store_dx(j, halves, queue):
+            queue.dma_start(out=out_rows[:, j, halves], in_=scaled[j][:, halves])
 
         def stream_bank(shape):
             return psum.tile(shape, F32, name="stream", tag="stream", bufs=STREAM_BANKS)
@@ -207,6 +208,11 @@ def tile_llamaselfattentionblock_pa_v_kernel(tc, x, g, wq, wk, rstd, grad_0, gra
                 rows = w_feat[u // 2, h][:, u % 2].bitcast(F32)[:, ip * 4 * P : (ip + 1) * 4 * P]
                 nc.scalar.copy(out=rows.rearrange("p (i q v) -> p i q v", i=2, v=2), in_=bank[:].rearrange("p (i v) q -> p i q v", v=2))
 
+        waiting = []
+
+        def store_dw(a, r, queue):
+            queue.dma_start(out=weight_grads[a][r * P : (r + 1) * P, :], in_=dw_rows[a, r])
+
         def dw(u, r):
             bank = stream_bank([P, UNIT])
             lhs, lhs_scale = h_q[r // 4]
@@ -221,8 +227,15 @@ def tile_llamaselfattentionblock_pa_v_kernel(tc, x, g, wq, wk, rstd, grad_0, gra
                 dw_rows[1, r], dw_rows[1, r + 1] = both[:, 0], both[:, 1]
             rows = dw_rows[u // 2, r]
             nc.scalar.copy(out=rows[:, (u % 2) * UNIT : (u % 2 + 1) * UNIT], in_=bank[:])
+            while waiting:
+                store_dw(*waiting.pop(), nc.scalar)
             if u % 2 == 1:
-                nc.sync.dma_start(out=weight_grads[u // 2][r * P : (r + 1) * P, :], in_=rows)
+                if r % 2 == 0 or (u == 1 and r < 4):
+                    store_dw(u // 2, r, nc.sync)
+                elif (u, r) == (UNITS - 1, ROW_TILES - 1):
+                    store_dw(u // 2, r, nc.scalar)
+                else:
+                    waiting.append((u // 2, r))
 
         def dh(j, h, u):
             if u == 0:
@@ -234,7 +247,7 @@ def tile_llamaselfattentionblock_pa_v_kernel(tc, x, g, wq, wk, rstd, grad_0, gra
             nc.tensor.matmul_mx(out=dh_bank[j, h][:], lhsT=lhs[:, cols].bitcast(E5M2), lhsT_scale=lhs_scale[:, cols],
                                 rhs=rhs[:, e_cols].bitcast(E4M3), rhs_scale=rhs_scale[:, e_cols], start=(u == 0), stop=(u == UNITS - 1))
 
-        whole_row, first_half, second_half = slice(0, E), slice(0, HALF), slice(HALF, E)
+        whole_row, first_half, second_half = slice(0, 2), slice(0, 1), slice(1, 2)
 
         rope(0, 0)
         rope(0, 1)
@@ -245,8 +258,6 @@ def tile_llamaselfattentionblock_pa_v_kernel(tc, x, g, wq, wk, rstd, grad_0, gra
         for u in range(2):
             turn_w(u, 0)
         load_grad(dk_sb, 1, 0, HEADS)
-        load_w(0, 1)
-        load_w(1, 1)
         turn_dz(1)
         for u in range(2, 4):
             turn_w(u, 0)
@@ -255,9 +266,12 @@ def tile_llamaselfattentionblock_pa_v_kernel(tc, x, g, wq, wk, rstd, grad_0, gra
         interleave(1)
         quantize_h(0)
         quantize_dz_tok(1)
+        load_w(0, 1, nc.scalar)
         for r in range(4):
             dw(0, r)
             dw(1, r)
+            if r == 1:
+                load_w(1, 1, nc.scalar)
 
         def out_1_rows(r):
             for k in range(2):
@@ -271,10 +285,10 @@ def tile_llamaselfattentionblock_pa_v_kernel(tc, x, g, wq, wk, rstd, grad_0, gra
         quantize_dz_feat(1)
         rope(2, 0)
         rope(2, 1)
-        turn_w(0, 1)
         out_1_rows(4)
-        turn_w(1, 1)
+        turn_w(0, 1)
         out_1_rows(5)
+        turn_w(1, 1)
         turn_dz(2)
         rope(3, 0)
         interleave(2)
@@ -309,6 +323,7 @@ def tile_llamaselfattentionblock_pa_v_kernel(tc, x, g, wq, wk, rstd, grad_0, gra
             scale(j, 1)
             if j > 0:
                 finish(j - 1, whole_row)
+                store_dx(j - 1, whole_row, nc.sync)
             dot(j)
 
         for j in range(2):
@@ -317,15 +332,15 @@ def tile_llamaselfattentionblock_pa_v_kernel(tc, x, g, wq, wk, rstd, grad_0, gra
                 dh(j, 1, 2 * k + 1)
                 dw(2 + k, 3 + j)
             norm_backward(j)
-        for r in range(5, ROW_TILES):
-            dw(2, r)
-            dw(3, r)
         for j in range(2, 4):
             for u in range(UNITS):
                 dh(j, 1, u)
-            norm_backward(j)
-        for j in range(3):
-            store_dx(j, whole_row)
-        for cols in (first_half, second_half):
-            finish(3, cols)
-            store_dx(3, cols)
+        for r in range(5, ROW_TILES):
+            dw(2, r)
+            dw(3, r)
+            if r == 5:
+                norm_backward(2)
+        norm_backward(3)
+        for halves, queue in ((first_half, nc.sync), (second_half, nc.scalar)):
+            finish(3, halves)
+            store_dx(3, halves, queue)

@@ -34,7 +34,7 @@ def tile_llamaselfattentionblock_pa_v_kernel(tc, x, g, wq, wk, rstd, grad_0, gra
     grads = (grad_0, grad_1)
     weights = (wq, wk)
     weight_grads = (out_1, out_2)
-    x_rows = x.flatten_outer_dims().rearrange("(p j) (h c) -> p h j c", j=SLOTS, h=2)
+    x_rows = x.flatten_outer_dims().rearrange("(p j) e -> p j e", j=SLOTS)
     out_rows = out_0.flatten_outer_dims().rearrange("(p j) (h c) -> p j h c", j=SLOTS, h=2)
 
     with ExitStack() as ctx:
@@ -51,13 +51,17 @@ def tile_llamaselfattentionblock_pa_v_kernel(tc, x, g, wq, wk, rstd, grad_0, gra
         def codes(name, width):
             return kept(name + "_codes", [P, width], U32), kept(name + "_scales", [P, width], U8)
 
+        def bank(k, shape):
+            return psum.tile(shape, F32, name="bank%d" % k, tag="bank%d" % k, bufs=1)
+
         dq_sb = [rotating("dq%d" % u, [P, UNIT_HEADS, SLOTS, HD], BF16, 1) for u in range(2)]
         dk_sb = rotating("dk", [P, HEADS, SLOTS, HD], BF16, 1)
         grad_sb = [dq_sb[0][:], dq_sb[1][:], dk_sb[:, 0:UNIT_HEADS], dk_sb[:, UNIT_HEADS:HEADS]]
         rstd_sb = kept("rstd_sb", [P, SLOTS], F32)
         g_sb = kept("g_sb", [P, E // P], BF16)
         identity = kept("identity", [P, P], F32)
-        x_sb = kept("x_sb", [P, 2, SLOTS, HALF], BF16)
+        x_sb = kept("x_sb", [P, SLOTS, E], BF16)
+        x_halves = x_sb[:].rearrange("p j (h c) -> p j h c", h=2)
         rg = kept("rg", [P, 2, SLOTS, HALF], F32)
         w_sb = [[rotating("w%d%d" % (a, h), [P, 4, J], BF16, 1) for h in range(2)] for a in range(2)]
         h_tok = [kept("h_tok%d" % h, [P, HALF, SLOTS], BF16) for h in range(2)]
@@ -77,8 +81,19 @@ def tile_llamaselfattentionblock_pa_v_kernel(tc, x, g, wq, wk, rstd, grad_0, gra
                     queue.dma_start(out=dst[32 * batch : 32 * batch + 32].rearrange("q n j d -> q n (j d)"),
                                     in_=grads[a][batch, first_head : first_head + heads].rearrange("n (q j) d -> q n (j d)", j=SLOTS))
 
+        def load_dk(queue, batches):
+            for batch in batches:
+                queue.dma_start(out=dk_sb[32 * batch : 32 * batch + 32].rearrange("q n j d -> q n (j d)"),
+                                in_=grad_1[batch].rearrange("n (q j) d -> q n (j d)", j=SLOTS))
+
+        def load_dk_scalar():
+            load_dk(nc.scalar, (2, 3))
+
+        def load_x():
+            nc.sync.dma_start(out=x_sb[:], in_=x_rows)
+
         def load_w(a, h, queue):
-            queue.dma_start(out=w_sb[a][h][:], in_=weights[a][h * HALF : (h + 1) * HALF, :].rearrange("(i q) f -> q i f", i=4))
+            queue.dma_start(out=w_sb[a][h][:], in_=weights[a][h * HALF : (h + 1) * HALF, :].rearrange("(q i) f -> q i f", i=4))
 
         tokens = kept("tokens", [P, SLOTS], I32)
         nc.gpsimd.iota(tokens[:], pattern=[[1, SLOTS]], base=0, channel_multiplier=SLOTS)
@@ -87,10 +102,6 @@ def tile_llamaselfattentionblock_pa_v_kernel(tc, x, g, wq, wk, rstd, grad_0, gra
         nc.sync.dma_start(out=g_sb[:], in_=g.rearrange("(p c) -> p c", p=P))
         for u in range(2):
             load_grad(dq_sb[u], 0, u * UNIT_HEADS, UNIT_HEADS)
-        nc.sync.dma_start(out=x_sb[:, 0], in_=x_rows[:, 0])
-        load_w(0, 0, nc.sync)
-        load_w(1, 0, nc.sync)
-        nc.sync.dma_start(out=x_sb[:, 1], in_=x_rows[:, 1])
 
         positions = kept("positions", [P, SLOTS], I32)
         coarse = kept("coarse", [P, SLOTS, 4], F32)
@@ -118,7 +129,7 @@ def tile_llamaselfattentionblock_pa_v_kernel(tc, x, g, wq, wk, rstd, grad_0, gra
             nc.vector.scalar_tensor_tensor(fraction[:, js].rearrange("p j i -> p (j i)"), turns[:, js].rearrange("p j i -> p (j i)"), 0.25,
                                            whole[:, js].rearrange("p j i -> p (j i)"), ALU.add, ALU.subtract)
 
-        gain_words = psum.tile([P, P, 4], F32, name="gain", tag="dh", bufs=DH_BANKS)
+        gain_words = bank(0, [P, P, 4])
         for k in range(4):
             nc.tensor.transpose(gain_words[:, :, k], g_sb[:].bitcast(F32)[:, k : k + 1].to_broadcast([P, P]), identity[:])
         gain = gain_words[:].rearrange("p q k -> p (q k)").bitcast(BF16)
@@ -127,8 +138,10 @@ def tile_llamaselfattentionblock_pa_v_kernel(tc, x, g, wq, wk, rstd, grad_0, gra
         for v in range(2):
             nc.scalar.activation(out=cosines[:, v].rearrange("p (k s) -> p k s", s=2), in_=angles[:, v].unsqueeze(2).to_broadcast([P, P, 2]),
                                  func=ACT.Sin, scale=2.0 * math.pi)
-        for j in range(SLOTS):
-            nc.scalar.activation(out=rg[:, :, j], in_=gain.rearrange("p (h c) -> p h c", h=2), func=ACT.Copy, scale=rstd_sb[:, j : j + 1])
+
+        def scale_gain(h):
+            for j in range(SLOTS):
+                nc.scalar.activation(out=rg[:, h, j], in_=gain[:, h * HALF : (h + 1) * HALF], func=ACT.Copy, scale=rstd_sb[:, j : j + 1])
 
         def rope(u, v):
             if v == 0:
@@ -137,14 +150,13 @@ def tile_llamaselfattentionblock_pa_v_kernel(tc, x, g, wq, wk, rstd, grad_0, gra
             nc.vector.tensor_tensor(out=dz[u][:, :, v, :].rearrange("p j (n c) -> p n j c", n=UNIT_HEADS), in0=pairs[:, :, v, :],
                                     in1=cosines[:, v, :].unsqueeze(1).to_broadcast([P, UNIT_HEADS, 2 * P]), op=ALU.mult)
 
-        def interleave(u):
+        def interleave(u, copy):
             dz_tok[u] = rotating("dz_tok", [P, UNIT, SLOTS], BF16, 2)
-            nc.vector.tensor_copy(out=dz_tok[u][:].rearrange("p (m v s) j -> p v m j s", v=2, s=2),
-                                  in_=dz[u][:].rearrange("p j v (m s) -> p v m j s", s=2))
+            copy(out=dz_tok[u][:].rearrange("p (m v s) j -> p v m j s", v=2, s=2), in_=dz[u][:].rearrange("p j v (m s) -> p v m j s", s=2))
 
         def norm(h):
             nc.vector.tensor_tensor(out=h_tok[h][:].rearrange("p (c i) j -> p c j i", i=2),
-                                    in0=x_sb[:, h].rearrange("p j (c i) -> p c j i", i=2),
+                                    in0=x_sb[:, :, h * HALF : (h + 1) * HALF].rearrange("p j (c i) -> p c j i", i=2),
                                     in1=rg[:, h].rearrange("p j (c i) -> p c j i", i=2), op=ALU.mult)
 
         def quantize(pair, dtype, values):
@@ -172,41 +184,45 @@ def tile_llamaselfattentionblock_pa_v_kernel(tc, x, g, wq, wk, rstd, grad_0, gra
 
         def dot(j):
             product = rotating("dz", [P, 2, HALF], F32, 2)
-            nc.vector.scalar_tensor_tensor(product[:], x_sb[:, :, j], neg_r2[:, j : j + 1], scaled[j], ALU.mult, ALU.mult,
+            nc.vector.scalar_tensor_tensor(product[:], x_halves[:, j], neg_r2[:, j : j + 1], scaled[j], ALU.mult, ALU.mult,
                                            accum_out=coef[j][:])
 
         def finish(j, halves):
-            nc.vector.scalar_tensor_tensor(scaled[j][:, halves], x_sb[:, halves, j], coef[j][:], scaled[j][:, halves], ALU.mult, ALU.add)
+            nc.vector.scalar_tensor_tensor(scaled[j][:, halves], x_halves[:, j, halves], coef[j][:], scaled[j][:, halves], ALU.mult, ALU.add)
 
         def store_dx(j, halves, queue):
             queue.dma_start(out=out_rows[:, j, halves], in_=scaled[j][:, halves])
 
+        stream = list(range(1, 8)) + [0]
+
         def stream_bank(shape):
-            return psum.tile(shape, F32, name="stream", tag="stream", bufs=STREAM_BANKS)
+            k = stream.pop(0)
+            stream.append(k)
+            return bank(k, shape)
 
         def turn_dz(u):
             dz_feat[u] = rotating("dz_feat", [P, 4 * T], BF16, UNITS)
             words = dz[u][:].rearrange("p j v c -> p (j v c)").bitcast(F32)
             for jp in range(2):
-                bank = stream_bank([P, 4, P])
+                ps = stream_bank([P, 4, P])
                 for k in range(4):
                     first = (4 * jp + k) * P
-                    nc.tensor.transpose(bank[:, k, :], words[:, first : first + P], identity[:])
+                    nc.tensor.transpose(ps[:, k, :], words[:, first : first + P], identity[:])
                 rows = dz_feat[u][:].bitcast(F32)[:, jp * 4 * P : (jp + 1) * 4 * P]
-                nc.scalar.copy(out=rows.rearrange("p (j q v) -> p j q v", j=2, v=2), in_=bank[:].rearrange("p (j v) q -> p j q v", v=2))
+                nc.scalar.copy(out=rows.rearrange("p (j q v) -> p j q v", j=2, v=2), in_=ps[:].rearrange("p (j v) q -> p j q v", v=2))
 
         def turn_w(u, h):
             if u % 2 == 0:
                 w_feat[u // 2, h] = rotating("w_feat", [P, 2, 4 * HALF], BF16, 4)
             words = w_sb[u // 2][h][:].rearrange("p i f -> p (i f)").bitcast(F32)
             for ip in range(2):
-                bank = stream_bank([P, 4, P])
+                ps = stream_bank([P, 4, P])
                 for i in range(2):
                     first = (2 * ip + i) * (J // 2) + (u % 2) * (UNIT // 2)
                     for v in range(2):
-                        nc.tensor.transpose(bank[:, 2 * i + v, :], words[:, first + v : first + UNIT // 2 : 2], identity[:])
-                rows = w_feat[u // 2, h][:, u % 2].bitcast(F32)[:, ip * 4 * P : (ip + 1) * 4 * P]
-                nc.scalar.copy(out=rows.rearrange("p (i q v) -> p i q v", i=2, v=2), in_=bank[:].rearrange("p (i v) q -> p i q v", v=2))
+                        nc.tensor.transpose(ps[:, 2 * i + v, :], words[:, first + v : first + UNIT // 2 : 2], identity[:])
+                rows = w_feat[u // 2, h][:, u % 2].bitcast(F32).rearrange("p (q i k) -> p i q k", i=2, k=4)
+                nc.scalar.copy(out=rows[:, ip], in_=ps[:].rearrange("p k q -> p q k"))
 
         waiting = []
 
@@ -214,11 +230,11 @@ def tile_llamaselfattentionblock_pa_v_kernel(tc, x, g, wq, wk, rstd, grad_0, gra
             queue.dma_start(out=weight_grads[a][r * P : (r + 1) * P, :], in_=dw_rows[a, r])
 
         def dw(u, r):
-            bank = stream_bank([P, UNIT])
+            ps = stream_bank([P, UNIT])
             lhs, lhs_scale = h_q[r // 4]
             rhs, rhs_scale = dz_tok_q[u]
             cols = slice((r % 4) * P, (r % 4 + 1) * P)
-            nc.tensor.matmul_mx(out=bank[:], lhsT=lhs[:, cols].bitcast(E4M3), lhsT_scale=lhs_scale[:, cols],
+            nc.tensor.matmul_mx(out=ps[:], lhsT=lhs[:, cols].bitcast(E4M3), lhsT_scale=lhs_scale[:, cols],
                                 rhs=rhs[:].bitcast(E5M2), rhs_scale=rhs_scale[:], start=True, stop=True)
             if u == 0:
                 dw_rows[0, r] = rotating("dw_rows", [P, J], F32, ROW_TILES)[:]
@@ -226,7 +242,7 @@ def tile_llamaselfattentionblock_pa_v_kernel(tc, x, g, wq, wk, rstd, grad_0, gra
                 both = rotating("w%d%d" % (r // 2 % 2, r // 4), [P, 2, J], F32, 1)
                 dw_rows[1, r], dw_rows[1, r + 1] = both[:, 0], both[:, 1]
             rows = dw_rows[u // 2, r]
-            nc.scalar.copy(out=rows[:, (u % 2) * UNIT : (u % 2 + 1) * UNIT], in_=bank[:])
+            nc.scalar.copy(out=rows[:, (u % 2) * UNIT : (u % 2 + 1) * UNIT], in_=ps[:])
             while waiting:
                 store_dw(*waiting.pop(), nc.scalar)
             if u % 2 == 1:
@@ -239,7 +255,9 @@ def tile_llamaselfattentionblock_pa_v_kernel(tc, x, g, wq, wk, rstd, grad_0, gra
 
         def dh(j, h, u):
             if u == 0:
-                dh_bank[j, h] = psum.tile([P, HALF], F32, name="dh", tag="dh", bufs=DH_BANKS)
+                if 4 + j in stream:
+                    stream.remove(4 + j)
+                dh_bank[j, h] = bank(4 + j, [P, HALF])
             cols = slice(j * P, (j + 1) * P)
             lhs, lhs_scale = dz_feat_q[u]
             rhs, rhs_scale = w_q[u // 2][h]
@@ -247,31 +265,48 @@ def tile_llamaselfattentionblock_pa_v_kernel(tc, x, g, wq, wk, rstd, grad_0, gra
             nc.tensor.matmul_mx(out=dh_bank[j, h][:], lhsT=lhs[:, cols].bitcast(E5M2), lhsT_scale=lhs_scale[:, cols],
                                 rhs=rhs[:, e_cols].bitcast(E4M3), rhs_scale=rhs_scale[:, e_cols], start=(u == 0), stop=(u == UNITS - 1))
 
-        whole_row, first_half, second_half = slice(0, 2), slice(0, 1), slice(1, 2)
 
+        whole_row, first_half, second_half = slice(0, 2), slice(0, 1), slice(1, 2)
+        on_vector, on_scalar = nc.vector.tensor_copy, nc.scalar.copy
+
+        def norm_backward(j):
+            scale(j, 1)
+            if j > 0:
+                finish(j - 1, whole_row)
+                store_dx(j - 1, whole_row, nc.sync)
+            dot(j)
+
+        load_w(0, 0, nc.sync)
+        load_x()
+        load_w(1, 0, nc.sync)
+        load_dk(nc.sync, (0, 1))
+        load_w(0, 1, nc.sync)
+        load_w(1, 1, nc.sync)
         rope(0, 0)
         rope(0, 1)
+        scale_gain(0)
+        scale_gain(1)
         rope(1, 0)
-        interleave(0)
+        interleave(0, on_vector)
         rope(1, 1)
         turn_dz(0)
-        for u in range(2):
-            turn_w(u, 0)
-        load_grad(dk_sb, 1, 0, HEADS)
+        turn_w(0, 0)
+
+        turn_w(1, 0)
+        load_dk_scalar()
         turn_dz(1)
-        for u in range(2, 4):
-            turn_w(u, 0)
+        turn_w(2, 0)
+
+        turn_w(3, 0)
+
         norm(0)
         quantize_dz_tok(0)
-        interleave(1)
+        interleave(1, on_vector)
         quantize_h(0)
         quantize_dz_tok(1)
-        load_w(0, 1, nc.scalar)
         for r in range(4):
             dw(0, r)
             dw(1, r)
-            if r == 1:
-                load_w(1, 1, nc.scalar)
 
         def out_1_rows(r):
             for k in range(2):
@@ -291,10 +326,10 @@ def tile_llamaselfattentionblock_pa_v_kernel(tc, x, g, wq, wk, rstd, grad_0, gra
         turn_w(1, 1)
         turn_dz(2)
         rope(3, 0)
-        interleave(2)
+        interleave(2, on_vector)
         rope(3, 1)
         quantize_dz_tok(2)
-        interleave(3)
+        interleave(3, on_vector)
         quantize_w(1, 0)
         quantize_dz_tok(3)
         out_1_rows(6)
@@ -307,7 +342,6 @@ def tile_llamaselfattentionblock_pa_v_kernel(tc, x, g, wq, wk, rstd, grad_0, gra
         dw(2, 0)
         dw(3, 0)
         turn_w(3, 1)
-
         for j in range(SLOTS):
             dh(j, 0, 2)
             dh(j, 0, 3)
@@ -318,29 +352,14 @@ def tile_llamaselfattentionblock_pa_v_kernel(tc, x, g, wq, wk, rstd, grad_0, gra
         quantize_w(1, 1)
         for j in range(2, 4):
             scale(j, 0)
-
-        def norm_backward(j):
-            scale(j, 1)
-            if j > 0:
-                finish(j - 1, whole_row)
-                store_dx(j - 1, whole_row, nc.sync)
-            dot(j)
-
-        for j in range(2):
+        for j in range(4):
             for k in range(2):
                 dh(j, 1, 2 * k)
                 dh(j, 1, 2 * k + 1)
                 dw(2 + k, 3 + j)
             norm_backward(j)
-        for j in range(2, 4):
-            for u in range(UNITS):
-                dh(j, 1, u)
-        for r in range(5, ROW_TILES):
-            dw(2, r)
-            dw(3, r)
-            if r == 5:
-                norm_backward(2)
-        norm_backward(3)
+        dw(2, 7)
+        dw(3, 7)
         for halves, queue in ((first_half, nc.sync), (second_half, nc.scalar)):
             finish(3, halves)
             store_dx(3, halves, queue)

@@ -62,7 +62,8 @@ def tile_llamaselfattentionblock_pa_v_kernel(tc, x, g, wq, wk, rstd, grad_0, gra
         identity = kept("identity", [P, P], F32)
         x_sb = kept("x_sb", [P, SLOTS, E], BF16)
         x_halves = x_sb[:].rearrange("p j (h c) -> p j h c", h=2)
-        rg = kept("rg", [P, 2, SLOTS, HALF], F32)
+        gain = kept("gain", [P, E], BF16)
+        h_flat = [kept("h_flat%d" % h, [P, SLOTS, HALF], BF16) for h in range(2)]
         w_sb = [[rotating("w%d%d" % (a, h), [P, 4, J], BF16, 1) for h in range(2)] for a in range(2)]
         h_tok = [kept("h_tok%d" % h, [P, HALF, SLOTS], BF16) for h in range(2)]
         h_q = [codes("h_q%d" % h, HALF) for h in range(2)]
@@ -132,32 +133,46 @@ def tile_llamaselfattentionblock_pa_v_kernel(tc, x, g, wq, wk, rstd, grad_0, gra
         gain_words = bank(0, [P, P, 4])
         for k in range(4):
             nc.tensor.transpose(gain_words[:, :, k], g_sb[:].bitcast(F32)[:, k : k + 1].to_broadcast([P, P]), identity[:])
-        gain = gain_words[:].rearrange("p q k -> p (q k)").bitcast(BF16)
+        gain_psum = gain_words[:].rearrange("p q k -> p (q k)")
 
         angles = fraction[:].rearrange("p j (w v) -> p v (j w)", v=2)
         for v in range(2):
             nc.scalar.activation(out=cosines[:, v].rearrange("p (k s) -> p k s", s=2), in_=angles[:, v].unsqueeze(2).to_broadcast([P, P, 2]),
                                  func=ACT.Sin, scale=2.0 * math.pi)
-
-        def scale_gain(h):
-            for j in range(SLOTS):
-                nc.scalar.activation(out=rg[:, h, j], in_=gain[:, h * HALF : (h + 1) * HALF], func=ACT.Copy, scale=rstd_sb[:, j : j + 1])
+        cosines_psum = bank(7, [P, 2, SLOTS * HD // 2])
+        for v in range(2):
+            nc.tensor.matmul(cosines_psum[:, v], lhsT=identity[:], rhs=cosines[:, v], start=True, stop=True)
+        nc.scalar.copy(out=gain[:].bitcast(F32), in_=gain_psum)
 
         def rope(u, v):
             if v == 0:
-                dz[u] = rotating("dz", [P, SLOTS, 2, UNIT // 2], BF16, 2)
+                dz[u] = rotating("dz", [P, SLOTS, 2, UNIT // 2], BF16, 4)
             pairs = grad_sb[u].rearrange("p n j (w v s) -> p (n j w) v s", v=2, s=2)
             nc.vector.tensor_tensor(out=dz[u][:, :, v, :].rearrange("p j (n c) -> p n j c", n=UNIT_HEADS), in0=pairs[:, :, v, :],
-                                    in1=cosines[:, v, :].unsqueeze(1).to_broadcast([P, UNIT_HEADS, 2 * P]), op=ALU.mult)
+                                    in1=(cosines if u == 0 else cosines_psum)[:, v, :].unsqueeze(1).to_broadcast([P, UNIT_HEADS, 2 * P]), op=ALU.mult)
 
         def interleave(u, copy):
-            dz_tok[u] = rotating("dz_tok", [P, UNIT, SLOTS], BF16, 2)
+            dz_tok[u] = rotating("dz_tok", [P, UNIT, SLOTS], BF16, 3)
             copy(out=dz_tok[u][:].rearrange("p (m v s) j -> p v m j s", v=2, s=2), in_=dz[u][:].rearrange("p j v (m s) -> p v m j s", s=2))
 
-        def norm(h):
-            nc.vector.tensor_tensor(out=h_tok[h][:].rearrange("p (c i) j -> p c j i", i=2),
-                                    in0=x_sb[:, :, h * HALF : (h + 1) * HALF].rearrange("p j (c i) -> p c j i", i=2),
-                                    in1=rg[:, h].rearrange("p j (c i) -> p c j i", i=2), op=ALU.mult)
+        def on_gpsimd(out, in_):
+            nc.gpsimd.tensor_scalar(out=out, in0=in_, scalar1=1.0, scalar2=1.0, op0=ALU.mult, op1=ALU.mult)
+
+        def interleave_gpsimd(u):
+            dz_tok[u] = rotating("dz_tok", [P, UNIT, SLOTS], BF16, 3)
+            for v in range(2):
+                on_gpsimd(dz_tok[u][:].rearrange("p (m v s) j -> p v m s j", v=2, s=2)[:, v], dz[u][:, :, v].rearrange("p j c -> p c j"))
+
+        def interleave_h_gpsimd(h):
+            on_gpsimd(h_tok[h][:], h_flat[h][:].rearrange("p j c -> p c j"))
+
+        def norm(h, j):
+            cols = slice(h * HALF, (h + 1) * HALF)
+            nc.vector.scalar_tensor_tensor(h_flat[h][:, j], x_sb[:, j, cols], rstd_sb[:, j : j + 1],
+                                           (gain_psum.bitcast(BF16) if (h, j) < (1, 2) else gain)[:, cols], ALU.mult, ALU.mult)
+
+        def interleave_h(h, copy):
+            copy(out=h_tok[h][:].rearrange("p (c i) j -> p c j i", i=4), in_=h_flat[h][:].rearrange("p j (c i) -> p c j i", i=4))
 
         def quantize(pair, dtype, values):
             nc.vector.quantize_mx(out=pair[0][:].bitcast(dtype), scales=pair[1][:], in_=values)
@@ -180,10 +195,10 @@ def tile_llamaselfattentionblock_pa_v_kernel(tc, x, g, wq, wk, rstd, grad_0, gra
             if h == 0 and j == 2:
                 both = rotating("dk", [P, 2, 2, HALF], F32, 1)
                 scaled[2], scaled[3] = both[:, 0], both[:, 1]
-            nc.vector.tensor_tensor(out=scaled[j][:, h], in0=dh_bank[j, h][:], in1=rg[:, h, j], op=ALU.mult)
+            nc.vector.scalar_tensor_tensor(scaled[j][:, h], dh_bank[j, h][:], rstd_sb[:, j : j + 1], gain[:, h * HALF : (h + 1) * HALF], ALU.mult, ALU.mult)
 
         def dot(j):
-            product = rotating("dz", [P, 2, HALF], F32, 2)
+            product = rotating("dz", [P, 2, HALF], F32, 4)
             nc.vector.scalar_tensor_tensor(product[:], x_halves[:, j], neg_r2[:, j : j + 1], scaled[j], ALU.mult, ALU.mult,
                                            accum_out=coef[j][:])
 
@@ -193,12 +208,17 @@ def tile_llamaselfattentionblock_pa_v_kernel(tc, x, g, wq, wk, rstd, grad_0, gra
         def store_dx(j, halves, queue):
             queue.dma_start(out=out_rows[:, j, halves], in_=scaled[j][:, halves])
 
-        stream = list(range(1, 8)) + [0]
+        stream = list(range(1, 7))
 
         def stream_bank(shape):
             k = stream.pop(0)
             stream.append(k)
             return bank(k, shape)
+
+        def narrow_stream():
+            for k in range(4, 7):
+                stream.remove(k)
+            stream.append(0)
 
         def turn_dz(u):
             dz_feat[u] = rotating("dz_feat", [P, 4 * T], BF16, UNITS)
@@ -255,8 +275,6 @@ def tile_llamaselfattentionblock_pa_v_kernel(tc, x, g, wq, wk, rstd, grad_0, gra
 
         def dh(j, h, u):
             if u == 0:
-                if 4 + j in stream:
-                    stream.remove(4 + j)
                 dh_bank[j, h] = bank(4 + j, [P, HALF])
             cols = slice(j * P, (j + 1) * P)
             lhs, lhs_scale = dz_feat_q[u]
@@ -279,87 +297,142 @@ def tile_llamaselfattentionblock_pa_v_kernel(tc, x, g, wq, wk, rstd, grad_0, gra
         load_w(0, 0, nc.sync)
         load_x()
         load_w(1, 0, nc.sync)
-        load_dk(nc.sync, (0, 1))
         load_w(0, 1, nc.sync)
+        load_dk(nc.sync, (0, 1))
         load_w(1, 1, nc.sync)
         rope(0, 0)
         rope(0, 1)
-        scale_gain(0)
-        scale_gain(1)
-        rope(1, 0)
-        interleave(0, on_vector)
-        rope(1, 1)
         turn_dz(0)
+        interleave_gpsimd(0)
         turn_w(0, 0)
-
-        turn_w(1, 0)
-        load_dk_scalar()
+        rope(1, 0)
+        rope(1, 1)
         turn_dz(1)
+        interleave_gpsimd(1)
+        turn_w(1, 0)
+        norm(0, 0)
         turn_w(2, 0)
-
+        norm(0, 1)
         turn_w(3, 0)
-
-        norm(0)
+        norm(0, 2)
+        load_dk_scalar()
+        norm(0, 3)
+        turn_w(0, 1)
+        norm(1, 0)
+        interleave_h(0, on_vector)
+        norm(1, 1)
+        narrow_stream()
         quantize_dz_tok(0)
-        interleave(1, on_vector)
         quantize_h(0)
+        dw(0, 0)
         quantize_dz_tok(1)
-        for r in range(4):
-            dw(0, r)
-            dw(1, r)
-
-        def out_1_rows(r):
-            for k in range(2):
-                dw(k, r)
-                dh(2 * (r % 2) + k, 0, (r - 4) // 2)
-
-        norm(1)
+        dw(1, 0)
         quantize_dz_feat(0)
-        quantize_h(1)
+        dw(0, 1)
         quantize_w(0, 0)
+        dw(1, 1)
         quantize_dz_feat(1)
+        turn_w(1, 1)
+        norm(1, 2)
+        dw(0, 2)
+        norm(1, 3)
+        dh(0, 0, 0)
+        interleave_h_gpsimd(1)
+        dw(1, 2)
         rope(2, 0)
         rope(2, 1)
-        out_1_rows(4)
-        turn_w(0, 1)
-        out_1_rows(5)
-        turn_w(1, 1)
-        turn_dz(2)
-        rope(3, 0)
-        interleave(2, on_vector)
-        rope(3, 1)
-        quantize_dz_tok(2)
-        interleave(3, on_vector)
-        quantize_w(1, 0)
-        quantize_dz_tok(3)
-        out_1_rows(6)
-        turn_dz(3)
-        out_1_rows(7)
+        dh(1, 0, 0)
+        interleave_gpsimd(2)
         turn_w(2, 1)
-        quantize_dz_feat(2)
-        quantize_dz_feat(3)
-        quantize_w(0, 1)
-        dw(2, 0)
-        dw(3, 0)
+        rope(3, 0)
+        rope(3, 1)
+        dw(0, 3)
+        quantize_w(1, 0)
+        dh(2, 0, 0)
+        quantize_h(1)
+        dw(1, 3)
+        interleave(3, on_vector)
+        dh(0, 0, 1)
         turn_w(3, 1)
-        for j in range(SLOTS):
-            dh(j, 0, 2)
-            dh(j, 0, 3)
-            dw(2 + j % 2, 1 + j // 2)
+        dh(1, 0, 1)
+        dh(2, 0, 1)
+        turn_dz(2)
+        quantize_dz_feat(2)
+        dh(3, 0, 0)
+        quantize_dz_tok(2)
+        dh(3, 0, 1)
+        turn_dz(3)
+        quantize_dz_feat(3)
+        dw(0, 4)
+        quantize_dz_tok(3)
+        dw(1, 4)
+        quantize_w(0, 1)
+        dw(0, 5)
         nc.vector.scalar_tensor_tensor(neg_r2[:], rstd_sb[:], -1.0 / E, rstd_sb[:], ALU.mult, ALU.mult)
-        for j in range(2):
-            scale(j, 0)
+        dw(1, 5)
+        dh(0, 0, 2)
+        dw(0, 6)
+        dh(1, 0, 2)
+        dw(1, 6)
+        dh(0, 0, 3)
+        scale(0, 0)
+        dw(0, 7)
+        dh(1, 0, 3)
+        scale(1, 0)
+        dw(1, 7)
         quantize_w(1, 1)
-        for j in range(2, 4):
-            scale(j, 0)
-        for j in range(4):
-            for k in range(2):
-                dh(j, 1, 2 * k)
-                dh(j, 1, 2 * k + 1)
-                dw(2 + k, 3 + j)
-            norm_backward(j)
+        dh(2, 0, 2)
+        dw(2, 0)
+        dh(2, 0, 3)
+        scale(2, 0)
+        dw(3, 0)
+        dh(3, 0, 2)
+        dh(3, 0, 3)
+        scale(3, 0)
+        dh(0, 1, 0)
+        dw(2, 1)
+        dh(0, 1, 1)
+        dw(3, 1)
+        dh(0, 1, 2)
+        dh(0, 1, 3)
+        scale(0, 1)
+        dw(2, 2)
+        dot(0)
+        dh(1, 1, 0)
+        dw(3, 2)
+        dh(1, 1, 1)
+        dw(2, 3)
+        dh(1, 1, 2)
+        dw(3, 3)
+        dh(1, 1, 3)
+        scale(1, 1)
+        dw(2, 4)
+        finish(0, whole_row)
+        store_dx(0, whole_row, nc.sync)
+        dw(3, 4)
+        dot(1)
+        dw(2, 5)
+        dh(2, 1, 0)
+        dw(3, 5)
+        dh(2, 1, 1)
+        dw(2, 6)
+        dh(2, 1, 2)
+        dw(3, 6)
+        dh(2, 1, 3)
+        scale(2, 1)
         dw(2, 7)
+        finish(1, whole_row)
+        store_dx(1, whole_row, nc.sync)
         dw(3, 7)
+        dot(2)
+        dh(3, 1, 0)
+        dh(3, 1, 1)
+        dh(3, 1, 2)
+        dh(3, 1, 3)
+        scale(3, 1)
+        finish(2, whole_row)
+        store_dx(2, whole_row, nc.sync)
+        dot(3)
         for halves, queue in ((first_half, nc.sync), (second_half, nc.scalar)):
             finish(3, halves)
             store_dx(3, halves, queue)

@@ -51,8 +51,8 @@ def tile_llamaselfattentionblock_pa_v_kernel(tc, x, g, wq, wk, rstd, grad_0, gra
         def codes(name, width):
             return kept(name + "_codes", [P, width], U32), kept(name + "_scales", [P, width], U8)
 
-        def bank(k, shape):
-            return psum.tile(shape, F32, name="bank%d" % k, tag="bank%d" % k, bufs=1)
+        def bank(k, shape, dtype=F32):
+            return psum.tile(shape, dtype, name="bank%d" % k, tag="bank%d" % k, bufs=1)
 
         dq_sb = [rotating("dq%d" % u, [P, UNIT_HEADS, SLOTS, HD], BF16, 1) for u in range(2)]
         dk_sb = rotating("dk", [P, HEADS, SLOTS, HD], BF16, 1)
@@ -76,19 +76,11 @@ def tile_llamaselfattentionblock_pa_v_kernel(tc, x, g, wq, wk, rstd, grad_0, gra
 
         ctx.enter_context(tc.manual_schedule())
 
-        def load_grad(dst, a, first_head, heads):
-            for b in range(2):
-                for batch, queue in ((b, nc.sync), (b + 2, nc.scalar)):
-                    queue.dma_start(out=dst[32 * batch : 32 * batch + 32].rearrange("q n j d -> q n (j d)"),
-                                    in_=grads[a][batch, first_head : first_head + heads].rearrange("n (q j) d -> q n (j d)", j=SLOTS))
-
-        def load_dk(queue, batches):
-            for batch in batches:
-                queue.dma_start(out=dk_sb[32 * batch : 32 * batch + 32].rearrange("q n j d -> q n (j d)"),
-                                in_=grad_1[batch].rearrange("n (q j) d -> q n (j d)", j=SLOTS))
-
-        def load_dk_scalar():
-            load_dk(nc.scalar, (2, 3))
+        def load_grad(u, queues):
+            for n in range(UNIT_HEADS):
+                head = (u % 2) * UNIT_HEADS + n
+                queues[n % len(queues)].dma_start(out=grad_sb[u][:, n].rearrange("p j d -> p (j d)"),
+                                                  in_=grads[u // 2][:, head].rearrange("b (q j) d -> q b (j d)", j=SLOTS))
 
         def load_x():
             nc.sync.dma_start(out=x_sb[:], in_=x_rows)
@@ -101,8 +93,11 @@ def tile_llamaselfattentionblock_pa_v_kernel(tc, x, g, wq, wk, rstd, grad_0, gra
         nc.gpsimd.dma_start(out=rstd_sb[:], in_=rstd.rearrange("b (q j) -> (b q) j", j=SLOTS))
         make_identity(nc, identity[:])
         nc.sync.dma_start(out=g_sb[:], in_=g.rearrange("(p c) -> p c", p=P))
-        for u in range(2):
-            load_grad(dq_sb[u], 0, u * UNIT_HEADS, UNIT_HEADS)
+        load_grad(0, (nc.sync,))
+        load_grad(1, (nc.sync,))
+
+        order = kept("order", [P, B, P // B], BF16)
+        nc.gpsimd.tensor_copy(out=order[:], in_=identity[:].rearrange("p (q b) -> p b q", b=B))
 
         positions = kept("positions", [P, SLOTS], I32)
         coarse = kept("coarse", [P, SLOTS, 4], F32)
@@ -139,17 +134,22 @@ def tile_llamaselfattentionblock_pa_v_kernel(tc, x, g, wq, wk, rstd, grad_0, gra
         for v in range(2):
             nc.scalar.activation(out=cosines[:, v].rearrange("p (k s) -> p k s", s=2), in_=angles[:, v].unsqueeze(2).to_broadcast([P, P, 2]),
                                  func=ACT.Sin, scale=2.0 * math.pi)
-        cosines_psum = bank(7, [P, 2, SLOTS * HD // 2])
-        for v in range(2):
-            nc.tensor.matmul(cosines_psum[:, v], lhsT=identity[:], rhs=cosines[:, v], start=True, stop=True)
         nc.scalar.copy(out=gain[:].bitcast(F32), in_=gain_psum)
+
+        grad_bank = {}
+
+        def place(u, v):
+            grad_bank[u, v] = bank((4 if u == 0 else 6) + v, [P, 2, UNIT], BF16)
+            pairs = grad_sb[u].rearrange("p (k n) j (w v s) -> p k (n j w) v s", k=2, v=2, s=2)
+            for k in range(2):
+                nc.tensor.matmul(grad_bank[u, v][:, k], lhsT=order[:].rearrange("p b q -> p (b q)"), rhs=pairs[:, k, :, v, :], start=True, stop=True)
 
         def rope(u, v):
             if v == 0:
                 dz[u] = rotating("dz", [P, SLOTS, 2, UNIT // 2], BF16, 4)
-            pairs = grad_sb[u].rearrange("p n j (w v s) -> p (n j w) v s", v=2, s=2)
-            nc.vector.tensor_tensor(out=dz[u][:, :, v, :].rearrange("p j (n c) -> p n j c", n=UNIT_HEADS), in0=pairs[:, :, v, :],
-                                    in1=(cosines if u == 0 else cosines_psum)[:, v, :].unsqueeze(1).to_broadcast([P, UNIT_HEADS, 2 * P]), op=ALU.mult)
+            nc.vector.tensor_tensor(out=dz[u][:, :, v, :].rearrange("p j (n c) -> p n j c", n=UNIT_HEADS),
+                                    in0=grad_bank[u, v][:].rearrange("p k c -> p (k c)"),
+                                    in1=cosines[:, v, :].unsqueeze(1).to_broadcast([P, UNIT_HEADS, 2 * P]), op=ALU.mult)
 
         def interleave(u, copy):
             dz_tok[u] = rotating("dz_tok", [P, UNIT, SLOTS], BF16, 3)
@@ -158,10 +158,14 @@ def tile_llamaselfattentionblock_pa_v_kernel(tc, x, g, wq, wk, rstd, grad_0, gra
         def on_gpsimd(out, in_):
             nc.gpsimd.tensor_scalar(out=out, in0=in_, scalar1=1.0, scalar2=1.0, op0=ALU.mult, op1=ALU.mult)
 
-        def interleave_gpsimd(u):
-            dz_tok[u] = rotating("dz_tok", [P, UNIT, SLOTS], BF16, 3)
-            for v in range(2):
+        def interleave_half(u, v, engine):
+            if u not in dz_tok:
+                dz_tok[u] = rotating("dz_tok", [P, UNIT, SLOTS], BF16, 3)
+            if engine == "gpsimd":
                 on_gpsimd(dz_tok[u][:].rearrange("p (m v s) j -> p v m s j", v=2, s=2)[:, v], dz[u][:, :, v].rearrange("p j c -> p c j"))
+            else:
+                copy = nc.vector.tensor_copy if engine == "vector" else nc.scalar.copy
+                copy(out=dz_tok[u][:].rearrange("p (m v s) j -> p v m j s", v=2, s=2)[:, v], in_=dz[u][:, :, v].rearrange("p j (m s) -> p m j s", s=2))
 
         def interleave_h_gpsimd(h):
             on_gpsimd(h_tok[h][:], h_flat[h][:].rearrange("p j c -> p c j"))
@@ -169,7 +173,7 @@ def tile_llamaselfattentionblock_pa_v_kernel(tc, x, g, wq, wk, rstd, grad_0, gra
         def norm(h, j):
             cols = slice(h * HALF, (h + 1) * HALF)
             nc.vector.scalar_tensor_tensor(h_flat[h][:, j], x_sb[:, j, cols], rstd_sb[:, j : j + 1],
-                                           (gain_psum.bitcast(BF16) if (h, j) < (1, 2) else gain)[:, cols], ALU.mult, ALU.mult)
+                                           gain_psum.bitcast(BF16)[:, cols], ALU.mult, ALU.mult)
 
         def interleave_h(h, copy):
             copy(out=h_tok[h][:].rearrange("p (c i) j -> p c j i", i=4), in_=h_flat[h][:].rearrange("p j (c i) -> p c j i", i=4))
@@ -208,7 +212,7 @@ def tile_llamaselfattentionblock_pa_v_kernel(tc, x, g, wq, wk, rstd, grad_0, gra
         def store_dx(j, halves, queue):
             queue.dma_start(out=out_rows[:, j, halves], in_=scaled[j][:, halves])
 
-        stream = list(range(1, 7))
+        stream = list(range(1, 6))
 
         def stream_bank(shape):
             k = stream.pop(0)
@@ -216,7 +220,7 @@ def tile_llamaselfattentionblock_pa_v_kernel(tc, x, g, wq, wk, rstd, grad_0, gra
             return bank(k, shape)
 
         def narrow_stream():
-            for k in range(4, 7):
+            for k in range(4, 6):
                 stream.remove(k)
             stream.append(0)
 
@@ -298,78 +302,89 @@ def tile_llamaselfattentionblock_pa_v_kernel(tc, x, g, wq, wk, rstd, grad_0, gra
         load_x()
         load_w(1, 0, nc.sync)
         load_w(0, 1, nc.sync)
-        load_dk(nc.sync, (0, 1))
+        load_grad(2, (nc.sync,))
         load_w(1, 1, nc.sync)
+        load_grad(3, (nc.sync,))
+        place(0, 0)
         rope(0, 0)
+        place(0, 1)
         rope(0, 1)
-        turn_dz(0)
-        interleave_gpsimd(0)
-        turn_w(0, 0)
+        place(1, 0)
+        interleave_half(0, 1, "gpsimd")
+        place(1, 1)
         rope(1, 0)
+        interleave_half(0, 0, "scalar")
+        interleave_half(1, 0, "gpsimd")
+        turn_w(0, 0)
         rope(1, 1)
-        turn_dz(1)
-        interleave_gpsimd(1)
+        turn_dz(0)
+        interleave_half(1, 1, "gpsimd")
         turn_w(1, 0)
         norm(0, 0)
-        turn_w(2, 0)
+        turn_dz(1)
         norm(0, 1)
-        turn_w(3, 0)
+        turn_w(2, 0)
         norm(0, 2)
-        load_dk_scalar()
+        turn_w(3, 0)
         norm(0, 3)
         turn_w(0, 1)
+        interleave_h_gpsimd(0)
         norm(1, 0)
-        interleave_h(0, on_vector)
         norm(1, 1)
+        norm(1, 2)
+        norm(1, 3)
         narrow_stream()
         quantize_dz_tok(0)
-        quantize_h(0)
-        dw(0, 0)
-        quantize_dz_tok(1)
-        dw(1, 0)
-        quantize_dz_feat(0)
-        dw(0, 1)
-        quantize_w(0, 0)
-        dw(1, 1)
-        quantize_dz_feat(1)
         turn_w(1, 1)
-        norm(1, 2)
-        dw(0, 2)
-        norm(1, 3)
-        dh(0, 0, 0)
-        interleave_h_gpsimd(1)
-        dw(1, 2)
-        rope(2, 0)
-        rope(2, 1)
-        dh(1, 0, 0)
-        interleave_gpsimd(2)
+        interleave_h(1, on_vector)
+        place(2, 0)
+        quantize_dz_tok(1)
+        place(2, 1)
+        quantize_h(0)
         turn_w(2, 1)
-        rope(3, 0)
-        rope(3, 1)
-        dw(0, 3)
-        quantize_w(1, 0)
-        dh(2, 0, 0)
+        quantize_dz_feat(0)
+        dw(0, 0)
         quantize_h(1)
-        dw(1, 3)
-        interleave(3, on_vector)
-        dh(0, 0, 1)
+        dw(1, 0)
+        quantize_w(0, 0)
         turn_w(3, 1)
-        dh(1, 0, 1)
-        dh(2, 0, 1)
+        quantize_dz_feat(1)
+        dw(0, 1)
+        rope(2, 0)
+        dw(1, 1)
+        interleave_half(2, 0, "gpsimd")
+        dw(0, 2)
+        rope(2, 1)
+        dh(0, 0, 0)
+        interleave_half(2, 1, "gpsimd")
+        place(3, 0)
+        rope(3, 0)
+        dw(1, 2)
+        dh(1, 0, 0)
+        dw(0, 3)
+        place(3, 1)
+        rope(3, 1)
+        dw(1, 3)
+        quantize_w(1, 0)
+        dh(0, 0, 1)
+        interleave(3, on_vector)
         turn_dz(2)
         quantize_dz_feat(2)
-        dh(3, 0, 0)
+        dh(1, 0, 1)
         quantize_dz_tok(2)
-        dh(3, 0, 1)
+        dw(0, 4)
+        dw(1, 4)
         turn_dz(3)
         quantize_dz_feat(3)
-        dw(0, 4)
+        dh(2, 0, 0)
         quantize_dz_tok(3)
-        dw(1, 4)
+        dh(2, 0, 1)
         quantize_w(0, 1)
         dw(0, 5)
         nc.vector.scalar_tensor_tensor(neg_r2[:], rstd_sb[:], -1.0 / E, rstd_sb[:], ALU.mult, ALU.mult)
+        dh(3, 0, 0)
         dw(1, 5)
+        dh(3, 0, 1)
         dh(0, 0, 2)
         dw(0, 6)
         dh(1, 0, 2)

@@ -63,9 +63,9 @@ def tile_llamaselfattentionblock_pa_v_kernel(tc, x, g, wq, wk, rstd, grad_0, gra
         x_sb = kept("x_sb", [P, SLOTS, E], BF16)
         x_halves = x_sb[:].rearrange("p j (h c) -> p j h c", h=2)
         gain = kept("gain", [P, E], BF16)
-        h_flat = [kept("h_flat%d" % h, [P, SLOTS, HALF], BF16) for h in range(2)]
+        h_flat = [rotating("h_flat%d" % h, [P, SLOTS, HALF], BF16, 1) for h in range(2)]
         w_sb = [[rotating("w%d%d" % (a, h), [P, 4, J], BF16, 1) for h in range(2)] for a in range(2)]
-        h_tok = [kept("h_tok%d" % h, [P, HALF, SLOTS], BF16) for h in range(2)]
+        h_tok = [rotating("h_tok%d" % h, [P, HALF, SLOTS], BF16, 1) for h in range(2)]
         h_q = [codes("h_q%d" % h, HALF) for h in range(2)]
         dz_tok_q = [codes("dz_tok_q%d" % u, UNIT) for u in range(UNITS)]
         dz_feat_q = [codes("dz_feat_q%d" % u, T) for u in range(UNITS)]
@@ -81,6 +81,11 @@ def tile_llamaselfattentionblock_pa_v_kernel(tc, x, g, wq, wk, rstd, grad_0, gra
                 head = (u % 2) * UNIT_HEADS + n
                 queues[n % len(queues)].dma_start(out=grad_sb[u][:, n].rearrange("p j d -> p (j d)"),
                                                   in_=grads[u // 2][:, head].rearrange("b (q j) d -> q b (j d)", j=SLOTS))
+
+        def load_dk(queue, batches):
+            for batch in batches:
+                queue.dma_start(out=dk_sb[32 * batch : 32 * batch + 32].rearrange("q n j d -> q n (j d)"),
+                                in_=grad_1[batch].rearrange("n (q j) d -> q n (j d)", j=SLOTS))
 
         def load_x():
             nc.sync.dma_start(out=x_sb[:], in_=x_rows)
@@ -139,17 +144,25 @@ def tile_llamaselfattentionblock_pa_v_kernel(tc, x, g, wq, wk, rstd, grad_0, gra
         grad_bank = {}
 
         def place(u, v):
-            grad_bank[u, v] = bank((4 if u == 0 else 6) + v, [P, 2, UNIT], BF16)
+            grad_bank[u, v] = bank(((4, 5), (6, 3))[u][v], [P, 2, UNIT], BF16)
             pairs = grad_sb[u].rearrange("p (k n) j (w v s) -> p k (n j w) v s", k=2, v=2, s=2)
             for k in range(2):
                 nc.tensor.matmul(grad_bank[u, v][:, k], lhsT=order[:].rearrange("p b q -> p (b q)"), rhs=pairs[:, k, :, v, :], start=True, stop=True)
 
+        cosine_bank = {}
+
+        def place_cosines():
+            cosine_bank[0] = bank(7, [P, 2, SLOTS * HD // 2])
+            for v in range(2):
+                nc.tensor.matmul(cosine_bank[0][:, v], lhsT=identity[:], rhs=cosines[:, v], start=True, stop=True)
+
         def rope(u, v):
-            if v == 0:
+            if u not in dz:
                 dz[u] = rotating("dz", [P, SLOTS, 2, UNIT // 2], BF16, 4)
             nc.vector.tensor_tensor(out=dz[u][:, :, v, :].rearrange("p j (n c) -> p n j c", n=UNIT_HEADS),
-                                    in0=grad_bank[u, v][:].rearrange("p k c -> p (k c)"),
-                                    in1=cosines[:, v, :].unsqueeze(1).to_broadcast([P, UNIT_HEADS, 2 * P]), op=ALU.mult)
+                                    in0=grad_bank[u, v][:].rearrange("p k c -> p (k c)") if u < 2 else
+                                    grad_sb[u].rearrange("p n j (w v s) -> p (n j w) v s", v=2, s=2)[:, :, v, :],
+                                    in1=(cosines if u < 2 else cosine_bank[0])[:, v, :].unsqueeze(1).to_broadcast([P, UNIT_HEADS, 2 * P]), op=ALU.mult)
 
         def interleave(u, copy):
             dz_tok[u] = rotating("dz_tok", [P, UNIT, SLOTS], BF16, 3)
@@ -194,11 +207,8 @@ def tile_llamaselfattentionblock_pa_v_kernel(tc, x, g, wq, wk, rstd, grad_0, gra
             quantize(w_q[a][h], E4M3, w_feat[a, h][:].rearrange("p u c -> p (u c)"))
 
         def scale(j, h):
-            if h == 0 and j < 2:
-                scaled[j] = rotating("dq%d" % j, [P, 2, HALF], F32, 1)[:]
-            if h == 0 and j == 2:
-                both = rotating("dk", [P, 2, 2, HALF], F32, 1)
-                scaled[2], scaled[3] = both[:, 0], both[:, 1]
+            if h == 0:
+                scaled[j] = rotating(("h_flat%d", "h_tok%d")[j // 2] % (j % 2), [P, 2, HALF], F32, 1)[:]
             nc.vector.scalar_tensor_tensor(scaled[j][:, h], dh_bank[j, h][:], rstd_sb[:, j : j + 1], gain[:, h * HALF : (h + 1) * HALF], ALU.mult, ALU.mult)
 
         def dot(j):
@@ -212,7 +222,7 @@ def tile_llamaselfattentionblock_pa_v_kernel(tc, x, g, wq, wk, rstd, grad_0, gra
         def store_dx(j, halves, queue):
             queue.dma_start(out=out_rows[:, j, halves], in_=scaled[j][:, halves])
 
-        stream = list(range(1, 6))
+        stream = [1, 2, 4, 5, 3]
 
         def stream_bank(shape):
             k = stream.pop(0)
@@ -302,16 +312,17 @@ def tile_llamaselfattentionblock_pa_v_kernel(tc, x, g, wq, wk, rstd, grad_0, gra
         load_x()
         load_w(1, 0, nc.sync)
         load_w(0, 1, nc.sync)
-        load_grad(2, (nc.sync,))
         load_w(1, 1, nc.sync)
-        load_grad(3, (nc.sync,))
+        load_dk(nc.sync, (0, 2, 1, 3))
         place(0, 0)
-        rope(0, 0)
+        nc.vector.scalar_tensor_tensor(neg_r2[:], rstd_sb[:], -1.0 / E, rstd_sb[:], ALU.mult, ALU.mult)
         place(0, 1)
-        rope(0, 1)
+        rope(0, 0)
         place(1, 0)
-        interleave_half(0, 1, "gpsimd")
+        rope(0, 1)
         place(1, 1)
+        interleave_half(0, 1, "gpsimd")
+        place_cosines()
         rope(1, 0)
         interleave_half(0, 0, "scalar")
         interleave_half(1, 0, "gpsimd")
@@ -337,77 +348,72 @@ def tile_llamaselfattentionblock_pa_v_kernel(tc, x, g, wq, wk, rstd, grad_0, gra
         quantize_dz_tok(0)
         turn_w(1, 1)
         interleave_h(1, on_vector)
-        place(2, 0)
-        quantize_dz_tok(1)
-        place(2, 1)
-        quantize_h(0)
         turn_w(2, 1)
-        quantize_dz_feat(0)
-        dw(0, 0)
-        quantize_h(1)
-        dw(1, 0)
-        quantize_w(0, 0)
+        quantize_dz_tok(1)
         turn_w(3, 1)
-        quantize_dz_feat(1)
+        quantize_h(0)
+        dw(0, 0)
+        quantize_dz_feat(0)
+        dw(1, 0)
+        quantize_h(1)
         dw(0, 1)
-        rope(2, 0)
+        quantize_w(0, 0)
         dw(1, 1)
-        interleave_half(2, 0, "gpsimd")
+        quantize_dz_feat(1)
         dw(0, 2)
+        rope(2, 0)
+        dw(1, 2)
+        interleave_half(2, 0, "gpsimd")
+        dw(0, 3)
         rope(2, 1)
         dh(0, 0, 0)
         interleave_half(2, 1, "gpsimd")
-        place(3, 0)
-        rope(3, 0)
-        dw(1, 2)
-        dh(1, 0, 0)
-        dw(0, 3)
-        place(3, 1)
-        rope(3, 1)
         dw(1, 3)
-        quantize_w(1, 0)
-        dh(0, 0, 1)
-        interleave(3, on_vector)
+        rope(3, 0)
+        dh(1, 0, 0)
+        rope(3, 1)
         turn_dz(2)
-        quantize_dz_feat(2)
-        dh(1, 0, 1)
-        quantize_dz_tok(2)
+        quantize_w(1, 0)
         dw(0, 4)
+        interleave(3, on_vector)
+        dh(2, 0, 0)
+        quantize_dz_feat(2)
         dw(1, 4)
+        quantize_dz_tok(2)
+        dh(0, 0, 1)
         turn_dz(3)
         quantize_dz_feat(3)
-        dh(2, 0, 0)
-        quantize_dz_tok(3)
-        dh(2, 0, 1)
-        quantize_w(0, 1)
         dw(0, 5)
-        nc.vector.scalar_tensor_tensor(neg_r2[:], rstd_sb[:], -1.0 / E, rstd_sb[:], ALU.mult, ALU.mult)
-        dh(3, 0, 0)
+        quantize_dz_tok(3)
+        dh(1, 0, 1)
+        quantize_w(0, 1)
         dw(1, 5)
-        dh(3, 0, 1)
-        dh(0, 0, 2)
+        dh(2, 0, 1)
         dw(0, 6)
-        dh(1, 0, 2)
+        dh(3, 0, 0)
         dw(1, 6)
+        dh(3, 0, 1)
+        dw(0, 7)
+        dh(0, 0, 2)
+        dw(1, 7)
+        dh(1, 0, 2)
         dh(0, 0, 3)
         scale(0, 0)
-        dw(0, 7)
         dh(1, 0, 3)
         scale(1, 0)
-        dw(1, 7)
+        dw(2, 0)
         quantize_w(1, 1)
         dh(2, 0, 2)
-        dw(2, 0)
+        dw(3, 0)
         dh(2, 0, 3)
         scale(2, 0)
-        dw(3, 0)
         dh(3, 0, 2)
         dh(3, 0, 3)
         scale(3, 0)
-        dh(0, 1, 0)
         dw(2, 1)
-        dh(0, 1, 1)
+        dh(0, 1, 0)
         dw(3, 1)
+        dh(0, 1, 1)
         dh(0, 1, 2)
         dh(0, 1, 3)
         scale(0, 1)

@@ -24,14 +24,13 @@ HALF = 512
 UNITS = 2 * J // UNIT
 UNIT_HEADS = UNIT // HD
 ROW_TILES = E // P
-DH_BANKS = 4
-STREAM_BANKS = 4
+H_ON_GPSIMD = 256
+GAIN_BANK, DH_BANK, COSINE_BANK = 0, 4, 7
 FLOPS = 2 * 2 * T * E * 2 * J
 
 
 def tile_llamaselfattentionblock_pa_v_kernel(tc, x, g, wq, wk, rstd, grad_0, grad_1, out_0, out_1, out_2):
     nc = tc.nc
-    grads = (grad_0, grad_1)
     weights = (wq, wk)
     weight_grads = (out_1, out_2)
     x_rows = x.flatten_outer_dims().rearrange("(p j) e -> p j e", j=SLOTS)
@@ -54,9 +53,8 @@ def tile_llamaselfattentionblock_pa_v_kernel(tc, x, g, wq, wk, rstd, grad_0, gra
         def bank(k, shape, dtype=F32):
             return psum.tile(shape, dtype, name="bank%d" % k, tag="bank%d" % k, bufs=1)
 
-        dq_sb = [rotating("dq%d" % u, [P, UNIT_HEADS, SLOTS, HD], BF16, 1) for u in range(2)]
-        dk_sb = rotating("dk", [P, HEADS, SLOTS, HD], BF16, 1)
-        grad_sb = [dq_sb[0][:], dq_sb[1][:], dk_sb[:, 0:UNIT_HEADS], dk_sb[:, UNIT_HEADS:HEADS]]
+        dq_sb = [kept("dq%d" % u, [P, UNIT_HEADS, SLOTS, HD], BF16) for u in range(2)]
+        dk_sb = kept("dk", [P, HEADS, SLOTS, HD], BF16)
         rstd_sb = kept("rstd_sb", [P, SLOTS], F32)
         g_sb = kept("g_sb", [P, E // P], BF16)
         identity = kept("identity", [P, P], F32)
@@ -67,39 +65,37 @@ def tile_llamaselfattentionblock_pa_v_kernel(tc, x, g, wq, wk, rstd, grad_0, gra
         w_sb = [[rotating("w%d%d" % (a, h), [P, 4, J], BF16, 1) for h in range(2)] for a in range(2)]
         h_tok = [rotating("h_tok%d" % h, [P, HALF, SLOTS], BF16, 1) for h in range(2)]
         h_q = [codes("h_q%d" % h, HALF) for h in range(2)]
-        dz_tok_q = [codes("dz_tok_q%d" % u, UNIT) for u in range(UNITS)]
-        dz_feat_q = [codes("dz_feat_q%d" % u, T) for u in range(UNITS)]
+        dz_tok_q = [codes("dz_tok_q%d" % a, 2 * UNIT) for a in range(2)]
+        dz_feat_q = [codes("dz_feat_q%d" % a, 2 * T) for a in range(2)]
         w_q = [[codes("w_q%d%d" % (a, h), 2 * HALF) for h in range(2)] for a in range(2)]
         neg_r2 = kept("neg_r2", [P, SLOTS], F32)
         coef = [kept("coef%d" % j, [P, 1], F32) for j in range(SLOTS)]
-        dz, dz_tok, dz_feat, w_feat, dh_bank, dw_rows, scaled = {}, {}, {}, {}, {}, {}, {}
+        dz_tok = [kept("dz_tok%d" % a, [P, 2, UNIT, SLOTS], BF16) for a in range(2)]
+        dz_feat = [kept("dz_feat%d" % a, [P, 2, 4 * T], BF16) for a in range(2)]
+        dz, dq_bank, w_feat, dh_bank, dw_rows, scaled = {}, {}, {}, {}, {}, {}
 
         ctx.enter_context(tc.manual_schedule())
-
-        def load_grad(u, queues):
-            for n in range(UNIT_HEADS):
-                head = (u % 2) * UNIT_HEADS + n
-                queues[n % len(queues)].dma_start(out=grad_sb[u][:, n].rearrange("p j d -> p (j d)"),
-                                                  in_=grads[u // 2][:, head].rearrange("b (q j) d -> q b (j d)", j=SLOTS))
-
-        def load_dk(queue, batches):
-            for batch in batches:
-                queue.dma_start(out=dk_sb[32 * batch : 32 * batch + 32].rearrange("q n j d -> q n (j d)"),
-                                in_=grad_1[batch].rearrange("n (q j) d -> q n (j d)", j=SLOTS))
-
-        def load_x():
-            nc.sync.dma_start(out=x_sb[:], in_=x_rows)
-
-        def load_w(a, h, queue):
-            queue.dma_start(out=w_sb[a][h][:], in_=weights[a][h * HALF : (h + 1) * HALF, :].rearrange("(q i) f -> q i f", i=4))
 
         tokens = kept("tokens", [P, SLOTS], I32)
         nc.gpsimd.iota(tokens[:], pattern=[[1, SLOTS]], base=0, channel_multiplier=SLOTS)
         nc.gpsimd.dma_start(out=rstd_sb[:], in_=rstd.rearrange("b (q j) -> (b q) j", j=SLOTS))
         make_identity(nc, identity[:])
         nc.sync.dma_start(out=g_sb[:], in_=g.rearrange("(p c) -> p c", p=P))
-        load_grad(0, (nc.sync,))
-        load_grad(1, (nc.sync,))
+        for head in range(HEADS):
+            nc.sync.dma_start(out=dq_sb[head // UNIT_HEADS][:, head % UNIT_HEADS].rearrange("p j d -> p (j d)"),
+                              in_=grad_0[:, head].rearrange("b (q j) d -> q b (j d)", j=SLOTS))
+
+        def load_w(a, h):
+            nc.sync.dma_start(out=w_sb[a][h][:], in_=weights[a][h * HALF : (h + 1) * HALF, :].rearrange("(q i) f -> q i f", i=4))
+
+        load_w(0, 0)
+        nc.sync.dma_start(out=x_sb[:], in_=x_rows)
+        load_w(1, 0)
+        load_w(0, 1)
+        load_w(1, 1)
+        for batch in (0, 2, 1, 3):
+            nc.sync.dma_start(out=dk_sb[32 * batch : 32 * batch + 32].rearrange("q n j d -> q n (j d)"),
+                              in_=grad_1[batch].rearrange("n (q j) d -> q n (j d)", j=SLOTS))
 
         order = kept("order", [P, B, P // B], BF16)
         nc.gpsimd.tensor_copy(out=order[:], in_=identity[:].rearrange("p (q b) -> p b q", b=B))
@@ -107,9 +103,9 @@ def tile_llamaselfattentionblock_pa_v_kernel(tc, x, g, wq, wk, rstd, grad_0, gra
         positions = kept("positions", [P, SLOTS], I32)
         coarse = kept("coarse", [P, SLOTS, 4], F32)
         fine = kept("fine", [P, 16], F32)
-        turns = kept("turns", [P, SLOTS, HD // 2], F32)
-        whole = kept("whole", [P, SLOTS, HD // 2], I32)
-        fraction = kept("fraction", [P, SLOTS, HD // 2], F32)
+        turns = kept("turns", [P, 2, SLOTS * HD // 4], F32)
+        whole = kept("whole", [P, 2, SLOTS * HD // 4], I32)
+        fraction = kept("fraction", [P, 2, SLOTS * HD // 4], F32)
         cosines = kept("cosines", [P, 2, SLOTS * HD // 2], F32)
         nc.vector.memset(fine[:, 0:1], 1.0)
         nc.vector.tensor_single_scalar(positions[:], tokens[:], L - 1, ALU.bitwise_and)
@@ -119,89 +115,83 @@ def tile_llamaselfattentionblock_pa_v_kernel(tc, x, g, wq, wk, rstd, grad_0, gra
             nc.vector.tensor_single_scalar(coarse[:, :, k], positions[:], 10000.0 ** (-k / 4.0) * 0.5 / math.pi, ALU.mult)
         for k in range(1, 4):
             nc.vector.tensor_single_scalar(fine[:, 4 * k : 4 * k + 4], fine[:, 0:4], 10000.0 ** (-k / 16.0), ALU.mult)
-        slot_pairs = [slice(0, 2), slice(2, 4)]
-        for js in slot_pairs:
-            nc.vector.tensor_tensor(turns[:, js].rearrange("p j (a b) -> p (j a) b", b=16),
-                                    coarse[:, js].rearrange("p j a -> p (j a)").unsqueeze(2).to_broadcast([P, 8, 16]),
-                                    fine[:].unsqueeze(1).to_broadcast([P, 8, 16]), ALU.mult)
-        for js in slot_pairs:
-            nc.vector.tensor_single_scalar(whole[:, js], turns[:, js], 0.25, ALU.add)
-        for js in slot_pairs:
-            nc.vector.scalar_tensor_tensor(fraction[:, js].rearrange("p j i -> p (j i)"), turns[:, js].rearrange("p j i -> p (j i)"), 0.25,
-                                           whole[:, js].rearrange("p j i -> p (j i)"), ALU.add, ALU.subtract)
+        for v in range(2):
+            nc.vector.tensor_tensor(turns[:, v].rearrange("p (k b) -> p k b", b=8),
+                                    coarse[:].rearrange("p j a -> p (j a)").unsqueeze(2).to_broadcast([P, 16, 8]),
+                                    fine[:, v:16:2].unsqueeze(1).to_broadcast([P, 16, 8]), ALU.mult)
+        for v in range(2):
+            nc.vector.tensor_single_scalar(whole[:, v], turns[:, v], 0.25, ALU.add)
+        for v in range(2):
+            nc.vector.scalar_tensor_tensor(fraction[:, v], turns[:, v], 0.25, whole[:, v], ALU.add, ALU.subtract)
 
-        gain_words = bank(0, [P, P, 4])
+        gain_words = bank(GAIN_BANK, [P, P, 4])
         for k in range(4):
             nc.tensor.transpose(gain_words[:, :, k], g_sb[:].bitcast(F32)[:, k : k + 1].to_broadcast([P, P]), identity[:])
         gain_psum = gain_words[:].rearrange("p q k -> p (q k)")
 
-        angles = fraction[:].rearrange("p j (w v) -> p v (j w)", v=2)
         for v in range(2):
-            nc.scalar.activation(out=cosines[:, v].rearrange("p (k s) -> p k s", s=2), in_=angles[:, v].unsqueeze(2).to_broadcast([P, P, 2]),
+            nc.scalar.activation(out=cosines[:, v].rearrange("p (k s) -> p k s", s=2), in_=fraction[:, v].unsqueeze(2).to_broadcast([P, P, 2]),
                                  func=ACT.Sin, scale=2.0 * math.pi)
         nc.scalar.copy(out=gain[:].bitcast(F32), in_=gain_psum)
 
-        grad_bank = {}
-
-        def place(u, v):
-            grad_bank[u, v] = bank(((4, 5), (6, 3))[u][v], [P, 2, UNIT], BF16)
-            pairs = grad_sb[u].rearrange("p (k n) j (w v s) -> p k (n j w) v s", k=2, v=2, s=2)
+        def place_dq(u, v):
+            dq_bank[u, v] = bank(((4, 5), (6, 3))[u][v], [P, 2, UNIT], BF16)
+            pairs = dq_sb[u][:].rearrange("p (k n) j (w v s) -> p k (n j w) v s", k=2, v=2, s=2)
             for k in range(2):
-                nc.tensor.matmul(grad_bank[u, v][:, k], lhsT=order[:].rearrange("p b q -> p (b q)"), rhs=pairs[:, k, :, v, :], start=True, stop=True)
-
-        cosine_bank = {}
+                nc.tensor.matmul(dq_bank[u, v][:, k], lhsT=order[:].rearrange("p b q -> p (b q)"), rhs=pairs[:, k, :, v, :], start=True, stop=True)
 
         def place_cosines():
-            cosine_bank[0] = bank(7, [P, 2, SLOTS * HD // 2])
+            ps = bank(COSINE_BANK, [P, 2, SLOTS * HD // 2])
             for v in range(2):
-                nc.tensor.matmul(cosine_bank[0][:, v], lhsT=identity[:], rhs=cosines[:, v], start=True, stop=True)
+                nc.tensor.matmul(ps[:, v], lhsT=identity[:], rhs=cosines[:, v], start=True, stop=True)
+            return ps
 
-        def rope(u, v):
-            if u not in dz:
+        def rope(u, v, grad, cos):
+            if v == 0:
                 dz[u] = rotating("dz", [P, SLOTS, 2, UNIT // 2], BF16, 4)
-            nc.vector.tensor_tensor(out=dz[u][:, :, v, :].rearrange("p j (n c) -> p n j c", n=UNIT_HEADS),
-                                    in0=grad_bank[u, v][:].rearrange("p k c -> p (k c)") if u < 2 else
-                                    grad_sb[u].rearrange("p n j (w v s) -> p (n j w) v s", v=2, s=2)[:, :, v, :],
-                                    in1=(cosines if u < 2 else cosine_bank[0])[:, v, :].unsqueeze(1).to_broadcast([P, UNIT_HEADS, 2 * P]), op=ALU.mult)
+            nc.vector.tensor_tensor(out=dz[u][:, :, v, :].rearrange("p j (n c) -> p n j c", n=UNIT_HEADS), in0=grad,
+                                    in1=cos[:, v, :].unsqueeze(1).to_broadcast([P, UNIT_HEADS, 2 * P]), op=ALU.mult)
 
-        def interleave(u, copy):
-            dz_tok[u] = rotating("dz_tok", [P, UNIT, SLOTS], BF16, 3)
-            copy(out=dz_tok[u][:].rearrange("p (m v s) j -> p v m j s", v=2, s=2), in_=dz[u][:].rearrange("p j v (m s) -> p v m j s", s=2))
+        def rope_dq(u, v):
+            rope(u, v, dq_bank[u, v][:].rearrange("p k c -> p (k c)"), cosines)
 
-        def on_gpsimd(out, in_):
+        def rope_dk(u, v, cos):
+            heads = dk_sb[:, (u - 2) * UNIT_HEADS : (u - 1) * UNIT_HEADS]
+            rope(u, v, heads.rearrange("p n j (w v s) -> p (n j w) v s", v=2, s=2)[:, :, v, :], cos)
+
+        def gpsimd_copy(out, in_):
             nc.gpsimd.tensor_scalar(out=out, in0=in_, scalar1=1.0, scalar2=1.0, op0=ALU.mult, op1=ALU.mult)
 
-        def interleave_half(u, v, engine):
-            if u not in dz_tok:
-                dz_tok[u] = rotating("dz_tok", [P, UNIT, SLOTS], BF16, 3)
-            if engine == "gpsimd":
-                on_gpsimd(dz_tok[u][:].rearrange("p (m v s) j -> p v m s j", v=2, s=2)[:, v], dz[u][:, :, v].rearrange("p j c -> p c j"))
-            else:
-                copy = nc.vector.tensor_copy if engine == "vector" else nc.scalar.copy
-                copy(out=dz_tok[u][:].rearrange("p (m v s) j -> p v m j s", v=2, s=2)[:, v], in_=dz[u][:, :, v].rearrange("p j (m s) -> p m j s", s=2))
+        def interleave_on_gpsimd(u, v):
+            gpsimd_copy(dz_tok[u // 2][:, u % 2].rearrange("p (m v s) j -> p v m s j", v=2, s=2)[:, v], dz[u][:, :, v].rearrange("p j c -> p c j"))
 
-        def interleave_h_gpsimd(h):
-            on_gpsimd(h_tok[h][:], h_flat[h][:].rearrange("p j c -> p c j"))
+        def interleave_on_vector(u):
+            nc.vector.tensor_copy(out=dz_tok[u // 2][:, u % 2].rearrange("p (m v s) j -> p v m j s", v=2, s=2),
+                                  in_=dz[u][:].rearrange("p j v (m s) -> p v m j s", s=2))
+
+        def interleave_h_on_gpsimd(h, cols):
+            gpsimd_copy(h_tok[h][:, cols], h_flat[h][:, :, cols].rearrange("p j c -> p c j"))
+
+        def interleave_h_on_vector(h, cols):
+            nc.vector.tensor_copy(out=h_tok[h][:, cols].rearrange("p (c i) j -> p c j i", i=4),
+                                  in_=h_flat[h][:, :, cols].rearrange("p j (c i) -> p c j i", i=4))
 
         def norm(h, j):
             cols = slice(h * HALF, (h + 1) * HALF)
             nc.vector.scalar_tensor_tensor(h_flat[h][:, j], x_sb[:, j, cols], rstd_sb[:, j : j + 1],
                                            gain_psum.bitcast(BF16)[:, cols], ALU.mult, ALU.mult)
 
-        def interleave_h(h, copy):
-            copy(out=h_tok[h][:].rearrange("p (c i) j -> p c j i", i=4), in_=h_flat[h][:].rearrange("p j (c i) -> p c j i", i=4))
-
         def quantize(pair, dtype, values):
             nc.vector.quantize_mx(out=pair[0][:].bitcast(dtype), scales=pair[1][:], in_=values)
 
-        def quantize_dz_tok(u):
-            quantize(dz_tok_q[u], E5M2, dz_tok[u][:].rearrange("p c j -> p (c j)"))
+        def quantize_dz_tok(a):
+            quantize(dz_tok_q[a], E5M2, dz_tok[a][:].rearrange("p u c j -> p (u c j)"))
 
         def quantize_h(h):
             quantize(h_q[h], E4M3, h_tok[h][:].rearrange("p c j -> p (c j)"))
 
-        def quantize_dz_feat(u):
-            quantize(dz_feat_q[u], E5M2, dz_feat[u][:])
+        def quantize_dz_feat(a):
+            quantize(dz_feat_q[a], E5M2, dz_feat[a][:].rearrange("p u c -> p (u c)"))
 
         def quantize_w(a, h):
             quantize(w_q[a][h], E4M3, w_feat[a, h][:].rearrange("p u c -> p (u c)"))
@@ -230,19 +220,18 @@ def tile_llamaselfattentionblock_pa_v_kernel(tc, x, g, wq, wk, rstd, grad_0, gra
             return bank(k, shape)
 
         def narrow_stream():
-            for k in range(4, 6):
-                stream.remove(k)
-            stream.append(0)
+            stream.remove(4)
+            stream.remove(5)
+            stream.append(GAIN_BANK)
 
         def turn_dz(u):
-            dz_feat[u] = rotating("dz_feat", [P, 4 * T], BF16, UNITS)
             words = dz[u][:].rearrange("p j v c -> p (j v c)").bitcast(F32)
             for jp in range(2):
                 ps = stream_bank([P, 4, P])
                 for k in range(4):
                     first = (4 * jp + k) * P
                     nc.tensor.transpose(ps[:, k, :], words[:, first : first + P], identity[:])
-                rows = dz_feat[u][:].bitcast(F32)[:, jp * 4 * P : (jp + 1) * 4 * P]
+                rows = dz_feat[u // 2][:, u % 2].bitcast(F32)[:, jp * 4 * P : (jp + 1) * 4 * P]
                 nc.scalar.copy(out=rows.rearrange("p (j q v) -> p j q v", j=2, v=2), in_=ps[:].rearrange("p (j v) q -> p j q v", v=2))
 
         def turn_w(u, h):
@@ -266,10 +255,11 @@ def tile_llamaselfattentionblock_pa_v_kernel(tc, x, g, wq, wk, rstd, grad_0, gra
         def dw(u, r):
             ps = stream_bank([P, UNIT])
             lhs, lhs_scale = h_q[r // 4]
-            rhs, rhs_scale = dz_tok_q[u]
+            rhs, rhs_scale = dz_tok_q[u // 2]
             cols = slice((r % 4) * P, (r % 4 + 1) * P)
+            f_cols = slice((u % 2) * UNIT, (u % 2 + 1) * UNIT)
             nc.tensor.matmul_mx(out=ps[:], lhsT=lhs[:, cols].bitcast(E4M3), lhsT_scale=lhs_scale[:, cols],
-                                rhs=rhs[:].bitcast(E5M2), rhs_scale=rhs_scale[:], start=True, stop=True)
+                                rhs=rhs[:, f_cols].bitcast(E5M2), rhs_scale=rhs_scale[:, f_cols], start=True, stop=True)
             if u == 0:
                 dw_rows[0, r] = rotating("dw_rows", [P, J], F32, ROW_TILES)[:]
             if u == 2 and r % 2 == 0:
@@ -289,17 +279,87 @@ def tile_llamaselfattentionblock_pa_v_kernel(tc, x, g, wq, wk, rstd, grad_0, gra
 
         def dh(j, h, u):
             if u == 0:
-                dh_bank[j, h] = bank(4 + j, [P, HALF])
-            cols = slice(j * P, (j + 1) * P)
-            lhs, lhs_scale = dz_feat_q[u]
+                dh_bank[j, h] = bank(DH_BANK + j, [P, HALF])
+            cols = slice((u % 2) * T + j * P, (u % 2) * T + (j + 1) * P)
+            lhs, lhs_scale = dz_feat_q[u // 2]
             rhs, rhs_scale = w_q[u // 2][h]
             e_cols = slice((u % 2) * HALF, (u % 2 + 1) * HALF)
             nc.tensor.matmul_mx(out=dh_bank[j, h][:], lhsT=lhs[:, cols].bitcast(E5M2), lhsT_scale=lhs_scale[:, cols],
                                 rhs=rhs[:, e_cols].bitcast(E4M3), rhs_scale=rhs_scale[:, e_cols], start=(u == 0), stop=(u == UNITS - 1))
 
+        nc.vector.scalar_tensor_tensor(neg_r2[:], rstd_sb[:], -1.0 / E, rstd_sb[:], ALU.mult, ALU.mult)
+        for u in range(2):
+            for v in range(2):
+                place_dq(u, v)
+                rope_dq(u, v)
+                interleave_on_gpsimd(u, v)
+        cosines_psum = place_cosines()
+        for u in range(2):
+            turn_w(u, 0)
+            turn_dz(u)
+        turn_w(2, 0)
+        turn_w(3, 0)
+        turn_w(0, 1)
+        for j in range(SLOTS):
+            norm(0, j)
+        interleave_h_on_gpsimd(0, slice(0, H_ON_GPSIMD))
+        for j in range(SLOTS):
+            norm(1, j)
+        narrow_stream()
+        for u in range(1, UNITS):
+            turn_w(u, 1)
+        interleave_h_on_vector(0, slice(H_ON_GPSIMD, HALF))
+        quantize_dz_tok(0)
+        interleave_h_on_vector(1, slice(0, HALF))
+        quantize_h(0)
+        quantize_dz_feat(0)
+        quantize_h(1)
+        quantize_w(0, 0)
+        for r in range(3):
+            dw(0, r)
+            dw(1, r)
+        for v in range(2):
+            rope_dk(2, v, cosines_psum)
+            interleave_on_gpsimd(2, v)
+        for v in range(2):
+            rope_dk(3, v, cosines_psum)
+        quantize_w(1, 0)
+        interleave_on_vector(3)
+        for k in range(2):
+            dw(k, 3)
+            dh(k, 0, 0)
+        turn_dz(2)
+        dh(2, 0, 0)
+        dh(0, 0, 1)
+        turn_dz(3)
+        quantize_dz_feat(1)
+        quantize_dz_tok(1)
+        quantize_w(0, 1)
+        for k in range(2):
+            dw(k, 4)
+            dh(1 + k, 0, 1)
+        dw(0, 5)
+        dw(1, 5)
+        for k in range(2):
+            dw(k, 6)
+            dh(3, 0, k)
+        for k in range(2):
+            dw(k, 7)
+            dh(k, 0, 2)
+        dh(0, 0, 3)
+        dh(1, 0, 3)
+        for k in range(2):
+            dw(2 + k, 0)
+            dh(2, 0, 2 + k)
+        dh(3, 0, 2)
+        dh(3, 0, 3)
+        scale(0, 0)
+        scale(1, 0)
+        quantize_w(1, 1)
+        scale(2, 0)
+        scale(3, 0)
 
-        whole_row, first_half, second_half = slice(0, 2), slice(0, 1), slice(1, 2)
-        on_vector, on_scalar = nc.vector.tensor_copy, nc.scalar.copy
+        whole_row = slice(0, 2)
 
         def norm_backward(j):
             scale(j, 1)
@@ -308,152 +368,22 @@ def tile_llamaselfattentionblock_pa_v_kernel(tc, x, g, wq, wk, rstd, grad_0, gra
                 store_dx(j - 1, whole_row, nc.sync)
             dot(j)
 
-        load_w(0, 0, nc.sync)
-        load_x()
-        load_w(1, 0, nc.sync)
-        load_w(0, 1, nc.sync)
-        load_w(1, 1, nc.sync)
-        load_dk(nc.sync, (0, 2, 1, 3))
-        place(0, 0)
-        nc.vector.scalar_tensor_tensor(neg_r2[:], rstd_sb[:], -1.0 / E, rstd_sb[:], ALU.mult, ALU.mult)
-        place(0, 1)
-        rope(0, 0)
-        place(1, 0)
-        rope(0, 1)
-        place(1, 1)
-        interleave_half(0, 1, "gpsimd")
-        place_cosines()
-        rope(1, 0)
-        interleave_half(0, 0, "scalar")
-        interleave_half(1, 0, "gpsimd")
-        turn_w(0, 0)
-        rope(1, 1)
-        turn_dz(0)
-        interleave_half(1, 1, "gpsimd")
-        turn_w(1, 0)
-        norm(0, 0)
-        turn_dz(1)
-        norm(0, 1)
-        turn_w(2, 0)
-        norm(0, 2)
-        turn_w(3, 0)
-        norm(0, 3)
-        turn_w(0, 1)
-        interleave_h_gpsimd(0)
-        norm(1, 0)
-        norm(1, 1)
-        norm(1, 2)
-        norm(1, 3)
-        narrow_stream()
-        quantize_dz_tok(0)
-        turn_w(1, 1)
-        interleave_h(1, on_vector)
-        turn_w(2, 1)
-        quantize_dz_tok(1)
-        turn_w(3, 1)
-        quantize_h(0)
-        dw(0, 0)
-        quantize_dz_feat(0)
-        dw(1, 0)
-        quantize_h(1)
-        dw(0, 1)
-        quantize_w(0, 0)
-        dw(1, 1)
-        quantize_dz_feat(1)
-        dw(0, 2)
-        rope(2, 0)
-        dw(1, 2)
-        interleave_half(2, 0, "gpsimd")
-        dw(0, 3)
-        rope(2, 1)
-        dh(0, 0, 0)
-        interleave_half(2, 1, "gpsimd")
-        dw(1, 3)
-        rope(3, 0)
-        dh(1, 0, 0)
-        rope(3, 1)
-        turn_dz(2)
-        quantize_w(1, 0)
-        dw(0, 4)
-        interleave(3, on_vector)
-        dh(2, 0, 0)
-        quantize_dz_feat(2)
-        dw(1, 4)
-        quantize_dz_tok(2)
-        dh(0, 0, 1)
-        turn_dz(3)
-        quantize_dz_feat(3)
-        dw(0, 5)
-        quantize_dz_tok(3)
-        dh(1, 0, 1)
-        quantize_w(0, 1)
-        dw(1, 5)
-        dh(2, 0, 1)
-        dw(0, 6)
-        dh(3, 0, 0)
-        dw(1, 6)
-        dh(3, 0, 1)
-        dw(0, 7)
-        dh(0, 0, 2)
-        dw(1, 7)
-        dh(1, 0, 2)
-        dh(0, 0, 3)
-        scale(0, 0)
-        dh(1, 0, 3)
-        scale(1, 0)
-        dw(2, 0)
-        quantize_w(1, 1)
-        dh(2, 0, 2)
-        dw(3, 0)
-        dh(2, 0, 3)
-        scale(2, 0)
-        dh(3, 0, 2)
-        dh(3, 0, 3)
-        scale(3, 0)
-        dw(2, 1)
-        dh(0, 1, 0)
-        dw(3, 1)
-        dh(0, 1, 1)
+        for k in range(2):
+            dw(2 + k, 1)
+            dh(0, 1, k)
         dh(0, 1, 2)
         dh(0, 1, 3)
-        scale(0, 1)
-        dw(2, 2)
-        dot(0)
-        dh(1, 1, 0)
-        dw(3, 2)
-        dh(1, 1, 1)
-        dw(2, 3)
-        dh(1, 1, 2)
-        dw(3, 3)
-        dh(1, 1, 3)
-        scale(1, 1)
-        dw(2, 4)
-        finish(0, whole_row)
-        store_dx(0, whole_row, nc.sync)
-        dw(3, 4)
-        dot(1)
-        dw(2, 5)
-        dh(2, 1, 0)
-        dw(3, 5)
-        dh(2, 1, 1)
-        dw(2, 6)
-        dh(2, 1, 2)
-        dw(3, 6)
-        dh(2, 1, 3)
-        scale(2, 1)
-        dw(2, 7)
-        finish(1, whole_row)
-        store_dx(1, whole_row, nc.sync)
-        dw(3, 7)
-        dot(2)
-        dh(3, 1, 0)
-        dh(3, 1, 1)
-        dh(3, 1, 2)
-        dh(3, 1, 3)
-        scale(3, 1)
-        finish(2, whole_row)
-        store_dx(2, whole_row, nc.sync)
-        dot(3)
-        for halves, queue in ((first_half, nc.sync), (second_half, nc.scalar)):
-            finish(3, halves)
-            store_dx(3, halves, queue)
+        norm_backward(0)
+        for j in (1, 2):
+            for u in range(UNITS):
+                dw(2 + u % 2, 3 * j - 1 + u // 2)
+                dh(j, 1, u)
+            norm_backward(j)
+            dw(2, 3 * j + 1)
+            dw(3, 3 * j + 1)
+        for u in range(UNITS):
+            dh(3, 1, u)
+        norm_backward(3)
+        for h, queue in enumerate((nc.sync, nc.scalar)):
+            finish(3, slice(h, h + 1))
+            store_dx(3, slice(h, h + 1), queue)

@@ -54,7 +54,7 @@ def tile_llamaselfattentionblock_pa_v_kernel(tc, x, g, wq, wk, rstd, grad_0, gra
             return psum.tile(shape, dtype, name="bank%d" % k, tag="bank%d" % k, bufs=1)
 
         dq_sb = [kept("dq%d" % u, [P, UNIT_HEADS, SLOTS, HD], BF16) for u in range(2)]
-        dk_sb = kept("dk", [P, HEADS, SLOTS, HD], BF16)
+        dk_sb = [kept("dk%d" % u, [P, UNIT_HEADS, SLOTS, HD], BF16) for u in range(2)]
         rstd_sb = kept("rstd_sb", [P, SLOTS], F32)
         g_sb = kept("g_sb", [P, E // P], BF16)
         identity = kept("identity", [P, P], F32)
@@ -78,9 +78,9 @@ def tile_llamaselfattentionblock_pa_v_kernel(tc, x, g, wq, wk, rstd, grad_0, gra
 
         tokens = kept("tokens", [P, SLOTS], I32)
         nc.gpsimd.iota(tokens[:], pattern=[[1, SLOTS]], base=0, channel_multiplier=SLOTS)
-        nc.gpsimd.dma_start(out=rstd_sb[:], in_=rstd.rearrange("b (q j) -> (b q) j", j=SLOTS))
         make_identity(nc, identity[:])
         nc.sync.dma_start(out=g_sb[:], in_=g.rearrange("(p c) -> p c", p=P))
+        nc.sync.dma_start(out=rstd_sb[:], in_=rstd.rearrange("b (q j) -> (b q) j", j=SLOTS))
         for head in range(HEADS):
             nc.sync.dma_start(out=dq_sb[head // UNIT_HEADS][:, head % UNIT_HEADS].rearrange("p j d -> p (j d)"),
                               in_=grad_0[:, head].rearrange("b (q j) d -> q b (j d)", j=SLOTS))
@@ -93,32 +93,30 @@ def tile_llamaselfattentionblock_pa_v_kernel(tc, x, g, wq, wk, rstd, grad_0, gra
         load_w(1, 0)
         load_w(0, 1)
         load_w(1, 1)
-        for batch in (0, 2, 1, 3):
-            nc.sync.dma_start(out=dk_sb[32 * batch : 32 * batch + 32].rearrange("q n j d -> q n (j d)"),
-                              in_=grad_1[batch].rearrange("n (q j) d -> q n (j d)", j=SLOTS))
+        for u in range(2):
+            for batch in (0, 2, 1, 3):
+                nc.sync.dma_start(out=dk_sb[u][32 * batch : 32 * batch + 32].rearrange("q n j d -> q n (j d)"),
+                                  in_=grad_1[batch, u * UNIT_HEADS : (u + 1) * UNIT_HEADS].rearrange("n (q j) d -> q n (j d)", j=SLOTS))
 
         order = kept("order", [P, B, P // B], BF16)
         nc.gpsimd.tensor_copy(out=order[:], in_=identity[:].rearrange("p (q b) -> p b q", b=B))
 
         positions = kept("positions", [P, SLOTS], I32)
-        coarse = kept("coarse", [P, SLOTS, 4], F32)
-        fine = kept("fine", [P, 16], F32)
+        ones = kept("ones", [P, HD // 4], F32)
+        ratio = kept("ratio", [P, HD // 4], F32)
+        theta = kept("theta", [P, 2, HD // 4], F32)
         turns = kept("turns", [P, 2, SLOTS * HD // 4], F32)
         whole = kept("whole", [P, 2, SLOTS * HD // 4], I32)
         fraction = kept("fraction", [P, 2, SLOTS * HD // 4], F32)
         cosines = kept("cosines", [P, 2, SLOTS * HD // 2], F32)
-        nc.vector.memset(fine[:, 0:1], 1.0)
+        nc.vector.memset(ones[:], 1.0)
+        nc.vector.tensor_single_scalar(ratio[:], ones[:], 10000.0 ** (-2 / 64.0), ALU.mult)
         nc.vector.tensor_single_scalar(positions[:], tokens[:], L - 1, ALU.bitwise_and)
-        for k in range(1, 4):
-            nc.vector.tensor_single_scalar(fine[:, k : k + 1], fine[:, 0:1], 10000.0 ** (-k / 64.0), ALU.mult)
-        for k in range(4):
-            nc.vector.tensor_single_scalar(coarse[:, :, k], positions[:], 10000.0 ** (-k / 4.0) * 0.5 / math.pi, ALU.mult)
-        for k in range(1, 4):
-            nc.vector.tensor_single_scalar(fine[:, 4 * k : 4 * k + 4], fine[:, 0:4], 10000.0 ** (-k / 16.0), ALU.mult)
         for v in range(2):
-            nc.vector.tensor_tensor(turns[:, v].rearrange("p (k b) -> p k b", b=8),
-                                    coarse[:].rearrange("p j a -> p (j a)").unsqueeze(2).to_broadcast([P, 16, 8]),
-                                    fine[:, v:16:2].unsqueeze(1).to_broadcast([P, 16, 8]), ALU.mult)
+            nc.vector.tensor_tensor_scan(theta[:, v], ratio[:], ones[:], 10000.0 ** ((2 - v) / 64.0) * 0.5 / math.pi, ALU.mult, ALU.mult)
+        for v in range(2):
+            nc.vector.tensor_tensor(turns[:, v].rearrange("p (j w) -> p j w", j=SLOTS), positions[:].unsqueeze(2).to_broadcast([P, SLOTS, HD // 4]),
+                                    theta[:, v].unsqueeze(1).to_broadcast([P, SLOTS, HD // 4]), ALU.mult)
         for v in range(2):
             nc.vector.tensor_single_scalar(whole[:, v], turns[:, v], 0.25, ALU.add)
         for v in range(2):
@@ -156,8 +154,7 @@ def tile_llamaselfattentionblock_pa_v_kernel(tc, x, g, wq, wk, rstd, grad_0, gra
             rope(u, v, dq_bank[u, v][:].rearrange("p k c -> p (k c)"), cosines)
 
         def rope_dk(u, v, cos):
-            heads = dk_sb[:, (u - 2) * UNIT_HEADS : (u - 1) * UNIT_HEADS]
-            rope(u, v, heads.rearrange("p n j (w v s) -> p (n j w) v s", v=2, s=2)[:, :, v, :], cos)
+            rope(u, v, dk_sb[u - 2][:].rearrange("p n j (w v s) -> p (n j w) v s", v=2, s=2)[:, :, v, :], cos)
 
         def gpsimd_copy(out, in_):
             nc.gpsimd.tensor_scalar(out=out, in0=in_, scalar1=1.0, scalar2=1.0, op0=ALU.mult, op1=ALU.mult)

@@ -156,18 +156,16 @@ def tile_llamaselfattentionblock_pa_v_kernel(tc, x, g, wq, wk, rstd, grad_0, gra
         def rope_dk(u, v, cos):
             rope(u, v, dk_sb[u - 2][:].rearrange("p n j (w v s) -> p (n j w) v s", v=2, s=2)[:, :, v, :], cos)
 
-        def gpsimd_copy(out, in_):
-            nc.gpsimd.tensor_scalar(out=out, in0=in_, scalar1=1.0, scalar2=1.0, op0=ALU.mult, op1=ALU.mult)
-
         def interleave_on_gpsimd(u, v):
-            gpsimd_copy(dz_tok[u // 2][:, u % 2].rearrange("p (m v s) j -> p v m s j", v=2, s=2)[:, v], dz[u][:, :, v].rearrange("p j c -> p c j"))
+            nc.gpsimd.tensor_copy(out=dz_tok[u // 2][:, u % 2].rearrange("p (m v s) j -> p v m s j", v=2, s=2)[:, v],
+                                  in_=dz[u][:, :, v].rearrange("p j c -> p c j"))
 
         def interleave_on_vector(u):
             nc.vector.tensor_copy(out=dz_tok[u // 2][:, u % 2].rearrange("p (m v s) j -> p v m j s", v=2, s=2),
                                   in_=dz[u][:].rearrange("p j v (m s) -> p v m j s", s=2))
 
         def interleave_h_on_gpsimd(h, cols):
-            gpsimd_copy(h_tok[h][:, cols], h_flat[h][:, :, cols].rearrange("p j c -> p c j"))
+            nc.gpsimd.tensor_copy(out=h_tok[h][:, cols], in_=h_flat[h][:, :, cols].rearrange("p j c -> p c j"))
 
         def interleave_h_on_vector(h, cols):
             nc.vector.tensor_copy(out=h_tok[h][:, cols].rearrange("p (c i) j -> p c j i", i=4),

@@ -81,15 +81,21 @@ def tile_llamaselfattentionblock_pa_v_kernel(tc, x, g, wq, wk, rstd, grad_0, gra
         make_identity(nc, identity[:])
         nc.sync.dma_start(out=g_sb[:], in_=g.rearrange("(p c) -> p c", p=P))
         nc.sync.dma_start(out=rstd_sb[:], in_=rstd.rearrange("b (q j) -> (b q) j", j=SLOTS))
-        for head in range(HEADS):
-            nc.sync.dma_start(out=dq_sb[head // UNIT_HEADS][:, head % UNIT_HEADS].rearrange("p j d -> p (j d)"),
-                              in_=grad_0[:, head].rearrange("b (q j) d -> q b (j d)", j=SLOTS))
 
-        def load_w(a, h):
-            nc.sync.dma_start(out=w_sb[a][h][:], in_=weights[a][h * HALF : (h + 1) * HALF, :].rearrange("(q i) f -> q i f", i=4))
+        def load_dq(u):
+            for n in range(UNIT_HEADS):
+                nc.sync.dma_start(out=dq_sb[u][:, n].rearrange("p j d -> p (j d)"),
+                                  in_=grad_0[:, u * UNIT_HEADS + n].rearrange("b (q j) d -> q b (j d)", j=SLOTS))
 
-        load_w(0, 0)
+        def load_w(a, h, sets=slice(0, 4)):
+            rows = weights[a][h * HALF : (h + 1) * HALF, :].rearrange("(q i) f -> q i f", i=4)
+            nc.sync.dma_start(out=w_sb[a][h][:, sets], in_=rows[:, sets])
+
+        load_dq(0)
+        load_w(0, 0, slice(0, 2))
+        load_dq(1)
         nc.sync.dma_start(out=x_sb[:], in_=x_rows)
+        load_w(0, 0, slice(2, 4))
         load_w(1, 0)
         load_w(0, 1)
         load_w(1, 1)
@@ -229,11 +235,11 @@ def tile_llamaselfattentionblock_pa_v_kernel(tc, x, g, wq, wk, rstd, grad_0, gra
                 rows = dz_feat[u // 2][:, u % 2].bitcast(F32)[:, jp * 4 * P : (jp + 1) * 4 * P]
                 nc.scalar.copy(out=rows.rearrange("p (j q v) -> p j q v", j=2, v=2), in_=ps[:].rearrange("p (j v) q -> p j q v", v=2))
 
-        def turn_w(u, h):
-            if u % 2 == 0:
+        def turn_w(u, h, banks=(0, 1)):
+            if (u // 2, h) not in w_feat:
                 w_feat[u // 2, h] = rotating("w_feat", [P, 2, 4 * HALF], BF16, 4)
             words = w_sb[u // 2][h][:].rearrange("p i f -> p (i f)").bitcast(F32)
-            for ip in range(2):
+            for ip in banks:
                 ps = stream_bank([P, 4, P])
                 for i in range(2):
                     first = (2 * ip + i) * (J // 2) + (u % 2) * (UNIT // 2)
@@ -288,10 +294,14 @@ def tile_llamaselfattentionblock_pa_v_kernel(tc, x, g, wq, wk, rstd, grad_0, gra
                 place_dq(u, v)
                 rope_dq(u, v)
                 interleave_on_gpsimd(u, v)
+            if u == 0:
+                turn_w(0, 0, (0,))
+                turn_w(1, 0, (0,))
         cosines_psum = place_cosines()
-        for u in range(2):
-            turn_w(u, 0)
-            turn_dz(u)
+        turn_dz(0)
+        turn_dz(1)
+        turn_w(0, 0, (1,))
+        turn_w(1, 0, (1,))
         turn_w(2, 0)
         turn_w(3, 0)
         turn_w(0, 1)
@@ -352,7 +362,6 @@ def tile_llamaselfattentionblock_pa_v_kernel(tc, x, g, wq, wk, rstd, grad_0, gra
         scale(1, 0)
         quantize_w(1, 1)
         scale(2, 0)
-        scale(3, 0)
 
         whole_row = slice(0, 2)
 
@@ -368,7 +377,9 @@ def tile_llamaselfattentionblock_pa_v_kernel(tc, x, g, wq, wk, rstd, grad_0, gra
             dh(0, 1, k)
         dh(0, 1, 2)
         dh(0, 1, 3)
-        norm_backward(0)
+        scale(0, 1)
+        scale(3, 0)
+        dot(0)
         for j in (1, 2):
             for u in range(UNITS):
                 dw(2 + u % 2, 3 * j - 1 + u // 2)

@@ -24,14 +24,17 @@ HALF = 512
 UNITS = 2 * J // UNIT
 UNIT_HEADS = UNIT // HD
 ROW_TILES = E // P
-H_ON_GPSIMD = 256
-GAIN_BANK, DH_BANK, COSINE_BANK = 0, 4, 7
+H_ON_GPSIMD = 384
+GAIN_BANK = 0
+DH_BANK = 4
+ROPE_BANKS = ((None, 5), (6, 3), (6, 7), (6, 7))
 FLOPS = 2 * 2 * T * E * 2 * J
 
 
 def tile_llamaselfattentionblock_pa_v_kernel(tc, x, g, wq, wk, rstd, grad_0, grad_1, out_0, out_1, out_2):
     nc = tc.nc
     weights = (wq, wk)
+    grads = (grad_0, grad_1)
     weight_grads = (out_1, out_2)
     x_rows = x.flatten_outer_dims().rearrange("(p j) e -> p j e", j=SLOTS)
     out_rows = out_0.flatten_outer_dims().rearrange("(p j) (h c) -> p j h c", j=SLOTS, h=2)
@@ -53,8 +56,7 @@ def tile_llamaselfattentionblock_pa_v_kernel(tc, x, g, wq, wk, rstd, grad_0, gra
         def bank(k, shape, dtype=F32):
             return psum.tile(shape, dtype, name="bank%d" % k, tag="bank%d" % k, bufs=1)
 
-        dq_sb = [kept("dq%d" % u, [P, UNIT_HEADS, SLOTS, HD], BF16) for u in range(2)]
-        dk_sb = [kept("dk%d" % u, [P, UNIT_HEADS, SLOTS, HD], BF16) for u in range(2)]
+        grad_sb = [kept("grad%d" % u, [P, UNIT_HEADS, SLOTS, HD], BF16) for u in range(UNITS)]
         rstd_sb = kept("rstd_sb", [P, SLOTS], F32)
         g_sb = kept("g_sb", [P, E // P], BF16)
         identity = kept("identity", [P, P], F32)
@@ -63,7 +65,7 @@ def tile_llamaselfattentionblock_pa_v_kernel(tc, x, g, wq, wk, rstd, grad_0, gra
         gain = kept("gain", [P, E], BF16)
         h_flat = [rotating("h_flat%d" % h, [P, SLOTS, HALF], BF16, 1) for h in range(2)]
         w_sb = [[rotating("w%d%d" % (a, h), [P, 4, J], BF16, 1) for h in range(2)] for a in range(2)]
-        h_tok = [rotating("h_tok%d" % h, [P, HALF, SLOTS], BF16, 1) for h in range(2)]
+        h_tok = [rotating("h_tok0", [P, HALF, SLOTS], BF16, 1), rotating("h_tok1", [P, HALF // 2, SLOTS], BF16, 1)]
         h_q = [codes("h_q%d" % h, HALF) for h in range(2)]
         dz_tok_q = [codes("dz_tok_q%d" % a, 2 * UNIT) for a in range(2)]
         dz_feat_q = [codes("dz_feat_q%d" % a, 2 * T) for a in range(2)]
@@ -72,7 +74,7 @@ def tile_llamaselfattentionblock_pa_v_kernel(tc, x, g, wq, wk, rstd, grad_0, gra
         coef = [kept("coef%d" % j, [P, 1], F32) for j in range(SLOTS)]
         dz_tok = [kept("dz_tok%d" % a, [P, 2, UNIT, SLOTS], BF16) for a in range(2)]
         dz_feat = [kept("dz_feat%d" % a, [P, 2, 4 * T], BF16) for a in range(2)]
-        dz, dq_bank, w_feat, dh_bank, dw_rows, scaled = {}, {}, {}, {}, {}, {}
+        dz, grad_bank, w_feat, dh_bank, dw_rows, scaled = {}, {}, {}, {}, {}, {}
 
         ctx.enter_context(tc.manual_schedule())
 
@@ -82,27 +84,26 @@ def tile_llamaselfattentionblock_pa_v_kernel(tc, x, g, wq, wk, rstd, grad_0, gra
         nc.sync.dma_start(out=g_sb[:], in_=g.rearrange("(p c) -> p c", p=P))
         nc.sync.dma_start(out=rstd_sb[:], in_=rstd.rearrange("b (q j) -> (b q) j", j=SLOTS))
 
-        def load_dq(u):
+        def load_grad(u):
             for n in range(UNIT_HEADS):
-                nc.sync.dma_start(out=dq_sb[u][:, n].rearrange("p j d -> p (j d)"),
-                                  in_=grad_0[:, u * UNIT_HEADS + n].rearrange("b (q j) d -> q b (j d)", j=SLOTS))
+                nc.sync.dma_start(out=grad_sb[u][:, n].rearrange("p j d -> p (j d)"),
+                                  in_=grads[u // 2][:, (u % 2) * UNIT_HEADS + n].rearrange("b (q j) d -> q b (j d)", j=SLOTS))
 
         def load_w(a, h, sets=slice(0, 4)):
             rows = weights[a][h * HALF : (h + 1) * HALF, :].rearrange("(q i) f -> q i f", i=4)
             nc.sync.dma_start(out=w_sb[a][h][:, sets], in_=rows[:, sets])
 
-        load_dq(0)
+        load_grad(0)
+        load_grad(1)
         load_w(0, 0, slice(0, 2))
-        load_dq(1)
         nc.sync.dma_start(out=x_sb[:], in_=x_rows)
         load_w(0, 0, slice(2, 4))
-        load_w(1, 0)
+        load_w(1, 0, slice(0, 2))
+        load_w(1, 0, slice(2, 4))
+        load_grad(2)
         load_w(0, 1)
+        load_grad(3)
         load_w(1, 1)
-        for u in range(2):
-            for batch in (0, 2, 1, 3):
-                nc.sync.dma_start(out=dk_sb[u][32 * batch : 32 * batch + 32].rearrange("q n j d -> q n (j d)"),
-                                  in_=grad_1[batch, u * UNIT_HEADS : (u + 1) * UNIT_HEADS].rearrange("n (q j) d -> q n (j d)", j=SLOTS))
 
         order = kept("order", [P, B, P // B], BF16)
         nc.gpsimd.tensor_copy(out=order[:], in_=identity[:].rearrange("p (q b) -> p b q", b=B))
@@ -138,29 +139,27 @@ def tile_llamaselfattentionblock_pa_v_kernel(tc, x, g, wq, wk, rstd, grad_0, gra
                                  func=ACT.Sin, scale=2.0 * math.pi)
         nc.scalar.copy(out=gain[:].bitcast(F32), in_=gain_psum)
 
-        def place_dq(u, v):
-            dq_bank[u, v] = bank(((4, 5), (6, 3))[u][v], [P, 2, UNIT], BF16)
-            pairs = dq_sb[u][:].rearrange("p (k n) j (w v s) -> p k (n j w) v s", k=2, v=2, s=2)
+        def place_grad(u, v):
+            grad_bank[u, v] = bank(ROPE_BANKS[u][v], [P, 2, UNIT], BF16)
+            pairs = grad_sb[u][:].rearrange("p (k n) j (w v s) -> p k (n j w) v s", k=2, v=2, s=2)
             for k in range(2):
-                nc.tensor.matmul(dq_bank[u, v][:, k], lhsT=order[:].rearrange("p b q -> p (b q)"), rhs=pairs[:, k, :, v, :], start=True, stop=True)
+                nc.tensor.matmul(grad_bank[u, v][:, k], lhsT=order[:].rearrange("p b q -> p (b q)"), rhs=pairs[:, k, :, v, :], start=True, stop=True)
 
-        def place_cosines():
-            ps = bank(COSINE_BANK, [P, 2, SLOTS * HD // 2])
-            for v in range(2):
-                nc.tensor.matmul(ps[:, v], lhsT=identity[:], rhs=cosines[:, v], start=True, stop=True)
-            return ps
+        def first_rope():
+            dz[0] = rotating("dz", [P, SLOTS, 2, UNIT // 2], BF16, 4)
+            pairs = grad_sb[0][:].rearrange("p (k n) j (w v s) -> p k (n j w) v s", k=2, v=2, s=2)
+            rows = dz[0][:, :, 0, :].rearrange("p j (k n c) -> p k n j c", k=2, n=2)
+            for k in range(2):
+                ps = bank((7, 4)[k], [P, UNIT], BF16)
+                nc.tensor.matmul(ps[:], lhsT=order[:].rearrange("p b q -> p (b q)"), rhs=pairs[:, k, :, 0, :], start=True, stop=True)
+                nc.vector.tensor_tensor(out=rows[:, k], in0=ps[:], in1=cosines[:, 0, :].unsqueeze(1).to_broadcast([P, 2, 2 * P]), op=ALU.mult)
 
-        def rope(u, v, grad, cos):
+        def rope(u, v):
             if v == 0:
                 dz[u] = rotating("dz", [P, SLOTS, 2, UNIT // 2], BF16, 4)
-            nc.vector.tensor_tensor(out=dz[u][:, :, v, :].rearrange("p j (n c) -> p n j c", n=UNIT_HEADS), in0=grad,
-                                    in1=cos[:, v, :].unsqueeze(1).to_broadcast([P, UNIT_HEADS, 2 * P]), op=ALU.mult)
-
-        def rope_dq(u, v):
-            rope(u, v, dq_bank[u, v][:].rearrange("p k c -> p (k c)"), cosines)
-
-        def rope_dk(u, v, cos):
-            rope(u, v, dk_sb[u - 2][:].rearrange("p n j (w v s) -> p (n j w) v s", v=2, s=2)[:, :, v, :], cos)
+            nc.vector.tensor_tensor(out=dz[u][:, :, v, :].rearrange("p j (n c) -> p n j c", n=UNIT_HEADS),
+                                    in0=grad_bank[u, v][:].rearrange("p k c -> p (k c)"),
+                                    in1=cosines[:, v, :].unsqueeze(1).to_broadcast([P, UNIT_HEADS, 2 * P]), op=ALU.mult)
 
         def interleave_on_gpsimd(u, v):
             nc.gpsimd.tensor_copy(out=dz_tok[u // 2][:, u % 2].rearrange("p (m v s) j -> p v m s j", v=2, s=2)[:, v],
@@ -170,12 +169,11 @@ def tile_llamaselfattentionblock_pa_v_kernel(tc, x, g, wq, wk, rstd, grad_0, gra
             nc.vector.tensor_copy(out=dz_tok[u // 2][:, u % 2].rearrange("p (m v s) j -> p v m j s", v=2, s=2),
                                   in_=dz[u][:].rearrange("p j v (m s) -> p v m j s", s=2))
 
-        def interleave_h_on_gpsimd(h, cols):
-            nc.gpsimd.tensor_copy(out=h_tok[h][:, cols], in_=h_flat[h][:, :, cols].rearrange("p j c -> p c j"))
+        def interleave_h_on_gpsimd(out, h, cols):
+            nc.gpsimd.tensor_copy(out=out, in_=h_flat[h][:, :, cols].rearrange("p j c -> p c j"))
 
-        def interleave_h_on_vector(h, cols):
-            nc.vector.tensor_copy(out=h_tok[h][:, cols].rearrange("p (c i) j -> p c j i", i=4),
-                                  in_=h_flat[h][:, :, cols].rearrange("p j (c i) -> p c j i", i=4))
+        def interleave_h(copy, out, h, cols):
+            copy(out=out.rearrange("p (c i) j -> p c j i", i=4), in_=h_flat[h][:, :, cols].rearrange("p j (c i) -> p c j i", i=4))
 
         def norm(h, j):
             cols = slice(h * HALF, (h + 1) * HALF)
@@ -188,8 +186,8 @@ def tile_llamaselfattentionblock_pa_v_kernel(tc, x, g, wq, wk, rstd, grad_0, gra
         def quantize_dz_tok(a):
             quantize(dz_tok_q[a], E5M2, dz_tok[a][:].rearrange("p u c j -> p (u c j)"))
 
-        def quantize_h(h):
-            quantize(h_q[h], E4M3, h_tok[h][:].rearrange("p c j -> p (c j)"))
+        def quantize_h(h, cols, values):
+            quantize((h_q[h][0][:, cols], h_q[h][1][:, cols]), E4M3, values.rearrange("p c j -> p (c j)"))
 
         def quantize_dz_feat(a):
             quantize(dz_feat_q[a], E5M2, dz_feat[a][:].rearrange("p u c -> p (u c)"))
@@ -198,8 +196,8 @@ def tile_llamaselfattentionblock_pa_v_kernel(tc, x, g, wq, wk, rstd, grad_0, gra
             quantize(w_q[a][h], E4M3, w_feat[a, h][:].rearrange("p u c -> p (u c)"))
 
         def scale(j, h):
-            if h == 0:
-                scaled[j] = rotating(("h_flat%d", "h_tok%d")[j // 2] % (j % 2), [P, 2, HALF], F32, 1)[:]
+            if j not in scaled:
+                scaled[j] = rotating(("h_flat0", "h_flat1", "h_tok0", "w_feat00")[j], [P, 2, HALF], F32, 1)[:]
             nc.vector.scalar_tensor_tensor(scaled[j][:, h], dh_bank[j, h][:], rstd_sb[:, j : j + 1], gain[:, h * HALF : (h + 1) * HALF], ALU.mult, ALU.mult)
 
         def dot(j):
@@ -213,70 +211,61 @@ def tile_llamaselfattentionblock_pa_v_kernel(tc, x, g, wq, wk, rstd, grad_0, gra
         def store_dx(j, halves, queue):
             queue.dma_start(out=out_rows[:, j, halves], in_=scaled[j][:, halves])
 
-        stream = [1, 2, 4, 5, 3]
+        stream = [1, 2, 7, 4, 5, 3]
 
         def stream_bank(shape):
             k = stream.pop(0)
             stream.append(k)
             return bank(k, shape)
 
-        def narrow_stream():
-            stream.remove(4)
-            stream.remove(5)
-            stream.append(GAIN_BANK)
+        def empty(pairs, copy=nc.scalar.copy):
+            for rows, ps in pairs:
+                copy(out=rows, in_=ps)
 
         def turn_dz(u):
             words = dz[u][:].rearrange("p j v c -> p (j v c)").bitcast(F32)
+            pairs = []
             for jp in range(2):
                 ps = stream_bank([P, 4, P])
                 for k in range(4):
                     first = (4 * jp + k) * P
                     nc.tensor.transpose(ps[:, k, :], words[:, first : first + P], identity[:])
                 rows = dz_feat[u // 2][:, u % 2].bitcast(F32)[:, jp * 4 * P : (jp + 1) * 4 * P]
-                nc.scalar.copy(out=rows.rearrange("p (j q v) -> p j q v", j=2, v=2), in_=ps[:].rearrange("p (j v) q -> p j q v", v=2))
+                pairs.append((rows.rearrange("p (j q v) -> p j q v", j=2, v=2), ps[:].rearrange("p (j v) q -> p j q v", v=2)))
+            empty(pairs)
 
-        def turn_w(u, h, banks=(0, 1)):
-            if (u // 2, h) not in w_feat:
-                w_feat[u // 2, h] = rotating("w_feat", [P, 2, 4 * HALF], BF16, 4)
-            words = w_sb[u // 2][h][:].rearrange("p i f -> p (i f)").bitcast(F32)
-            for ip in banks:
+        def turn_w(a, h, ip):
+            if ip == 0:
+                w_feat[a, h] = rotating("w_feat%d%d" % (a, h), [P, 2, 4 * HALF], BF16, 1)
+            words = w_sb[a][h][:].rearrange("p i f -> p (i f)").bitcast(F32)
+            pairs = []
+            for u in range(2):
                 ps = stream_bank([P, 4, P])
                 for i in range(2):
-                    first = (2 * ip + i) * (J // 2) + (u % 2) * (UNIT // 2)
+                    first = (2 * ip + i) * (J // 2) + u * (UNIT // 2)
                     for v in range(2):
                         nc.tensor.transpose(ps[:, 2 * i + v, :], words[:, first + v : first + UNIT // 2 : 2], identity[:])
-                rows = w_feat[u // 2, h][:, u % 2].bitcast(F32).rearrange("p (q i k) -> p i q k", i=2, k=4)
-                nc.scalar.copy(out=rows[:, ip], in_=ps[:].rearrange("p k q -> p q k"))
+                rows = w_feat[a, h][:, u].bitcast(F32).rearrange("p (q i k) -> p i q k", i=2, k=4)
+                pairs.append((rows[:, ip], ps[:].rearrange("p k q -> p q k")))
+            empty(pairs)
 
-        waiting = []
-
-        def store_dw(a, r, queue):
-            queue.dma_start(out=weight_grads[a][r * P : (r + 1) * P, :], in_=dw_rows[a, r])
-
-        def dw(u, r):
-            ps = stream_bank([P, UNIT])
+        def dw(u, r, vector_bank=None):
+            if u == 0:
+                dw_rows[0, r] = rotating("dw_rows", [P, J], F32, ROW_TILES)[:]
+            if u == 2 and r % 2 == 0:
+                both = rotating("w%d%d" % (r // 2 % 2, r // 4), [P, 2, J], F32, 1)
+                dw_rows[1, r], dw_rows[1, r + 1] = both[:, 0], both[:, 1]
+            ps = stream_bank([P, UNIT]) if vector_bank is None else bank(vector_bank, [P, UNIT])
+            copy = nc.scalar.copy if vector_bank is None else nc.vector.tensor_copy
             lhs, lhs_scale = h_q[r // 4]
             rhs, rhs_scale = dz_tok_q[u // 2]
             cols = slice((r % 4) * P, (r % 4 + 1) * P)
             f_cols = slice((u % 2) * UNIT, (u % 2 + 1) * UNIT)
             nc.tensor.matmul_mx(out=ps[:], lhsT=lhs[:, cols].bitcast(E4M3), lhsT_scale=lhs_scale[:, cols],
                                 rhs=rhs[:, f_cols].bitcast(E5M2), rhs_scale=rhs_scale[:, f_cols], start=True, stop=True)
-            if u == 0:
-                dw_rows[0, r] = rotating("dw_rows", [P, J], F32, ROW_TILES)[:]
-            if u == 2 and r % 2 == 0:
-                both = rotating("w%d%d" % (r // 2 % 2, r // 4), [P, 2, J], F32, 1)
-                dw_rows[1, r], dw_rows[1, r + 1] = both[:, 0], both[:, 1]
-            rows = dw_rows[u // 2, r]
-            nc.scalar.copy(out=rows[:, (u % 2) * UNIT : (u % 2 + 1) * UNIT], in_=ps[:])
-            while waiting:
-                store_dw(*waiting.pop(), nc.scalar)
+            copy(out=dw_rows[u // 2, r][:, f_cols], in_=ps[:])
             if u % 2 == 1:
-                if r % 2 == 0 or (u == 1 and r < 4):
-                    store_dw(u // 2, r, nc.sync)
-                elif (u, r) == (UNITS - 1, ROW_TILES - 1):
-                    store_dw(u // 2, r, nc.scalar)
-                else:
-                    waiting.append((u // 2, r))
+                nc.sync.dma_start(out=weight_grads[u // 2][r * P : (r + 1) * P, :], in_=dw_rows[u // 2, r])
 
         def dh(j, h, u):
             if u == 0:
@@ -289,107 +278,112 @@ def tile_llamaselfattentionblock_pa_v_kernel(tc, x, g, wq, wk, rstd, grad_0, gra
                                 rhs=rhs[:, e_cols].bitcast(E4M3), rhs_scale=rhs_scale[:, e_cols], start=(u == 0), stop=(u == UNITS - 1))
 
         nc.vector.scalar_tensor_tensor(neg_r2[:], rstd_sb[:], -1.0 / E, rstd_sb[:], ALU.mult, ALU.mult)
-        for u in range(2):
-            for v in range(2):
-                place_dq(u, v)
-                rope_dq(u, v)
-                interleave_on_gpsimd(u, v)
-            if u == 0:
-                turn_w(0, 0, (0,))
-                turn_w(1, 0, (0,))
-        cosines_psum = place_cosines()
+        first_rope()
+        interleave_on_gpsimd(0, 0)
+        for u, v in ((0, 1), (1, 0), (1, 1)):
+            place_grad(u, v)
+            rope(u, v)
+            interleave_on_gpsimd(u, v)
+        turn_w(0, 0, 0)
         turn_dz(0)
         turn_dz(1)
-        turn_w(0, 0, (1,))
-        turn_w(1, 0, (1,))
-        turn_w(2, 0)
-        turn_w(3, 0)
-        turn_w(0, 1)
+        turn_w(0, 0, 1)
+        stream.remove(7)
+        turn_w(1, 0, 0)
+        turn_w(1, 0, 1)
         for j in range(SLOTS):
             norm(0, j)
-        interleave_h_on_gpsimd(0, slice(0, H_ON_GPSIMD))
+        interleave_h_on_gpsimd(h_tok[0][:, :H_ON_GPSIMD], 0, slice(0, H_ON_GPSIMD))
         for j in range(SLOTS):
             norm(1, j)
-        narrow_stream()
-        for u in range(1, UNITS):
-            turn_w(u, 1)
-        interleave_h_on_vector(0, slice(H_ON_GPSIMD, HALF))
+        stream.append(GAIN_BANK)
+        interleave_h(nc.scalar.copy, h_tok[1][:], 1, slice(0, HALF // 2))
+        interleave_h(nc.vector.tensor_copy, h_tok[0][:, H_ON_GPSIMD:], 0, slice(H_ON_GPSIMD, HALF))
         quantize_dz_tok(0)
-        interleave_h_on_vector(1, slice(0, HALF))
-        quantize_h(0)
+        quantize_h(0, slice(0, HALF), h_tok[0][:])
         quantize_dz_feat(0)
-        quantize_h(1)
         quantize_w(0, 0)
-        for r in range(3):
-            dw(0, r)
-            dw(1, r)
+        quantize_h(1, slice(0, 2 * P), h_tok[1][:])
+        h_rest = rotating("h_tok1", [P, 2 * P, SLOTS], BF16, 1)
+        interleave_h_on_gpsimd(h_rest[:, :P], 1, slice(2 * P, 3 * P))
         for v in range(2):
-            rope_dk(2, v, cosines_psum)
+            place_grad(2, v)
+            rope(2, v)
             interleave_on_gpsimd(2, v)
-        for v in range(2):
-            rope_dk(3, v, cosines_psum)
-        quantize_w(1, 0)
-        interleave_on_vector(3)
-        for k in range(2):
-            dw(k, 3)
-            dh(k, 0, 0)
-        turn_dz(2)
-        dh(2, 0, 0)
+        dw(0, 0)
+        dw(1, 0)
+        turn_w(0, 1, 0)
+        dw(0, 1)
+        dw(1, 1)
+        stream.remove(DH_BANK)
+        turn_w(0, 1, 1)
+        stream.remove(DH_BANK + 1)
+        dh(0, 0, 0)
         dh(0, 0, 1)
+        place_grad(3, 0)
+        turn_w(1, 1, 0)
+        place_grad(3, 1)
+        for v in range(2):
+            rope(3, v)
+            interleave_on_gpsimd(3, v)
+        turn_dz(2)
+        dw(0, 2, 6)
+        dw(0, 4)
+        dw(1, 4)
+        dw(1, 2, 7)
         turn_dz(3)
+        dw(0, 3, 6)
+        interleave_h(nc.vector.tensor_copy, h_rest[:, P:], 1, slice(3 * P, HALF))
+        quantize_w(1, 0)
         quantize_dz_feat(1)
-        quantize_dz_tok(1)
+        quantize_h(1, slice(2 * P, HALF), h_rest[:])
         quantize_w(0, 1)
-        for k in range(2):
-            dw(k, 4)
-            dh(1 + k, 0, 1)
+        quantize_dz_tok(1)
+        dw(1, 3)
+        dh(1, 0, 0)
+        dh(1, 0, 1)
+        turn_w(1, 1, 1)
+        dh(3, 0, 0)
         dw(0, 5)
+        dh(3, 0, 1)
         dw(1, 5)
-        for k in range(2):
-            dw(k, 6)
-            dh(3, 0, k)
-        for k in range(2):
-            dw(k, 7)
-            dh(k, 0, 2)
-        dh(0, 0, 3)
-        dh(1, 0, 3)
-        for k in range(2):
-            dw(2 + k, 0)
-            dh(2, 0, 2 + k)
-        dh(3, 0, 2)
-        dh(3, 0, 3)
+        dh(2, 0, 0)
+        dh(2, 0, 1)
+        for k in range(4):
+            dh(k // 2, 0, 2 + k % 2)
+            dw(k % 2, 6 + k // 2)
         scale(0, 0)
         scale(1, 0)
         quantize_w(1, 1)
+        for j in (2, 3):
+            dh(j, 0, 2)
+            dh(j, 0, 3)
         scale(2, 0)
-
-        whole_row = slice(0, 2)
-
-        def norm_backward(j):
-            scale(j, 1)
-            if j > 0:
-                finish(j - 1, whole_row)
-                store_dx(j - 1, whole_row, nc.sync)
-            dot(j)
-
         for k in range(2):
-            dw(2 + k, 1)
+            dw(2 + k, 0)
             dh(0, 1, k)
+        dw(2, 1)
+        dw(3, 1)
         dh(0, 1, 2)
         dh(0, 1, 3)
+        whole_row = slice(0, 2)
         scale(0, 1)
         scale(3, 0)
         dot(0)
-        for j in (1, 2):
+        for j in (1, 2, 3):
             for u in range(UNITS):
-                dw(2 + u % 2, 3 * j - 1 + u // 2)
                 dh(j, 1, u)
-            norm_backward(j)
-            dw(2, 3 * j + 1)
-            dw(3, 3 * j + 1)
-        for u in range(UNITS):
-            dh(3, 1, u)
-        norm_backward(3)
+                dw(2 + u % 2, 2 * j + u // 2)
+            scale(j, 1)
+            if j < 3:
+                finish(j - 1, whole_row)
+                store_dx(j - 1, whole_row, nc.sync)
+                dot(j)
+        finish(2, slice(0, 1))
+        store_dx(2, slice(0, 1), nc.sync)
+        dot(3)
+        finish(2, slice(1, 2))
+        store_dx(2, slice(1, 2), nc.sync)
         for h, queue in enumerate((nc.sync, nc.scalar)):
             finish(3, slice(h, h + 1))
             store_dx(3, slice(h, h + 1), queue)

@@ -249,6 +249,11 @@ def tile_llamaselfattentionblock_pa_v_kernel(tc, x, g, wq, wk, rstd, grad_0, gra
                 pairs.append((rows[:, ip], ps[:].rearrange("p k q -> p q k")))
             empty(pairs)
 
+        waiting = []
+
+        def store_dw(a, r, queue):
+            queue.dma_start(out=weight_grads[a][r * P : (r + 1) * P, :], in_=dw_rows[a, r])
+
         def dw(u, r, vector_bank=None):
             if u == 0:
                 dw_rows[0, r] = rotating("dw_rows", [P, J], F32, ROW_TILES)[:]
@@ -264,8 +269,12 @@ def tile_llamaselfattentionblock_pa_v_kernel(tc, x, g, wq, wk, rstd, grad_0, gra
             nc.tensor.matmul_mx(out=ps[:], lhsT=lhs[:, cols].bitcast(E4M3), lhsT_scale=lhs_scale[:, cols],
                                 rhs=rhs[:, f_cols].bitcast(E5M2), rhs_scale=rhs_scale[:, f_cols], start=True, stop=True)
             copy(out=dw_rows[u // 2, r][:, f_cols], in_=ps[:])
-            if u % 2 == 1:
-                nc.sync.dma_start(out=weight_grads[u // 2][r * P : (r + 1) * P, :], in_=dw_rows[u // 2, r])
+            if waiting:
+                store_dw(*waiting.pop(), nc.scalar)
+            if u == 3 and r % 2 == 0:
+                waiting.append((1, r))
+            elif u % 2 == 1:
+                store_dw(u // 2, r, nc.sync)
 
         def dh(j, h, u):
             if u == 0:

@@ -27,7 +27,8 @@ ROW_TILES = E // P
 H_ON_GPSIMD = 384
 GAIN_BANK = 0
 DH_BANK = 4
-ROPE_BANKS = ((None, 5), (6, 3), (6, 7), (6, 7))
+COSINE_BANK = 7
+ROPE_BANKS = ((None, 5), (6, 3), (5, 6))
 FLOPS = 2 * 2 * T * E * 2 * J
 
 
@@ -102,7 +103,9 @@ def tile_llamaselfattentionblock_pa_v_kernel(tc, x, g, wq, wk, rstd, grad_0, gra
         load_w(1, 0, slice(2, 4))
         load_grad(2)
         load_w(0, 1)
-        load_grad(3)
+        for b in range(B):
+            nc.sync.dma_start(out=grad_sb[3][32 * b : 32 * (b + 1)].rearrange("p n j d -> p n (j d)"),
+                              in_=grad_1[b, UNIT_HEADS:].rearrange("n (q j) d -> q n (j d)", j=SLOTS))
         load_w(1, 1)
 
         order = kept("order", [P, B, P // B], BF16)
@@ -116,6 +119,7 @@ def tile_llamaselfattentionblock_pa_v_kernel(tc, x, g, wq, wk, rstd, grad_0, gra
         whole = kept("whole", [P, 2, SLOTS * HD // 4], I32)
         fraction = kept("fraction", [P, 2, SLOTS * HD // 4], F32)
         cosines = kept("cosines", [P, 2, SLOTS * HD // 2], F32)
+        turned_cosines = kept("turned_cosines", [P, 2, P], F32)
         nc.vector.memset(ones[:], 1.0)
         nc.vector.tensor_single_scalar(ratio[:], ones[:], 10000.0 ** (-2 / 64.0), ALU.mult)
         nc.vector.tensor_single_scalar(positions[:], tokens[:], L - 1, ALU.bitwise_and)
@@ -160,6 +164,25 @@ def tile_llamaselfattentionblock_pa_v_kernel(tc, x, g, wq, wk, rstd, grad_0, gra
             nc.vector.tensor_tensor(out=dz[u][:, :, v, :].rearrange("p j (n c) -> p n j c", n=UNIT_HEADS),
                                     in0=grad_bank[u, v][:].rearrange("p k c -> p (k c)"),
                                     in1=cosines[:, v, :].unsqueeze(1).to_broadcast([P, UNIT_HEADS, 2 * P]), op=ALU.mult)
+
+        def turn_fractions():
+            ps = bank(COSINE_BANK, [P, 2, P])
+            for v in range(2):
+                nc.tensor.transpose(ps[:, v], fraction[:, v], identity[:])
+            nc.scalar.activation(out=turned_cosines[:], in_=ps[:], func=ACT.Sin, scale=2.0 * math.pi)
+
+        def place_cosines():
+            ps = bank(COSINE_BANK, [P, 2, P])
+            for v in range(2):
+                nc.tensor.transpose(ps[:, v], turned_cosines[:, v], identity[:])
+            return ps
+
+        def rope_in_token_order(u, v, cosines_psum):
+            if v == 0:
+                dz[u] = rotating("dz", [P, SLOTS, 2, UNIT // 2], BF16, 4)
+            nc.vector.tensor_tensor(out=dz[u][:, :, v, :].rearrange("p j (n c) -> p n j c", n=UNIT_HEADS),
+                                    in0=grad_sb[u][:].rearrange("p n j (w v s) -> p (n j w) v s", v=2, s=2)[:, :, v, :],
+                                    in1=cosines_psum[:, v, :].unsqueeze(1).unsqueeze(3).to_broadcast([P, UNIT_HEADS, P, 2]), op=ALU.mult)
 
         def interleave_on_gpsimd(u, v):
             nc.gpsimd.tensor_copy(out=dz_tok[u // 2][:, u % 2].rearrange("p (m v s) j -> p v m s j", v=2, s=2)[:, v],
@@ -211,7 +234,7 @@ def tile_llamaselfattentionblock_pa_v_kernel(tc, x, g, wq, wk, rstd, grad_0, gra
         def store_dx(j, halves, queue):
             queue.dma_start(out=out_rows[:, j, halves], in_=scaled[j][:, halves])
 
-        stream = [1, 2, 7, 4, 5, 3]
+        stream = [1, 2, 4, 5, 6, 3]
 
         def stream_bank(shape):
             k = stream.pop(0)
@@ -254,14 +277,13 @@ def tile_llamaselfattentionblock_pa_v_kernel(tc, x, g, wq, wk, rstd, grad_0, gra
         def store_dw(a, r, queue):
             queue.dma_start(out=weight_grads[a][r * P : (r + 1) * P, :], in_=dw_rows[a, r])
 
-        def dw(u, r, vector_bank=None):
+        def dw(u, r, copy=nc.scalar.copy, own_bank=None):
             if u == 0:
                 dw_rows[0, r] = rotating("dw_rows", [P, J], F32, ROW_TILES)[:]
             if u == 2 and r % 2 == 0:
                 both = rotating("w%d%d" % (r // 2 % 2, r // 4), [P, 2, J], F32, 1)
                 dw_rows[1, r], dw_rows[1, r + 1] = both[:, 0], both[:, 1]
-            ps = stream_bank([P, UNIT]) if vector_bank is None else bank(vector_bank, [P, UNIT])
-            copy = nc.scalar.copy if vector_bank is None else nc.vector.tensor_copy
+            ps = stream_bank([P, UNIT]) if own_bank is None else bank(own_bank, [P, UNIT])
             lhs, lhs_scale = h_q[r // 4]
             rhs, rhs_scale = dz_tok_q[u // 2]
             cols = slice((r % 4) * P, (r % 4 + 1) * P)
@@ -293,11 +315,14 @@ def tile_llamaselfattentionblock_pa_v_kernel(tc, x, g, wq, wk, rstd, grad_0, gra
             place_grad(u, v)
             rope(u, v)
             interleave_on_gpsimd(u, v)
+        turn_fractions()
         turn_w(0, 0, 0)
         turn_dz(0)
+        cosines_psum = place_cosines()
         turn_dz(1)
         turn_w(0, 0, 1)
-        stream.remove(7)
+        stream.remove(5)
+        stream.remove(6)
         turn_w(1, 0, 0)
         turn_w(1, 0, 1)
         for j in range(SLOTS):
@@ -314,75 +339,76 @@ def tile_llamaselfattentionblock_pa_v_kernel(tc, x, g, wq, wk, rstd, grad_0, gra
         quantize_w(0, 0)
         quantize_h(1, slice(0, 2 * P), h_tok[1][:])
         h_rest = rotating("h_tok1", [P, 2 * P, SLOTS], BF16, 1)
-        interleave_h_on_gpsimd(h_rest[:, :P], 1, slice(2 * P, 3 * P))
+        interleave_h_on_gpsimd(h_rest[:], 1, slice(2 * P, HALF))
         for v in range(2):
             place_grad(2, v)
             rope(2, v)
             interleave_on_gpsimd(2, v)
+        for v in range(2):
+            rope_in_token_order(3, v, cosines_psum)
+            interleave_on_gpsimd(3, v)
         dw(0, 0)
         dw(1, 0)
         turn_w(0, 1, 0)
+        stream.remove(DH_BANK)
         dw(0, 1)
         dw(1, 1)
-        stream.remove(DH_BANK)
         turn_w(0, 1, 1)
-        stream.remove(DH_BANK + 1)
         dh(0, 0, 0)
         dh(0, 0, 1)
-        place_grad(3, 0)
-        turn_w(1, 1, 0)
-        place_grad(3, 1)
-        for v in range(2):
-            rope(3, v)
-            interleave_on_gpsimd(3, v)
-        turn_dz(2)
-        dw(0, 2, 6)
         dw(0, 4)
-        dw(1, 4)
-        dw(1, 2, 7)
-        turn_dz(3)
-        dw(0, 3, 6)
-        interleave_h(nc.vector.tensor_copy, h_rest[:, P:], 1, slice(3 * P, HALF))
-        quantize_w(1, 0)
-        quantize_dz_feat(1)
-        quantize_h(1, slice(2 * P, HALF), h_rest[:])
-        quantize_w(0, 1)
-        quantize_dz_tok(1)
-        dw(1, 3)
         dh(1, 0, 0)
+        dw(1, 4)
         dh(1, 0, 1)
-        turn_w(1, 1, 1)
-        dh(3, 0, 0)
-        dw(0, 5)
-        dh(3, 0, 1)
-        dw(1, 5)
+        turn_dz(2)
         dh(2, 0, 0)
         dh(2, 0, 1)
-        for k in range(4):
-            dh(k // 2, 0, 2 + k % 2)
-            dw(k % 2, 6 + k // 2)
-        scale(0, 0)
-        scale(1, 0)
-        quantize_w(1, 1)
-        for j in (2, 3):
-            dh(j, 0, 2)
-            dh(j, 0, 3)
-        scale(2, 0)
-        for k in range(2):
-            dw(2 + k, 0)
-            dh(0, 1, k)
-        dw(2, 1)
-        dw(3, 1)
-        dh(0, 1, 2)
-        dh(0, 1, 3)
+        dw(0, 2, nc.vector.tensor_copy)
+        dw(0, 5)
+        dw(1, 5)
+        dw(1, 2, nc.vector.tensor_copy, COSINE_BANK)
+        dw(0, 3, nc.vector.tensor_copy)
+        turn_dz(3)
+        dh(3, 0, 0)
+        dw(1, 3)
+        dh(3, 0, 1)
+        quantize_h(1, slice(2 * P, HALF), h_rest[:])
+        quantize_w(1, 0)
+        quantize_dz_feat(1)
+        quantize_dz_tok(1)
+        quantize_w(0, 1)
+        turn_w(1, 1, 0)
+        dw(0, 6)
+        dw(1, 6)
+        turn_w(1, 1, 1)
+        passes = [(j, 0, u) for j in range(3) for u in (2, 3)] + [(0, 1, u) for u in range(UNITS)] + [(3, 0, 2), (3, 0, 3)]
+        passes.extend([(j, 1, u) for j in (1, 2, 3) for u in range(UNITS)])
+        products = [(2 * (k // 16) + k % 2, k // 2 % ROW_TILES) for k in range(14, 32)]
+
+        def multiply(count, each=1):
+            for k in range(count):
+                for i in range(each):
+                    dh(*passes.pop(0))
+                dw(*products.pop(0))
+
         whole_row = slice(0, 2)
+        multiply(1, 2)
+        multiply(2)
+        scale(0, 0)
+        quantize_w(1, 1)
+        scale(1, 0)
+        multiply(1, 2)
+        scale(2, 0)
+        multiply(2)
+        multiply(1, 2)
         scale(0, 1)
+        multiply(1, 2)
         scale(3, 0)
         dot(0)
+        multiply(2, 2)
         for j in (1, 2, 3):
-            for u in range(UNITS):
-                dh(j, 1, u)
-                dw(2 + u % 2, 2 * j + u // 2)
+            if j > 1:
+                multiply(4)
             scale(j, 1)
             if j < 3:
                 finish(j - 1, whole_row)

@@ -24,7 +24,7 @@ HALF = 512
 UNITS = 2 * J // UNIT
 UNIT_HEADS = UNIT // HD
 ROW_TILES = E // P
-H_ON_GPSIMD = 384
+H_ON_GPSIMD = 320
 GAIN_BANK = 0
 DH_BANK = 4
 COSINE_BANK = 7
@@ -184,13 +184,13 @@ def tile_llamaselfattentionblock_pa_v_kernel(tc, x, g, wq, wk, rstd, grad_0, gra
                                     in0=grad_sb[u][:].rearrange("p n j (w v s) -> p (n j w) v s", v=2, s=2)[:, :, v, :],
                                     in1=cosines_psum[:, v, :].unsqueeze(1).unsqueeze(3).to_broadcast([P, UNIT_HEADS, P, 2]), op=ALU.mult)
 
-        def interleave_on_gpsimd(u, v):
-            nc.gpsimd.tensor_copy(out=dz_tok[u // 2][:, u % 2].rearrange("p (m v s) j -> p v m s j", v=2, s=2)[:, v],
-                                  in_=dz[u][:, :, v].rearrange("p j c -> p c j"))
+        def interleave_on_gpsimd(u, v, groups=slice(0, P)):
+            nc.gpsimd.tensor_copy(out=dz_tok[u // 2][:, u % 2].rearrange("p (m v s) j -> p v m s j", v=2, s=2)[:, v, groups],
+                                  in_=dz[u][:, :, v].rearrange("p j c -> p c j")[:, 2 * groups.start : 2 * groups.stop])
 
-        def interleave_on_vector(u):
-            nc.vector.tensor_copy(out=dz_tok[u // 2][:, u % 2].rearrange("p (m v s) j -> p v m j s", v=2, s=2),
-                                  in_=dz[u][:].rearrange("p j v (m s) -> p v m j s", s=2))
+        def interleave_on_vector(u, groups):
+            nc.vector.tensor_copy(out=dz_tok[u // 2][:, u % 2].rearrange("p (m v s) j -> p v m j s", v=2, s=2)[:, :, groups],
+                                  in_=dz[u][:].rearrange("p j v (m s) -> p v m j s", s=2)[:, :, groups])
 
         def interleave_h_on_gpsimd(out, h, cols):
             nc.gpsimd.tensor_copy(out=out, in_=h_flat[h][:, :, cols].rearrange("p j c -> p c j"))
@@ -310,7 +310,8 @@ def tile_llamaselfattentionblock_pa_v_kernel(tc, x, g, wq, wk, rstd, grad_0, gra
 
         nc.vector.scalar_tensor_tensor(neg_r2[:], rstd_sb[:], -1.0 / E, rstd_sb[:], ALU.mult, ALU.mult)
         first_rope()
-        interleave_on_gpsimd(0, 0)
+        for k in range(2):
+            interleave_on_gpsimd(0, 0, slice(k * P // 2, (k + 1) * P // 2))
         for u, v in ((0, 1), (1, 0), (1, 1)):
             place_grad(u, v)
             rope(u, v)
@@ -346,7 +347,7 @@ def tile_llamaselfattentionblock_pa_v_kernel(tc, x, g, wq, wk, rstd, grad_0, gra
             interleave_on_gpsimd(2, v)
         for v in range(2):
             rope_in_token_order(3, v, cosines_psum)
-            interleave_on_gpsimd(3, v)
+            interleave_on_gpsimd(3, v, slice(0, P // 2))
         dw(0, 0)
         dw(1, 0)
         turn_w(0, 1, 0)
@@ -372,6 +373,7 @@ def tile_llamaselfattentionblock_pa_v_kernel(tc, x, g, wq, wk, rstd, grad_0, gra
         dh(3, 0, 0)
         dw(1, 3)
         dh(3, 0, 1)
+        interleave_on_vector(3, slice(P // 2, P))
         quantize_h(1, slice(2 * P, HALF), h_rest[:])
         quantize_w(1, 0)
         quantize_dz_feat(1)

@@ -354,16 +354,15 @@ def tile_llamaselfattentionblock_pa_v_kernel(tc, x, g, wq, wk, rstd, grad_0, gra
         stream.remove(DH_BANK)
         dw(0, 1)
         dw(1, 1)
-        turn_w(0, 1, 1)
         dh(0, 0, 0)
         dh(0, 0, 1)
+        turn_w(0, 1, 1)
         dw(0, 4)
         dh(1, 0, 0)
         dw(1, 4)
         dh(1, 0, 1)
         turn_dz(2)
         dh(2, 0, 0)
-        dh(2, 0, 1)
         dw(0, 2, nc.vector.tensor_copy)
         dw(0, 5)
         dw(1, 5)
@@ -381,6 +380,7 @@ def tile_llamaselfattentionblock_pa_v_kernel(tc, x, g, wq, wk, rstd, grad_0, gra
         quantize_w(0, 1)
         turn_w(1, 1, 0)
         dw(0, 6)
+        dh(2, 0, 1)
         dw(1, 6)
         turn_w(1, 1, 1)
         passes = [(j, 0, u) for j in range(3) for u in (2, 3)] + [(0, 1, u) for u in range(UNITS)] + [(3, 0, 2), (3, 0, 3)]

@@ -293,7 +293,7 @@ def tile_llamaselfattentionblock_pa_v_kernel(tc, x, g, wq, wk, rstd, grad_0, gra
             copy(out=dw_rows[u // 2, r][:, f_cols], in_=ps[:])
             if waiting:
                 store_dw(*waiting.pop(), nc.scalar)
-            if u == 3 and r % 2 == 0:
+            if u == 3 and r in (4, 6):
                 waiting.append((1, r))
             elif u % 2 == 1:
                 store_dw(u // 2, r, nc.sync)
@@ -414,13 +414,13 @@ def tile_llamaselfattentionblock_pa_v_kernel(tc, x, g, wq, wk, rstd, grad_0, gra
             scale(j, 1)
             if j < 3:
                 finish(j - 1, whole_row)
-                store_dx(j - 1, whole_row, nc.sync)
+                if j == 1:
+                    store_dx(0, whole_row, nc.sync)
                 dot(j)
-        finish(2, slice(0, 1))
-        store_dx(2, slice(0, 1), nc.sync)
+        store_dx(1, whole_row, nc.scalar)
+        finish(2, whole_row)
+        store_dx(2, whole_row, nc.sync)
         dot(3)
-        finish(2, slice(1, 2))
-        store_dx(2, slice(1, 2), nc.sync)
         for h, queue in enumerate((nc.sync, nc.scalar)):
             finish(3, slice(h, h + 1))
             store_dx(3, slice(h, h + 1), queue)

import math
from contextlib import ExitStack

import concourse.mybir as mybir
from concourse.masks import make_identity

F32 = mybir.dt.float32
BF16 = mybir.dt.bfloat16
I32 = mybir.dt.int32
U32 = mybir.dt.uint32
U8 = mybir.dt.uint8
E4M3 = mybir.dt.float8_e4m3fn_x4
E5M2 = mybir.dt.float8_e5m2_x4
ALU = mybir.AluOpType
ACT = mybir.ActivationFunctionType

P = 128
B, L, E, HEADS, HD = 4, 128, 1024, 8, 128
T = B * L
J = HEADS * HD
SLOTS = 4
UNIT = 512
HALF = 512
UNITS = 2 * J // UNIT
UNIT_HEADS = UNIT // HD
ROW_TILES = E // P
H_ON_GPSIMD = 320
GAIN_BANK = 0
DH_BANK = 4
COSINE_BANK = 7
ROPE_BANKS = ((None, 5), (6, 3), (5, 6))
FLOPS = 2 * 2 * T * E * 2 * J


def tile_llamaselfattentionblock_pa_v_kernel(tc, x, g, wq, wk, rstd, grad_0, grad_1, out_0, out_1, out_2):
    nc = tc.nc
    weights = (wq, wk)
    grads = (grad_0, grad_1)
    weight_grads = (out_1, out_2)
    x_rows = x.flatten_outer_dims().rearrange("(p j) e -> p j e", j=SLOTS)
    out_rows = out_0.flatten_outer_dims().rearrange("(p j) (h c) -> p j h c", j=SLOTS, h=2)

    with ExitStack() as ctx:
        keep = ctx.enter_context(tc.tile_pool(name="keep", bufs=1))
        reused = ctx.enter_context(tc.tile_pool(name="reused", bufs=2))
        psum = ctx.enter_context(tc.psum_pool(name="psum", bufs=1))

        def kept(name, shape, dtype):
            return keep.tile(shape, dtype, name=name, align_bytes=64)

        def rotating(tag, shape, dtype, bufs):
            return reused.tile(shape, dtype, name=tag, tag=tag, bufs=bufs, align_bytes=64)

        def codes(name, width):
            return kept(name + "_codes", [P, width], U32), kept(name + "_scales", [P, width], U8)

        def bank(k, shape, dtype=F32):
            return psum.tile(shape, dtype, name="bank%d" % k, tag="bank%d" % k, bufs=1)

        grad_sb = [kept("grad%d" % u, [P, UNIT_HEADS, SLOTS, HD], BF16) for u in range(UNITS)]
        rstd_sb = kept("rstd_sb", [P, SLOTS], F32)
        g_sb = kept("g_sb", [P, E // P], BF16)
        identity = kept("identity", [P, P], F32)
        x_sb = kept("x_sb", [P, SLOTS, E], BF16)
        x_halves = x_sb[:].rearrange("p j (h c) -> p j h c", h=2)
        gain = kept("gain", [P, E], BF16)
        h_flat = [rotating("h_flat%d" % h, [P, SLOTS, HALF], BF16, 1) for h in range(2)]
        w_sb = [[rotating("w%d%d" % (a, h), [P, 4, J], BF16, 1) for h in range(2)] for a in range(2)]
        h_tok = [rotating("h_tok0", [P, HALF, SLOTS], BF16, 1), rotating("h_tok1", [P, HALF // 2, SLOTS], BF16, 1)]
        h_q = [codes("h_q%d" % h, HALF) for h in range(2)]
        dz_tok_q = [codes("dz_tok_q%d" % a, 2 * UNIT) for a in range(2)]
        dz_feat_q = [codes("dz_feat_q%d" % a, 2 * T) for a in range(2)]
        w_q = [[codes("w_q%d%d" % (a, h), 2 * HALF) for h in range(2)] for a in range(2)]
        neg_r2 = kept("neg_r2", [P, SLOTS], F32)
        coef = [kept("coef%d" % j, [P, 1], F32) for j in range(SLOTS)]
        dz_tok = [kept("dz_tok%d" % a, [P, 2, UNIT, SLOTS], BF16) for a in range(2)]
        dz_feat = [kept("dz_feat%d" % a, [P, 2, 4 * T], BF16) for a in range(2)]
        dz, grad_bank, w_feat, dh_bank, dw_rows, scaled = {}, {}, {}, {}, {}, {}

        ctx.enter_context(tc.manual_schedule())

        tokens = kept("tokens", [P, SLOTS], I32)
        nc.gpsimd.iota(tokens[:], pattern=[[1, SLOTS]], base=0, channel_multiplier=SLOTS)
        make_identity(nc, identity[:])
        nc.sync.dma_start(out=g_sb[:], in_=g.rearrange("(p c) -> p c", p=P))
        nc.sync.dma_start(out=rstd_sb[:], in_=rstd.rearrange("b (q j) -> (b q) j", j=SLOTS))

        def load_grad(u):
            for n in range(UNIT_HEADS):
                nc.sync.dma_start(out=grad_sb[u][:, n].rearrange("p j d -> p (j d)"),
                                  in_=grads[u // 2][:, (u % 2) * UNIT_HEADS + n].rearrange("b (q j) d -> q b (j d)", j=SLOTS))

        def load_w(a, h, sets=slice(0, 4)):
            rows = weights[a][h * HALF : (h + 1) * HALF, :].rearrange("(q i) f -> q i f", i=4)
            nc.sync.dma_start(out=w_sb[a][h][:, sets], in_=rows[:, sets])

        load_grad(0)
        load_grad(1)
        load_w(0, 0, slice(0, 2))
        nc.sync.dma_start(out=x_sb[:], in_=x_rows)
        load_w(0, 0, slice(2, 4))
        load_w(1, 0, slice(0, 2))
        load_w(1, 0, slice(2, 4))
        load_grad(2)
        load_w(0, 1)
        for b in range(B):
            nc.sync.dma_start(out=grad_sb[3][32 * b : 32 * (b + 1)].rearrange("p n j d -> p n (j d)"),
                              in_=grad_1[b, UNIT_HEADS:].rearrange("n (q j) d -> q n (j d)", j=SLOTS))
        load_w(1, 1)

        order = kept("order", [P, B, P // B], BF16)
        nc.gpsimd.tensor_copy(out=order[:], in_=identity[:].rearrange("p (q b) -> p b q", b=B))

        positions = kept("positions", [P, SLOTS], I32)
        ones = kept("ones", [P, HD // 4], F32)
        ratio = kept("ratio", [P, HD // 4], F32)
        theta = kept("theta", [P, 2, HD // 4], F32)
        turns = kept("turns", [P, 2, SLOTS * HD // 4], F32)
        whole = kept("whole", [P, 2, SLOTS * HD // 4], I32)
        fraction = kept("fraction", [P, 2, SLOTS * HD // 4], F32)
        cosines = kept("cosines", [P, 2, SLOTS * HD // 2], F32)
        turned_cosines = kept("turned_cosines", [P, 2, P], F32)
        nc.vector.memset(ones[:], 1.0)
        nc.vector.tensor_single_scalar(ratio[:], ones[:], 10000.0 ** (-2 / 64.0), ALU.mult)
        nc.vector.tensor_single_scalar(positions[:], tokens[:], L - 1, ALU.bitwise_and)
        for v in range(2):
            nc.vector.tensor_tensor_scan(theta[:, v], ratio[:], ones[:], 10000.0 ** ((2 - v) / 64.0) * 0.5 / math.pi, ALU.mult, ALU.mult)
        for v in range(2):
            nc.vector.tensor_tensor(turns[:, v].rearrange("p (j w) -> p j w", j=SLOTS), positions[:].unsqueeze(2).to_broadcast([P, SLOTS, HD // 4]),
                                    theta[:, v].unsqueeze(1).to_broadcast([P, SLOTS, HD // 4]), ALU.mult)
        for v in range(2):
            nc.vector.tensor_single_scalar(whole[:, v], turns[:, v], 0.25, ALU.add)
        for v in range(2):
            nc.vector.scalar_tensor_tensor(fraction[:, v], turns[:, v], 0.25, whole[:, v], ALU.add, ALU.subtract)

        gain_words = bank(GAIN_BANK, [P, P, 4])
        for k in range(4):
            nc.tensor.transpose(gain_words[:, :, k], g_sb[:].bitcast(F32)[:, k : k + 1].to_broadcast([P, P]), identity[:])
        gain_psum = gain_words[:].rearrange("p q k -> p (q k)")

        for v in range(2):
            nc.scalar.activation(out=cosines[:, v].rearrange("p (k s) -> p k s", s=2), in_=fraction[:, v].unsqueeze(2).to_broadcast([P, P, 2]),
                                 func=ACT.Sin, scale=2.0 * math.pi)
        nc.scalar.copy(out=gain[:].bitcast(F32), in_=gain_psum)

        def place_grad(u, v):
            grad_bank[u, v] = bank(ROPE_BANKS[u][v], [P, 2, UNIT], BF16)
            pairs = grad_sb[u][:].rearrange("p (k n) j (w v s) -> p k (n j w) v s", k=2, v=2, s=2)
            for k in range(2):
                nc.tensor.matmul(grad_bank[u, v][:, k], lhsT=order[:].rearrange("p b q -> p (b q)"), rhs=pairs[:, k, :, v, :], start=True, stop=True)

        def first_rope():
            dz[0] = rotating("dz", [P, SLOTS, 2, UNIT // 2], BF16, 4)
            pairs = grad_sb[0][:].rearrange("p (k n) j (w v s) -> p k (n j w) v s", k=2, v=2, s=2)
            rows = dz[0][:, :, 0, :].rearrange("p j (k n c) -> p k n j c", k=2, n=2)
            for k in range(2):
                ps = bank((7, 4)[k], [P, UNIT], BF16)
                nc.tensor.matmul(ps[:], lhsT=order[:].rearrange("p b q -> p (b q)"), rhs=pairs[:, k, :, 0, :], start=True, stop=True)
                nc.vector.tensor_tensor(out=rows[:, k], in0=ps[:], in1=cosines[:, 0, :].unsqueeze(1).to_broadcast([P, 2, 2 * P]), op=ALU.mult)

        def rope(u, v):
            if v == 0:
                dz[u] = rotating("dz", [P, SLOTS, 2, UNIT // 2], BF16, 4)
            nc.vector.tensor_tensor(out=dz[u][:, :, v, :].rearrange("p j (n c) -> p n j c", n=UNIT_HEADS),
                                    in0=grad_bank[u, v][:].rearrange("p k c -> p (k c)"),
                                    in1=cosines[:, v, :].unsqueeze(1).to_broadcast([P, UNIT_HEADS, 2 * P]), op=ALU.mult)

        def turn_fractions():
            ps = bank(COSINE_BANK, [P, 2, P])
            for v in range(2):
                nc.tensor.transpose(ps[:, v], fraction[:, v], identity[:])
            nc.scalar.activation(out=turned_cosines[:], in_=ps[:], func=ACT.Sin, scale=2.0 * math.pi)

        def place_cosines():
            ps = bank(COSINE_BANK, [P, 2, P])
            for v in range(2):
                nc.tensor.transpose(ps[:, v], turned_cosines[:, v], identity[:])
            return ps

        def rope_in_token_order(u, v, cosines_psum):
            if v == 0:
                dz[u] = rotating("dz", [P, SLOTS, 2, UNIT // 2], BF16, 4)
            nc.vector.tensor_tensor(out=dz[u][:, :, v, :].rearrange("p j (n c) -> p n j c", n=UNIT_HEADS),
                                    in0=grad_sb[u][:].rearrange("p n j (w v s) -> p (n j w) v s", v=2, s=2)[:, :, v, :],
                                    in1=cosines_psum[:, v, :].unsqueeze(1).unsqueeze(3).to_broadcast([P, UNIT_HEADS, P, 2]), op=ALU.mult)

        def interleave_on_gpsimd(u, v, groups=slice(0, P)):
            nc.gpsimd.tensor_copy(out=dz_tok[u // 2][:, u % 2].rearrange("p (m v s) j -> p v m s j", v=2, s=2)[:, v, groups],
                                  in_=dz[u][:, :, v].rearrange("p j c -> p c j")[:, 2 * groups.start : 2 * groups.stop])

        def interleave_on_vector(u, groups):
            nc.vector.tensor_copy(out=dz_tok[u // 2][:, u % 2].rearrange("p (m v s) j -> p v m j s", v=2, s=2)[:, :, groups],
                                  in_=dz[u][:].rearrange("p j v (m s) -> p v m j s", s=2)[:, :, groups])

        def interleave_h_on_gpsimd(out, h, cols):
            nc.gpsimd.tensor_copy(out=out, in_=h_flat[h][:, :, cols].rearrange("p j c -> p c j"))

        def interleave_h(copy, out, h, cols):
            copy(out=out.rearrange("p (c i) j -> p c j i", i=4), in_=h_flat[h][:, :, cols].rearrange("p j (c i) -> p c j i", i=4))

        def norm(h, j):
            cols = slice(h * HALF, (h + 1) * HALF)
            nc.vector.scalar_tensor_tensor(h_flat[h][:, j], x_sb[:, j, cols], rstd_sb[:, j : j + 1],
                                           gain_psum.bitcast(BF16)[:, cols], ALU.mult, ALU.mult)

        def quantize(pair, dtype, values):
            nc.vector.quantize_mx(out=pair[0][:].bitcast(dtype), scales=pair[1][:], in_=values)

        def quantize_dz_tok(a):
            quantize(dz_tok_q[a], E5M2, dz_tok[a][:].rearrange("p u c j -> p (u c j)"))

        def quantize_h(h, cols, values):
            quantize((h_q[h][0][:, cols], h_q[h][1][:, cols]), E4M3, values.rearrange("p c j -> p (c j)"))

        def quantize_dz_feat(a):
            quantize(dz_feat_q[a], E5M2, dz_feat[a][:].rearrange("p u c -> p (u c)"))

        def quantize_w(a, h):
            quantize(w_q[a][h], E4M3, w_feat[a, h][:].rearrange("p u c -> p (u c)"))

        def scale(j, h):
            if j not in scaled:
                scaled[j] = rotating(("h_flat0", "h_flat1", "h_tok0", "w_feat00")[j], [P, 2, HALF], F32, 1)[:]
            nc.vector.scalar_tensor_tensor(scaled[j][:, h], dh_bank[j, h][:], rstd_sb[:, j : j + 1], gain[:, h * HALF : (h + 1) * HALF], ALU.mult, ALU.mult)

        def dot(j):
            product = rotating("dz", [P, 2, HALF], F32, 4)
            nc.vector.scalar_tensor_tensor(product[:], x_halves[:, j], neg_r2[:, j : j + 1], scaled[j], ALU.mult, ALU.mult,
                                           accum_out=coef[j][:])

        def finish(j, halves):
            nc.vector.scalar_tensor_tensor(scaled[j][:, halves], x_halves[:, j, halves], coef[j][:], scaled[j][:, halves], ALU.mult, ALU.add)

        def store_dx(j, halves, queue):
            queue.dma_start(out=out_rows[:, j, halves], in_=scaled[j][:, halves])

        stream = [1, 2, 4, 5, 6, 3]

        def stream_bank(shape):
            k = stream.pop(0)
            stream.append(k)
            return bank(k, shape)

        def empty(pairs, copy=nc.scalar.copy):
            for rows, ps in pairs:
                copy(out=rows, in_=ps)

        def turn_dz(u):
            words = dz[u][:].rearrange("p j v c -> p (j v c)").bitcast(F32)
            pairs = []
            for jp in range(2):
                ps = stream_bank([P, 4, P])
                for k in range(4):
                    first = (4 * jp + k) * P
                    nc.tensor.transpose(ps[:, k, :], words[:, first : first + P], identity[:])
                rows = dz_feat[u // 2][:, u % 2].bitcast(F32)[:, jp * 4 * P : (jp + 1) * 4 * P]
                pairs.append((rows.rearrange("p (j q v) -> p j q v", j=2, v=2), ps[:].rearrange("p (j v) q -> p j q v", v=2)))
            empty(pairs)

        def turn_w(a, h, ip):
            if ip == 0:
                w_feat[a, h] = rotating("w_feat%d%d" % (a, h), [P, 2, 4 * HALF], BF16, 1)
            words = w_sb[a][h][:].rearrange("p i f -> p (i f)").bitcast(F32)
            pairs = []
            for u in range(2):
                ps = stream_bank([P, 4, P])
                for i in range(2):
                    first = (2 * ip + i) * (J // 2) + u * (UNIT // 2)
                    for v in range(2):
                        nc.tensor.transpose(ps[:, 2 * i + v, :], words[:, first + v : first + UNIT // 2 : 2], identity[:])
                rows = w_feat[a, h][:, u].bitcast(F32).rearrange("p (q i k) -> p i q k", i=2, k=4)
                pairs.append((rows[:, ip], ps[:].rearrange("p k q -> p q k")))
            empty(pairs)

        waiting = []

        def store_dw(a, r, queue):
            queue.dma_start(out=weight_grads[a][r * P : (r + 1) * P, :], in_=dw_rows[a, r])

        def dw(u, r, copy=nc.scalar.copy, own_bank=None):
            if u == 0:
                dw_rows[0, r] = rotating("dw_rows", [P, J], F32, ROW_TILES)[:]
            if u == 2 and r % 2 == 0:
                both = rotating("w%d%d" % (r // 2 % 2, r // 4), [P, 2, J], F32, 1)
                dw_rows[1, r], dw_rows[1, r + 1] = both[:, 0], both[:, 1]
            ps = stream_bank([P, UNIT]) if own_bank is None else bank(own_bank, [P, UNIT])
            lhs, lhs_scale = h_q[r // 4]
            rhs, rhs_scale = dz_tok_q[u // 2]
            cols = slice((r % 4) * P, (r % 4 + 1) * P)
            f_cols = slice((u % 2) * UNIT, (u % 2 + 1) * UNIT)
            nc.tensor.matmul_mx(out=ps[:], lhsT=lhs[:, cols].bitcast(E4M3), lhsT_scale=lhs_scale[:, cols],
                                rhs=rhs[:, f_cols].bitcast(E5M2), rhs_scale=rhs_scale[:, f_cols], start=True, stop=True)
            copy(out=dw_rows[u // 2, r][:, f_cols], in_=ps[:])
            if waiting:
                store_dw(*waiting.pop(), nc.scalar)
            if u == 3 and r in (4, 6):
                waiting.append((1, r))
            elif u % 2 == 1:
                store_dw(u // 2, r, nc.sync)

        def dh(j, h, u):
            if u == 0:
                dh_bank[j, h] = bank(DH_BANK + j, [P, HALF])
            cols = slice((u % 2) * T + j * P, (u % 2) * T + (j + 1) * P)
            lhs, lhs_scale = dz_feat_q[u // 2]
            rhs, rhs_scale = w_q[u // 2][h]
            e_cols = slice((u % 2) * HALF, (u % 2 + 1) * HALF)
            nc.tensor.matmul_mx(out=dh_bank[j, h][:], lhsT=lhs[:, cols].bitcast(E5M2), lhsT_scale=lhs_scale[:, cols],
                                rhs=rhs[:, e_cols].bitcast(E4M3), rhs_scale=rhs_scale[:, e_cols], start=(u == 0), stop=(u == UNITS - 1))

        nc.vector.scalar_tensor_tensor(neg_r2[:], rstd_sb[:], -1.0 / E, rstd_sb[:], ALU.mult, ALU.mult)
        first_rope()
        for k in range(2):
            interleave_on_gpsimd(0, 0, slice(k * P // 2, (k + 1) * P // 2))
        for u, v in ((0, 1), (1, 0), (1, 1)):
            place_grad(u, v)
            rope(u, v)
            interleave_on_gpsimd(u, v)
        turn_fractions()
        turn_w(0, 0, 0)
        turn_dz(0)
        cosines_psum = place_cosines()
        turn_dz(1)
        turn_w(0, 0, 1)
        stream.remove(5)
        stream.remove(6)
        turn_w(1, 0, 0)
        turn_w(1, 0, 1)
        for j in range(SLOTS):
            norm(0, j)
        interleave_h_on_gpsimd(h_tok[0][:, :H_ON_GPSIMD], 0, slice(0, H_ON_GPSIMD))
        for j in range(SLOTS):
            norm(1, j)
        stream.append(GAIN_BANK)
        interleave_h(nc.scalar.copy, h_tok[1][:], 1, slice(0, HALF // 2))
        interleave_h(nc.vector.tensor_copy, h_tok[0][:, H_ON_GPSIMD:], 0, slice(H_ON_GPSIMD, HALF))
        quantize_dz_tok(0)
        quantize_h(0, slice(0, HALF), h_tok[0][:])
        quantize_dz_feat(0)
        quantize_w(0, 0)
        quantize_h(1, slice(0, 2 * P), h_tok[1][:])
        h_rest = rotating("h_tok1", [P, 2 * P, SLOTS], BF16, 1)
        interleave_h_on_gpsimd(h_rest[:], 1, slice(2 * P, HALF))
        for v in range(2):
            place_grad(2, v)
            rope(2, v)
            interleave_on_gpsimd(2, v)
        for v in range(2):
            rope_in_token_order(3, v, cosines_psum)
            interleave_on_gpsimd(3, v, slice(0, P // 2))
        dw(0, 0)
        dw(1, 0)
        turn_w(0, 1, 0)
        stream.remove(DH_BANK)
        dw(0, 1)
        dw(1, 1)
        dh(0, 0, 0)
        dh(0, 0, 1)
        turn_w(0, 1, 1)
        dw(0, 4)
        dh(1, 0, 0)
        dw(1, 4)
        dh(1, 0, 1)
        turn_dz(2)
        dh(2, 0, 0)
        dw(0, 2, nc.vector.tensor_copy)
        dw(0, 5)
        dw(1, 5)
        dw(1, 2, nc.vector.tensor_copy, COSINE_BANK)
        dw(0, 3, nc.vector.tensor_copy)
        turn_dz(3)
        dh(3, 0, 0)
        dw(1, 3)
        dh(3, 0, 1)
        interleave_on_vector(3, slice(P // 2, P))
        quantize_h(1, slice(2 * P, HALF), h_rest[:])
        quantize_w(1, 0)
        quantize_dz_feat(1)
        quantize_dz_tok(1)
        quantize_w(0, 1)
        turn_w(1, 1, 0)
        dw(0, 6)
        dh(2, 0, 1)
        dw(1, 6)
        turn_w(1, 1, 1)
        passes = [(j, 0, u) for j in range(3) for u in (2, 3)] + [(0, 1, u) for u in range(UNITS)] + [(3, 0, 2), (3, 0, 3)]
        passes.extend([(j, 1, u) for j in (1, 2, 3) for u in range(UNITS)])
        products = [(2 * (k // 16) + k % 2, k // 2 % ROW_TILES) for k in range(14, 32)]

        def multiply(count, each=1):
            for k in range(count):
                for i in range(each):
                    dh(*passes.pop(0))
                dw(*products.pop(0))

        whole_row = slice(0, 2)
        multiply(1, 2)
        multiply(2)
        scale(0, 0)
        quantize_w(1, 1)
        scale(1, 0)
        multiply(1, 2)
        scale(2, 0)
        multiply(2)
        multiply(1, 2)
        scale(0, 1)
        multiply(1, 2)
        scale(3, 0)
        dot(0)
        multiply(2, 2)
        for j in (1, 2, 3):
            if j > 1:
                multiply(4)
            scale(j, 1)
            if j < 3:
                finish(j - 1, whole_row)
                if j == 1:
                    store_dx(0, whole_row, nc.sync)
                dot(j)
        store_dx(1, whole_row, nc.scalar)
        finish(2, whole_row)
        store_dx(2, whole_row, nc.sync)
        dot(3)
        for h, queue in enumerate((nc.sync, nc.scalar)):
            finish(3, slice(h, h + 1))
            store_dx(3, slice(h, h + 1), queue)
